import numpy as np
import ml_dtypes


def mxq(x, axis, fmt="e4m3"):
    dtype, down = {"e4m3": (ml_dtypes.float8_e4m3fn, 7), "e5m2": (ml_dtypes.float8_e5m2, 14)}[fmt]
    v = np.moveaxis(np.asarray(x, np.float32).astype(ml_dtypes.bfloat16).astype(np.float64), axis, -1)
    blocks = v.reshape(v.shape[:-1] + (-1, 32))
    amax = np.abs(blocks).max(-1, keepdims=True)
    byte = np.maximum(np.where(amax > 0, np.frexp(amax)[1] - 1 + 127, 0) - down, 1)
    scale = np.exp2(byte - 127.0)
    codes = (blocks / scale).astype(np.float32).astype(dtype).astype(np.float64)
    return np.moveaxis((codes * scale).reshape(v.shape), -1, axis)


WIDE = False


def mx_kscale(k):
    if not WIDE:
        return np.ones(k)
    levels = np.array([20, -20, 10, -10, 0])
    a = np.random.permutation(np.resize(levels, k // 512 * 4)).reshape(k // 512, 4)
    idx = np.arange(k)
    return np.exp2(a[idx // 512, idx % 128 // 32])


BF16 = ml_dtypes.bfloat16


def bf(x):
    return np.asarray(x, np.float32).astype(BF16)


def f64(x):
    return np.asarray(x).astype(np.float64)


B, S, K, M = 2, 16, 512, 128
D = K * M


def fwht(v):
    m = v.shape[-1]
    lead = v.shape[:-1]
    h = 1
    while h < m:
        v = v.reshape(lead + (m // (2 * h), 2, h))
        a = v[..., 0, :]
        b = v[..., 1, :]
        v = np.stack([a + b, a - b], axis=-2)
        h *= 2
    return v.reshape(lead + (m,))


def setup_inputs():
    s = mx_kscale(K)
    x = np.random.standard_normal((B, S, K, M)) * K ** 0.25
    had_K = np.random.standard_normal((K, K)) / K ** 0.25 / s[:, None]
    g = np.random.standard_normal((B, S, K, M)) * np.exp2(np.random.randint(-12, 1, (B, S, 1, 1))) * 16.0 * s[:, None]
    return {"x": bf(x.reshape(B, S, D)), "had_K": bf(had_K), "grad_out": bf(g.reshape(B, S, D))}


def reference(x, had_K, grad_out):
    g = f64(grad_out)
    n = g.shape[-1]
    m = n // K
    t = g.size // n
    g2 = g.reshape(t, K, m).transpose(1, 0, 2).reshape(K, t * m)
    z = mxq(f64(had_K), 0, "e4m3").T @ mxq(g2, 0, "e5m2")
    z = z.reshape(K, t, m).transpose(1, 0, 2)
    gx = fwht(z) * (1.0 / np.sqrt(n))
    return gx.reshape(g.shape)

@@ -1,0 +1,177 @@
+from contextlib import ExitStack
+
+import concourse.mybir as mybir
+from concourse.masks import make_identity
+
+F32 = mybir.dt.float32
+BF16 = mybir.dt.bfloat16
+U32 = mybir.dt.uint32
+U8 = mybir.dt.uint8
+E4X4 = mybir.dt.float8_e4m3fn_x4
+E5X4 = mybir.dt.float8_e5m2_x4
+ALU = mybir.AluOpType
+
+P = 128
+T = 32
+K = 512
+M = 128
+SCALE = 1.0 / 256.0
+FLOPS = 2 * K * K * T * M + 7 * T * K * M
+BYTES = T * K * M * 2 + K * K * 2 + T * K * M * 4
+
+N0 = 4
+NA = 16
+NB = 12
+TA0 = N0
+TB0 = N0 + NA
+
+
+def tile_fullonlinehadamardhook_kernel(tc, x, had_K, grad_out, out):
+    nc = tc.nc
+    g_view = grad_out.rearrange("b s (p x) -> p (b s) x", p=P)
+    o_view = out.rearrange("b s (p x) -> p (b s) x", p=P)
+    with ExitStack() as ctx:
+        keep = ctx.enter_context(tc.tile_pool(name="keep", bufs=1))
+        grp = ctx.enter_context(tc.tile_pool(name="grp", bufs=3))
+        wk = ctx.enter_context(tc.tile_pool(name="wk", bufs=4))
+        sm = ctx.enter_context(tc.tile_pool(name="sm", bufs=4))
+        zsp = ctx.enter_context(tc.tile_pool(name="zsp", bufs=3))
+        psa = ctx.enter_context(tc.psum_pool(name="psa", bufs=4))
+        psz = ctx.enter_context(tc.psum_pool(name="psz", bufs=2))
+        pso = ctx.enter_context(tc.psum_pool(name="pso", bufs=2))
+
+        raw_h = keep.tile([P, 4, K], BF16)
+        nc.sync.dma_start(out=raw_h[:], in_=had_K.rearrange("(p j) c -> p j c", j=4))
+        raw_g = keep.tile([P, T, K], BF16)
+        for c in range(T // 4):
+            nc.sync.dma_start(out=raw_g[:, c * 4:(c + 1) * 4, :], in_=g_view[:, c * 4:(c + 1) * 4, :])
+
+        cur = keep.tile([P, P], F32, name="hid")
+        make_identity(nc, cur[:])
+        for k in range(7):
+            h = 1 << k
+            nxt = keep.tile([P, P], F32, name="hst%d" % k)
+            xv = cur[:].rearrange("p (m two h) -> p m two h", two=2, h=h)
+            yv = nxt[:].rearrange("p (m two h) -> p m two h", two=2, h=h)
+            nc.vector.tensor_tensor(out=yv[:, :, 0, :], in0=xv[:, :, 0, :], in1=xv[:, :, 1, :], op=ALU.add)
+            nc.vector.tensor_tensor(out=yv[:, :, 1, :], in0=xv[:, :, 0, :], in1=xv[:, :, 1, :], op=ALU.subtract)
+            cur = nxt
+        hmat = cur
+
+        g_codes = keep.tile([P, T * M], U32, align_bytes=64)
+        g_scales = keep.tile([P, T * M], U8, align_bytes=64)
+        res = keep.tile([P, T, K], F32)
+
+        h_codes = []
+        h_scales = []
+        for s in range(2):
+            hg = keep.tile([P, K, 4], BF16, align_bytes=64, name="hg%d" % s)
+            dst = hg[:].rearrange("p (r q) j -> p r q j", r=4)
+            src = raw_h[:].rearrange("p j (q r) -> p r q j", r=4)
+            if s == 0:
+                nc.vector.tensor_copy(out=dst, in_=src)
+            else:
+                nc.scalar.mul(out=dst, in_=src, mul=-1.0)
+            hc = keep.tile([P, K], U32, align_bytes=64, name="hc%d" % s)
+            hs = keep.tile([P, K], U8, align_bytes=64, name="hs%d" % s)
+            nc.vector.quantize_mx(out=hc[:].bitcast(E4X4), scales=hs[:], in_=hg[:].rearrange("p c j -> p (c j)"))
+            h_codes.append(hc)
+            h_scales.append(hs)
+
+        def quantise(col0, src4, on_vector):
+            gt = grp.tile([P, K, 4], BF16, align_bytes=64, tag="g", name="gt")
+            dst = gt[:].rearrange("p (x y) j -> p x y j", x=src4.shape[1])
+            if on_vector:
+                nc.vector.tensor_copy(out=dst, in_=src4)
+            else:
+                nc.scalar.copy(out=dst, in_=src4)
+            cols = slice(col0, col0 + K)
+            nc.vector.quantize_mx(out=g_codes[:, cols].bitcast(E5X4), scales=g_scales[:, cols], in_=gt[:].rearrange("p c j -> p (c j)"))
+
+        def token_major(t0):
+            return raw_g[:, t0:t0 + 4, :].rearrange("p t (j a) -> p t a j", j=4)
+
+        def unit(banks, gb, length, out_view):
+            n_stage = {32: 5, 128: 7}[length]
+            w = wk.tile([P, 4 * gb, length], F32, tag="w", name="w")
+            for b in range(4):
+                bv = banks[b][:].rearrange("p (g q two) -> p g q two", g=gb, two=2)
+                odd = sm.tile([P, gb, length // 2], F32, tag="odd", name="odd")
+                nc.scalar.mul(out=odd[:], in_=bv[:, :, :, 1], mul=SCALE)
+                wv = w[:, b * gb:(b + 1) * gb, :].rearrange("p g (h q) -> p g h q", h=2)
+                nc.vector.scalar_tensor_tensor(out=wv[:, :, 0, :], in0=bv[:, :, :, 0], scalar=SCALE, in1=odd[:], op0=ALU.mult, op1=ALU.add)
+                nc.vector.scalar_tensor_tensor(out=wv[:, :, 1, :], in0=bv[:, :, :, 0], scalar=SCALE, in1=odd[:], op0=ALU.mult, op1=ALU.subtract)
+            for s in range(2, n_stage):
+                wn = wk.tile([P, 4 * gb, length], F32, tag="w", name="wn")
+                for half in range(2):
+                    gs = slice(half * 2 * gb, (half + 1) * 2 * gb)
+                    xv = w[:, gs, :].rearrange("p g (q two) -> p g q two", two=2)
+                    yv = wn[:, gs, :].rearrange("p g (h q) -> p g h q", h=2)
+                    nc.vector.tensor_tensor(out=yv[:, :, 0, :], in0=xv[:, :, :, 0], in1=xv[:, :, :, 1], op=ALU.add)
+                    nc.vector.tensor_tensor(out=yv[:, :, 1, :], in0=xv[:, :, :, 0], in1=xv[:, :, :, 1], op=ALU.subtract)
+                w = wn
+            for half in range(2):
+                gs = slice(half * 2 * gb, (half + 1) * 2 * gb)
+                xv = w[:, gs, :].rearrange("p (b g) (q two) -> p b g q two", b=2, two=2)
+                nc.vector.tensor_tensor(out=out_view[:, 2 * half:2 * half + 2, :, 0, :], in0=xv[:, :, :, :, 0], in1=xv[:, :, :, :, 1], op=ALU.add)
+                nc.vector.tensor_tensor(out=out_view[:, 2 * half:2 * half + 2, :, 1, :], in0=xv[:, :, :, :, 0], in1=xv[:, :, :, :, 1], op=ALU.subtract)
+
+        quantise(0, token_major(0), True)
+        banks0 = []
+        for r in range(4):
+            bank = psa.tile([P, K], F32, tag="a", name="bank")
+            nc.tensor.matmul_mx(
+                out=bank[:],
+                lhsT=h_codes[0][:, r * P:(r + 1) * P].bitcast(E4X4), lhsT_scale=h_scales[0][:, r * P:(r + 1) * P],
+                rhs=g_codes[:, 0:K].bitcast(E5X4), rhs_scale=g_scales[:, 0:K],
+                start=True, stop=True,
+            )
+            banks0.append(bank)
+
+        slabs = raw_g[:, TA0:TA0 + NA, :].rearrange("p t (j c e) -> p c t e j", j=4, c=4)
+        for c in range(4):
+            quantise(K * (1 + c), slabs[:, c], False)
+
+        unit(banks0, 4, 128, res[:, 0:N0, :].rearrange("p t (r h q) -> p r t h q", r=4, h=2))
+        nc.sync.dma_start(out=o_view[:, 0:N0, :], in_=res[:, 0:N0, :])
+
+        def plain_token(tb):
+            t = TB0 + tb
+            cols = slice(K * 5 + tb * M, K * 5 + (tb + 1) * M)
+            zp = psz.tile([P, K], F32, name="zp")
+            nc.tensor.matmul_mx(
+                out=zp[:],
+                lhsT=g_codes[:, cols].bitcast(E5X4), lhsT_scale=g_scales[:, cols],
+                rhs=h_codes[0][:].bitcast(E4X4), rhs_scale=h_scales[0][:],
+                start=True, stop=True,
+            )
+            zs = zsp.tile([P, K], F32, name="zs")
+            nc.scalar.copy(out=zs[:], in_=zp[:])
+            op = pso.tile([P, K], F32, name="op")
+            for r in range(4):
+                rc = slice(r * P, (r + 1) * P)
+                nc.tensor.matmul(out=op[:, rc], lhsT=zs[:, rc], rhs=hmat[:], start=True, stop=True)
+            nc.scalar.mul(out=res[:, t, :], in_=op[:], mul=SCALE)
+            if tb % 2 == 1:
+                nc.sync.dma_start(out=o_view[:, t - 1:t + 1, :], in_=res[:, t - 1:t + 1, :])
+
+        for r in range(4):
+            banks = []
+            for d in range(4):
+                bank = psa.tile([P, K], F32, tag="a", name="bank")
+                for c in range(4):
+                    s = (((c & d) >> 1) ^ (c & d)) & 1
+                    nc.tensor.matmul_mx(
+                        out=bank[:],
+                        lhsT=h_codes[s][:, r * P:(r + 1) * P].bitcast(E4X4), lhsT_scale=h_scales[s][:, r * P:(r + 1) * P],
+                        rhs=g_codes[:, K * (1 + c):K * (2 + c)].bitcast(E5X4), rhs_scale=g_scales[:, K * (1 + c):K * (2 + c)],
+                        start=(c == 0), stop=(c == 3),
+                    )
+                banks.append(bank)
+            if r < 3:
+                quantise(K * 5 + r * K, token_major(TB0 + 4 * r), False)
+                for tb in range(4 * r, 4 * r + 4):
+                    plain_token(tb)
+            rcols = slice(r * M, (r + 1) * M)
+            unit(banks, NA, 32, res[:, TA0:TA0 + NA, rcols].rearrange("p t (d h q) -> p d t h q", d=4, h=2))
+            nc.sync.dma_start(out=o_view[:, TA0:TA0 + NA, rcols], in_=res[:, TA0:TA0 + NA, rcols])

@@ -91,30 +91,27 @@ def tile_fullonlinehadamardhook_kernel(tc, x, had_K, grad_out, out):
         def token_major(t0):
             return raw_g[:, t0:t0 + 4, :].rearrange("p t (j a) -> p t a j", j=4)
 
-        def unit(banks, gb, length, out_view):
-            n_stage = {32: 5, 128: 7}[length]
-            w = wk.tile([P, 4 * gb, length], F32, tag="w", name="w")
-            for b in range(4):
-                bv = banks[b][:].rearrange("p (g q two) -> p g q two", g=gb, two=2)
-                odd = sm.tile([P, gb, length // 2], F32, tag="odd", name="odd")
-                nc.scalar.mul(out=odd[:], in_=bv[:, :, :, 1], mul=SCALE)
-                wv = w[:, b * gb:(b + 1) * gb, :].rearrange("p g (h q) -> p g h q", h=2)
-                nc.vector.scalar_tensor_tensor(out=wv[:, :, 0, :], in0=bv[:, :, :, 0], scalar=SCALE, in1=odd[:], op0=ALU.mult, op1=ALU.add)
-                nc.vector.scalar_tensor_tensor(out=wv[:, :, 1, :], in0=bv[:, :, :, 0], scalar=SCALE, in1=odd[:], op0=ALU.mult, op1=ALU.subtract)
-            for s in range(2, n_stage):
-                wn = wk.tile([P, 4 * gb, length], F32, tag="w", name="wn")
-                for half in range(2):
-                    gs = slice(half * 2 * gb, (half + 1) * 2 * gb)
+        def butterfly(out_u, out_v, in_even, in_odd):
+            nc.vector.tensor_tensor(out=out_u, in0=in_even, in1=in_odd, op=ALU.add)
+            nc.vector.tensor_tensor(out=out_v, in0=in_even, in1=in_odd, op=ALU.subtract)
+
+        def first_stage(bank, gb, length, w_rows):
+            bv = bank.rearrange("p (g q two) -> p g q two", g=gb, two=2)
+            odd = sm.tile([P, gb, length // 2], F32, tag="odd", name="odd")
+            nc.scalar.mul(out=odd[:], in_=bv[:, :, :, 1], mul=SCALE)
+            wv = w_rows.rearrange("p g (h q) -> p g h q", h=2)
+            nc.vector.scalar_tensor_tensor(out=wv[:, :, 0, :], in0=bv[:, :, :, 0], scalar=SCALE, in1=odd[:], op0=ALU.mult, op1=ALU.add)
+            nc.vector.scalar_tensor_tensor(out=wv[:, :, 1, :], in0=bv[:, :, :, 0], scalar=SCALE, in1=odd[:], op0=ALU.mult, op1=ALU.subtract)
+
+        def middle_stages(w, groups, length, parts, n_middle):
+            for s in range(n_middle):
+                wn = wk.tile([P, groups, length], F32, tag="w", name="wn")
+                for gs in parts:
                     xv = w[:, gs, :].rearrange("p g (q two) -> p g q two", two=2)
                     yv = wn[:, gs, :].rearrange("p g (h q) -> p g h q", h=2)
-                    nc.vector.tensor_tensor(out=yv[:, :, 0, :], in0=xv[:, :, :, 0], in1=xv[:, :, :, 1], op=ALU.add)
-                    nc.vector.tensor_tensor(out=yv[:, :, 1, :], in0=xv[:, :, :, 0], in1=xv[:, :, :, 1], op=ALU.subtract)
+                    butterfly(yv[:, :, 0, :], yv[:, :, 1, :], xv[:, :, :, 0], xv[:, :, :, 1])
                 w = wn
-            for half in range(2):
-                gs = slice(half * 2 * gb, (half + 1) * 2 * gb)
-                xv = w[:, gs, :].rearrange("p (b g) (q two) -> p b g q two", b=2, two=2)
-                nc.vector.tensor_tensor(out=out_view[:, 2 * half:2 * half + 2, :, 0, :], in0=xv[:, :, :, :, 0], in1=xv[:, :, :, :, 1], op=ALU.add)
-                nc.vector.tensor_tensor(out=out_view[:, 2 * half:2 * half + 2, :, 1, :], in0=xv[:, :, :, :, 0], in1=xv[:, :, :, :, 1], op=ALU.subtract)
+            return w
 
         quantise(0, token_major(0), True)
         banks0 = []
@@ -132,12 +129,19 @@ def tile_fullonlinehadamardhook_kernel(tc, x, had_K, grad_out, out):
         for c in range(4):
             quantise(K * (1 + c), slabs[:, c], False)
 
-        unit(banks0, 4, 128, res[:, 0:N0, :].rearrange("p t (r h q) -> p r t h q", r=4, h=2))
-        nc.sync.dma_start(out=o_view[:, 0:N0, :], in_=res[:, 0:N0, :])
+        w0 = wk.tile([P, 13, M], F32, tag="w", name="w0")
+        first_stage(banks0[0][:], 4, M, w0[:, 0:4, :])
+        for r in range(1, 4):
+            first_stage(banks0[r][:, 0:3 * M], 3, M, w0[:, 1 + 3 * r:4 + 3 * r, :])
+        w0 = middle_stages(w0, 13, M, [slice(0, 4), slice(4, 13)], 5)
+        res0 = res[:, 0:N0, :].rearrange("p t (r h q) -> p r t h q", r=4, h=2)
+        xa = w0[:, 0:4, :].rearrange("p g (q two) -> p g q two", two=2)
+        butterfly(res0[:, 0, :, 0, :], res0[:, 0, :, 1, :], xa[:, :, :, 0], xa[:, :, :, 1])
+        xb = w0[:, 4:13, :].rearrange("p (r g) (q two) -> p r g q two", r=3, two=2)
+        butterfly(res0[:, 1:4, 0:3, 0, :], res0[:, 1:4, 0:3, 1, :], xb[:, :, :, :, 0], xb[:, :, :, :, 1])
 
-        def plain_token(tb):
-            t = TB0 + tb
-            cols = slice(K * 5 + tb * M, K * 5 + (tb + 1) * M)
+        def plain_token(t, col0, r0):
+            cols = slice(col0, col0 + M)
             zp = psz.tile([P, K], F32, name="zp")
             nc.tensor.matmul_mx(
                 out=zp[:],
@@ -146,14 +150,15 @@ def tile_fullonlinehadamardhook_kernel(tc, x, had_K, grad_out, out):
                 start=True, stop=True,
             )
             zs = zsp.tile([P, K], F32, name="zs")
-            nc.scalar.copy(out=zs[:], in_=zp[:])
+            nc.scalar.copy(out=zs[:, r0 * P:], in_=zp[:, r0 * P:])
             op = pso.tile([P, K], F32, name="op")
-            for r in range(4):
+            for r in range(r0, 4):
                 rc = slice(r * P, (r + 1) * P)
                 nc.tensor.matmul(out=op[:, rc], lhsT=zs[:, rc], rhs=hmat[:], start=True, stop=True)
-            nc.scalar.mul(out=res[:, t, :], in_=op[:], mul=SCALE)
-            if tb % 2 == 1:
-                nc.sync.dma_start(out=o_view[:, t - 1:t + 1, :], in_=res[:, t - 1:t + 1, :])
+            nc.scalar.mul(out=res[:, t, r0 * P:], in_=op[:, r0 * P:], mul=SCALE)
+
+        plain_token(3, 3 * M, 1)
+        nc.sync.dma_start(out=o_view[:, 0:N0, :], in_=res[:, 0:N0, :])
 
         for r in range(4):
             banks = []
@@ -171,7 +176,23 @@ def tile_fullonlinehadamardhook_kernel(tc, x, had_K, grad_out, out):
             if r < 3:
                 quantise(K * 5 + r * K, token_major(TB0 + 4 * r), False)
                 for tb in range(4 * r, 4 * r + 4):
-                    plain_token(tb)
+                    t = TB0 + tb
+                    plain_token(t, K * 5 + tb * M, 0)
+                    if tb % 2 == 1:
+                        nc.sync.dma_start(out=o_view[:, t - 1:t + 1, :], in_=res[:, t - 1:t + 1, :])
             rcols = slice(r * M, (r + 1) * M)
-            unit(banks, NA, 32, res[:, TA0:TA0 + NA, rcols].rearrange("p t (d h q) -> p d t h q", d=4, h=2))
-            nc.sync.dma_start(out=o_view[:, TA0:TA0 + NA, rcols], in_=res[:, TA0:TA0 + NA, rcols])
+            w = wk.tile([P, 4 * NA, 32], F32, tag="w", name="w")
+            for d in range(4):
+                first_stage(banks[d][:], NA, 32, w[:, d * NA:(d + 1) * NA, :])
+            w = middle_stages(w, 4 * NA, 32, [slice(0, 2 * NA), slice(2 * NA, 4 * NA)], 3)
+            resa = res[:, TA0:TA0 + NA, rcols].rearrange("p t (d h q) -> p d t h q", d=4, h=2)
+            xv = w[:].rearrange("p (d t) (q two) -> p d t q two", d=4, two=2)
+            n_cut = 4 if r == 3 else 2
+            step = NA // n_cut
+            for i in range(n_cut):
+                ts = slice(i * step, (i + 1) * step)
+                butterfly(resa[:, :, ts, 0, :], resa[:, :, ts, 1, :], xv[:, :, ts, :, 0], xv[:, :, ts, :, 1])
+                if r == 3:
+                    nc.sync.dma_start(out=o_view[:, TA0 + i * step:TA0 + (i + 1) * step, rcols], in_=res[:, TA0 + i * step:TA0 + (i + 1) * step, rcols])
+            if r < 3:
+                nc.sync.dma_start(out=o_view[:, TA0:TA0 + NA, rcols], in_=res[:, TA0:TA0 + NA, rcols])

@@ -95,13 +95,15 @@ def tile_fullonlinehadamardhook_kernel(tc, x, had_K, grad_out, out):
             nc.vector.tensor_tensor(out=out_u, in0=in_even, in1=in_odd, op=ALU.add)
             nc.vector.tensor_tensor(out=out_v, in0=in_even, in1=in_odd, op=ALU.subtract)
 
-        def first_stage(bank, gb, length, w_rows):
-            bv = bank.rearrange("p (g q two) -> p g q two", g=gb, two=2)
-            odd = sm.tile([P, gb, length // 2], F32, tag="odd", name="odd")
-            nc.scalar.mul(out=odd[:], in_=bv[:, :, :, 1], mul=SCALE)
-            wv = w_rows.rearrange("p g (h q) -> p g h q", h=2)
-            nc.vector.scalar_tensor_tensor(out=wv[:, :, 0, :], in0=bv[:, :, :, 0], scalar=SCALE, in1=odd[:], op0=ALU.mult, op1=ALU.add)
-            nc.vector.scalar_tensor_tensor(out=wv[:, :, 1, :], in0=bv[:, :, :, 0], scalar=SCALE, in1=odd[:], op0=ALU.mult, op1=ALU.subtract)
+        def first_stage(bank_views, gb, length, w_rows):
+            n = len(bank_views)
+            half = gb * length // 2
+            planes = sm.tile([P, n, 2, half], F32, tag="planes", name="planes")
+            for b in range(n):
+                nc.scalar.mul(out=planes[:, b], in_=bank_views[b].rearrange("p (x two) -> p two x", two=2), mul=SCALE)
+            pv = planes[:].rearrange("p b two (g q) -> p b two g q", g=gb)
+            wv = w_rows.rearrange("p (b g) (h q) -> p b g h q", b=n, h=2)
+            butterfly(wv[:, :, :, 0, :], wv[:, :, :, 1, :], pv[:, :, 0], pv[:, :, 1])
 
         def middle_stages(w, groups, length, parts, n_middle):
             for s in range(n_middle):
@@ -130,9 +132,8 @@ def tile_fullonlinehadamardhook_kernel(tc, x, had_K, grad_out, out):
             quantise(K * (1 + c), slabs[:, c], False)
 
         w0 = wk.tile([P, 13, M], F32, tag="w", name="w0")
-        first_stage(banks0[0][:], 4, M, w0[:, 0:4, :])
-        for r in range(1, 4):
-            first_stage(banks0[r][:, 0:3 * M], 3, M, w0[:, 1 + 3 * r:4 + 3 * r, :])
+        first_stage([banks0[0][:]], 4, M, w0[:, 0:4, :])
+        first_stage([banks0[r][:, 0:3 * M] for r in range(1, 4)], 3, M, w0[:, 4:13, :])
         w0 = middle_stages(w0, 13, M, [slice(0, 4), slice(4, 13)], 5)
         res0 = res[:, 0:N0, :].rearrange("p t (r h q) -> p r t h q", r=4, h=2)
         xa = w0[:, 0:4, :].rearrange("p g (q two) -> p g q two", two=2)
@@ -182,8 +183,8 @@ def tile_fullonlinehadamardhook_kernel(tc, x, had_K, grad_out, out):
                         nc.sync.dma_start(out=o_view[:, t - 1:t + 1, :], in_=res[:, t - 1:t + 1, :])
             rcols = slice(r * M, (r + 1) * M)
             w = wk.tile([P, 4 * NA, 32], F32, tag="w", name="w")
-            for d in range(4):
-                first_stage(banks[d][:], NA, 32, w[:, d * NA:(d + 1) * NA, :])
+            for d in range(0, 4, 2):
+                first_stage([banks[d][:], banks[d + 1][:]], NA, 32, w[:, d * NA:(d + 2) * NA, :])
             w = middle_stages(w, 4 * NA, 32, [slice(0, 2 * NA), slice(2 * NA, 4 * NA)], 3)
             resa = res[:, TA0:TA0 + NA, rcols].rearrange("p t (d h q) -> p d t h q", d=4, h=2)
             xv = w[:].rearrange("p (d t) (q two) -> p d t q two", d=4, two=2)

@@ -34,7 +34,7 @@ def tile_fullonlinehadamardhook_kernel(tc, x, had_K, grad_out, out):
         keep = ctx.enter_context(tc.tile_pool(name="keep", bufs=1))
         grp = ctx.enter_context(tc.tile_pool(name="grp", bufs=3))
         wk = ctx.enter_context(tc.tile_pool(name="wk", bufs=4))
-        sm = ctx.enter_context(tc.tile_pool(name="sm", bufs=4))
+        sm = ctx.enter_context(tc.tile_pool(name="sm", bufs=2))
         zsp = ctx.enter_context(tc.tile_pool(name="zsp", bufs=3))
         psa = ctx.enter_context(tc.psum_pool(name="psa", bufs=4))
         psz = ctx.enter_context(tc.psum_pool(name="psz", bufs=2))
@@ -95,25 +95,27 @@ def tile_fullonlinehadamardhook_kernel(tc, x, had_K, grad_out, out):
             nc.vector.tensor_tensor(out=out_u, in0=in_even, in1=in_odd, op=ALU.add)
             nc.vector.tensor_tensor(out=out_v, in0=in_even, in1=in_odd, op=ALU.subtract)
 
-        def first_stage(bank_views, gb, length, w_rows):
-            n = len(bank_views)
-            half = gb * length // 2
-            planes = sm.tile([P, n, 2, half], F32, tag="planes", name="planes")
-            for b in range(n):
-                nc.scalar.mul(out=planes[:, b], in_=bank_views[b].rearrange("p (x two) -> p two x", two=2), mul=SCALE)
-            pv = planes[:].rearrange("p b two (g q) -> p b two g q", g=gb)
-            wv = w_rows.rearrange("p (b g) (h q) -> p b g h q", b=n, h=2)
-            butterfly(wv[:, :, :, 0, :], wv[:, :, :, 1, :], pv[:, :, 0], pv[:, :, 1])
+        def empty_bank(bank_view, gb, w_rows):
+            nc.scalar.mul(
+                out=w_rows.rearrange("p g (x y) -> p g x y", y=4),
+                in_=bank_view.rearrange("p (g y x) -> p g x y", g=gb, y=4),
+                mul=SCALE,
+            )
 
-        def middle_stages(w, groups, length, parts, n_middle):
-            for s in range(n_middle):
+        def middle_stages(w, groups, length, parts):
+            for run in [h for h in (64, 32, 16, 8, 4) if h < length]:
                 wn = wk.tile([P, groups, length], F32, tag="w", name="wn")
                 for gs in parts:
-                    xv = w[:, gs, :].rearrange("p g (q two) -> p g q two", two=2)
-                    yv = wn[:, gs, :].rearrange("p g (h q) -> p g h q", h=2)
-                    butterfly(yv[:, :, 0, :], yv[:, :, 1, :], xv[:, :, :, 0], xv[:, :, :, 1])
+                    xv = w[:, gs, :].rearrange("p g (m two h) -> p g m two h", two=2, h=run)
+                    yv = wn[:, gs, :].rearrange("p g (m two h) -> p g m two h", two=2, h=run)
+                    butterfly(yv[:, :, :, 0, :], yv[:, :, :, 1, :], xv[:, :, :, 0, :], xv[:, :, :, 1, :])
                 w = wn
-            return w
+            wn = wk.tile([P, groups, length], F32, tag="w", name="wn")
+            for gs in parts:
+                xv = w[:, gs, :].rearrange("p g (q two) -> p g q two", two=2)
+                yv = wn[:, gs, :].rearrange("p g (h q) -> p g h q", h=2)
+                butterfly(yv[:, :, 0, :], yv[:, :, 1, :], xv[:, :, :, 0], xv[:, :, :, 1])
+            return wn
 
         quantise(0, token_major(0), True)
         banks0 = []
@@ -131,10 +133,11 @@ def tile_fullonlinehadamardhook_kernel(tc, x, had_K, grad_out, out):
         for c in range(4):
             quantise(K * (1 + c), slabs[:, c], False)
 
-        w0 = wk.tile([P, 13, M], F32, tag="w", name="w0")
-        first_stage([banks0[0][:]], 4, M, w0[:, 0:4, :])
-        first_stage([banks0[r][:, 0:3 * M] for r in range(1, 4)], 3, M, w0[:, 4:13, :])
-        w0 = middle_stages(w0, 13, M, [slice(0, 4), slice(4, 13)], 5)
+        w0 = sm.tile([P, 13, M], F32, tag="w0", name="w0")
+        empty_bank(banks0[0][:], 4, w0[:, 0:4, :])
+        for r in range(1, 4):
+            empty_bank(banks0[r][:, 0:3 * M], 3, w0[:, 1 + 3 * r:4 + 3 * r, :])
+        w0 = middle_stages(w0, 13, M, [slice(0, 4), slice(4, 13)])
         res0 = res[:, 0:N0, :].rearrange("p t (r h q) -> p r t h q", r=4, h=2)
         xa = w0[:, 0:4, :].rearrange("p g (q two) -> p g q two", two=2)
         butterfly(res0[:, 0, :, 0, :], res0[:, 0, :, 1, :], xa[:, :, :, 0], xa[:, :, :, 1])
@@ -182,10 +185,10 @@ def tile_fullonlinehadamardhook_kernel(tc, x, had_K, grad_out, out):
                     if tb % 2 == 1:
                         nc.sync.dma_start(out=o_view[:, t - 1:t + 1, :], in_=res[:, t - 1:t + 1, :])
             rcols = slice(r * M, (r + 1) * M)
-            w = wk.tile([P, 4 * NA, 32], F32, tag="w", name="w")
-            for d in range(0, 4, 2):
-                first_stage([banks[d][:], banks[d + 1][:]], NA, 32, w[:, d * NA:(d + 2) * NA, :])
-            w = middle_stages(w, 4 * NA, 32, [slice(0, 2 * NA), slice(2 * NA, 4 * NA)], 3)
+            w = sm.tile([P, 4 * NA, 32], F32, tag="w0", name="w")
+            for d in range(4):
+                empty_bank(banks[d][:], NA, w[:, d * NA:(d + 1) * NA, :])
+            w = middle_stages(w, 4 * NA, 32, [slice(0, 2 * NA), slice(2 * NA, 4 * NA)])
             resa = res[:, TA0:TA0 + NA, rcols].rearrange("p t (d h q) -> p d t h q", d=4, h=2)
             xv = w[:].rearrange("p (d t) (q two) -> p d t q two", d=4, two=2)
             n_cut = 4 if r == 3 else 2

@@ -24,6 +24,7 @@ NA = 16
 NB = 12
 TA0 = N0
 TB0 = N0 + NA
+CUT = 96
 
 
 def tile_fullonlinehadamardhook_kernel(tc, x, had_K, grad_out, out):
@@ -46,17 +47,9 @@ def tile_fullonlinehadamardhook_kernel(tc, x, had_K, grad_out, out):
         for c in range(T // 4):
             nc.sync.dma_start(out=raw_g[:, c * 4:(c + 1) * 4, :], in_=g_view[:, c * 4:(c + 1) * 4, :])
 
-        cur = keep.tile([P, P], F32, name="hid")
-        make_identity(nc, cur[:])
-        for k in range(7):
-            h = 1 << k
-            nxt = keep.tile([P, P], F32, name="hst%d" % k)
-            xv = cur[:].rearrange("p (m two h) -> p m two h", two=2, h=h)
-            yv = nxt[:].rearrange("p (m two h) -> p m two h", two=2, h=h)
-            nc.vector.tensor_tensor(out=yv[:, :, 0, :], in0=xv[:, :, 0, :], in1=xv[:, :, 1, :], op=ALU.add)
-            nc.vector.tensor_tensor(out=yv[:, :, 1, :], in0=xv[:, :, 0, :], in1=xv[:, :, 1, :], op=ALU.subtract)
-            cur = nxt
-        hmat = cur
+        ident = keep.tile([P, P], F32)
+        make_identity(nc, ident[:])
+        hmat = keep.tile([P, P], F32)
 
         g_codes = keep.tile([P, T * M], U32, align_bytes=64)
         g_scales = keep.tile([P, T * M], U8, align_bytes=64)
@@ -69,7 +62,8 @@ def tile_fullonlinehadamardhook_kernel(tc, x, had_K, grad_out, out):
             dst = hg[:].rearrange("p (r q) j -> p r q j", r=4)
             src = raw_h[:].rearrange("p j (q r) -> p r q j", r=4)
             if s == 0:
-                nc.vector.tensor_copy(out=dst, in_=src)
+                nc.vector.tensor_copy(out=dst[:, :, 0:CUT, :], in_=src[:, :, 0:CUT, :])
+                nc.scalar.copy(out=dst[:, :, CUT:, :], in_=src[:, :, CUT:, :])
             else:
                 nc.scalar.mul(out=dst, in_=src, mul=-1.0)
             hc = keep.tile([P, K], U32, align_bytes=64, name="hc%d" % s)
@@ -117,7 +111,13 @@ def tile_fullonlinehadamardhook_kernel(tc, x, had_K, grad_out, out):
                 butterfly(yv[:, :, 0, :], yv[:, :, 1, :], xv[:, :, :, 0], xv[:, :, :, 1])
             return wn
 
-        quantise(0, token_major(0), True)
+        g0 = grp.tile([P, K, 4], BF16, align_bytes=64, tag="g", name="g0")
+        nc.vector.tensor_copy(
+            out=g0[:].rearrange("p (t a) j -> p t a j", t=4)[:, :, 0:CUT, :].rearrange("p t (c i) j -> p t c j i", i=4),
+            in_=raw_g[:, 0:4, :].rearrange("p t (j a) -> p t j a", j=4)[:, :, :, 0:CUT].rearrange("p t j (c i) -> p t c j i", i=4),
+        )
+        nc.scalar.copy(out=g0[:].rearrange("p (t a) j -> p t a j", t=4)[:, :, CUT:, :], in_=token_major(0)[:, :, CUT:, :])
+        nc.vector.quantize_mx(out=g_codes[:, 0:K].bitcast(E5X4), scales=g_scales[:, 0:K], in_=g0[:].rearrange("p c j -> p (c j)"))
         banks0 = []
         for r in range(4):
             bank = psa.tile([P, K], F32, tag="a", name="bank")
@@ -133,16 +133,19 @@ def tile_fullonlinehadamardhook_kernel(tc, x, had_K, grad_out, out):
         for c in range(4):
             quantise(K * (1 + c), slabs[:, c], False)
 
-        w0 = sm.tile([P, 13, M], F32, tag="w0", name="w0")
+        w0 = sm.tile([P, 14, M], F32, tag="w0", name="w0")
         empty_bank(banks0[0][:], 4, w0[:, 0:4, :])
         for r in range(1, 4):
             empty_bank(banks0[r][:, 0:3 * M], 3, w0[:, 1 + 3 * r:4 + 3 * r, :])
-        w0 = middle_stages(w0, 13, M, [slice(0, 4), slice(4, 13)])
+        empty_bank(ident[:], 1, w0[:, 13:14, :])
+        w0 = middle_stages(w0, 14, M, [slice(0, 4), slice(4, 14)])
         res0 = res[:, 0:N0, :].rearrange("p t (r h q) -> p r t h q", r=4, h=2)
         xa = w0[:, 0:4, :].rearrange("p g (q two) -> p g q two", two=2)
         butterfly(res0[:, 0, :, 0, :], res0[:, 0, :, 1, :], xa[:, :, :, 0], xa[:, :, :, 1])
         xb = w0[:, 4:13, :].rearrange("p (r g) (q two) -> p r g q two", r=3, two=2)
         butterfly(res0[:, 1:4, 0:3, 0, :], res0[:, 1:4, 0:3, 1, :], xb[:, :, :, :, 0], xb[:, :, :, :, 1])
+        xh = w0[:, 13, :].rearrange("p (q two) -> p q two", two=2)
+        butterfly(hmat[:, 0:M // 2], hmat[:, M // 2:M], xh[:, :, 0], xh[:, :, 1])
 
         def plain_token(t, col0, r0):
             cols = slice(col0, col0 + M)
@@ -159,7 +162,7 @@ def tile_fullonlinehadamardhook_kernel(tc, x, had_K, grad_out, out):
             for r in range(r0, 4):
                 rc = slice(r * P, (r + 1) * P)
                 nc.tensor.matmul(out=op[:, rc], lhsT=zs[:, rc], rhs=hmat[:], start=True, stop=True)
-            nc.scalar.mul(out=res[:, t, r0 * P:], in_=op[:, r0 * P:], mul=SCALE)
+            nc.scalar.copy(out=res[:, t, r0 * P:], in_=op[:, r0 * P:])
 
         plain_token(3, 3 * M, 1)
         nc.sync.dma_start(out=o_view[:, 0:N0, :], in_=res[:, 0:N0, :])

@@ -24,7 +24,12 @@ NA = 16
 NB = 12
 TA0 = N0
 TB0 = N0 + NA
-CUT = 96
+SUB = 256
+STRIP = 3 * SUB
+STRIP0 = K
+TBC = STRIP0 + 4 * STRIP
+N_COLS = TBC + NB * M
+FOLD3 = (False, False, True, True)
 
 
 def tile_fullonlinehadamardhook_kernel(tc, x, had_K, grad_out, out):
@@ -47,12 +52,20 @@ def tile_fullonlinehadamardhook_kernel(tc, x, had_K, grad_out, out):
         for c in range(T // 4):
             nc.sync.dma_start(out=raw_g[:, c * 4:(c + 1) * 4, :], in_=g_view[:, c * 4:(c + 1) * 4, :])
 
-        ident = keep.tile([P, P], F32)
-        make_identity(nc, ident[:])
-        hmat = keep.tile([P, P], F32)
+        cur = keep.tile([P, P], F32, name="hid")
+        make_identity(nc, cur[:])
+        for k in range(7):
+            h = 1 << k
+            nxt = keep.tile([P, P], F32, name="hst%d" % k)
+            xv = cur[:].rearrange("p (m two h) -> p m two h", two=2, h=h)
+            yv = nxt[:].rearrange("p (m two h) -> p m two h", two=2, h=h)
+            nc.vector.tensor_tensor(out=yv[:, :, 0, :], in0=xv[:, :, 0, :], in1=xv[:, :, 1, :], op=ALU.add)
+            nc.vector.tensor_tensor(out=yv[:, :, 1, :], in0=xv[:, :, 0, :], in1=xv[:, :, 1, :], op=ALU.subtract)
+            cur = nxt
+        hmat = cur
 
-        g_codes = keep.tile([P, T * M], U32, align_bytes=64)
-        g_scales = keep.tile([P, T * M], U8, align_bytes=64)
+        g_codes = keep.tile([P, N_COLS], U32, align_bytes=64)
+        g_scales = keep.tile([P, N_COLS], U8, align_bytes=64)
         res = keep.tile([P, T, K], F32)
 
         h_codes = []
@@ -62,8 +75,7 @@ def tile_fullonlinehadamardhook_kernel(tc, x, had_K, grad_out, out):
             dst = hg[:].rearrange("p (r q) j -> p r q j", r=4)
             src = raw_h[:].rearrange("p j (q r) -> p r q j", r=4)
             if s == 0:
-                nc.vector.tensor_copy(out=dst[:, :, 0:CUT, :], in_=src[:, :, 0:CUT, :])
-                nc.scalar.copy(out=dst[:, :, CUT:, :], in_=src[:, :, CUT:, :])
+                nc.vector.tensor_copy(out=dst, in_=src)
             else:
                 nc.scalar.mul(out=dst, in_=src, mul=-1.0)
             hc = keep.tile([P, K], U32, align_bytes=64, name="hc%d" % s)
@@ -89,11 +101,11 @@ def tile_fullonlinehadamardhook_kernel(tc, x, had_K, grad_out, out):
             nc.vector.tensor_tensor(out=out_u, in0=in_even, in1=in_odd, op=ALU.add)
             nc.vector.tensor_tensor(out=out_v, in0=in_even, in1=in_odd, op=ALU.subtract)
 
-        def empty_bank(bank_view, gb, w_rows):
+        def empty_bank(bank_view, gb, w_rows, scale=SCALE):
             nc.scalar.mul(
                 out=w_rows.rearrange("p g (x y) -> p g x y", y=4),
                 in_=bank_view.rearrange("p (g y x) -> p g x y", g=gb, y=4),
-                mul=SCALE,
+                mul=scale,
             )
 
         def middle_stages(w, groups, length, parts):
@@ -111,13 +123,7 @@ def tile_fullonlinehadamardhook_kernel(tc, x, had_K, grad_out, out):
                 butterfly(yv[:, :, 0, :], yv[:, :, 1, :], xv[:, :, :, 0], xv[:, :, :, 1])
             return wn
 
-        g0 = grp.tile([P, K, 4], BF16, align_bytes=64, tag="g", name="g0")
-        nc.vector.tensor_copy(
-            out=g0[:].rearrange("p (t a) j -> p t a j", t=4)[:, :, 0:CUT, :].rearrange("p t (c i) j -> p t c j i", i=4),
-            in_=raw_g[:, 0:4, :].rearrange("p t (j a) -> p t j a", j=4)[:, :, :, 0:CUT].rearrange("p t j (c i) -> p t c j i", i=4),
-        )
-        nc.scalar.copy(out=g0[:].rearrange("p (t a) j -> p t a j", t=4)[:, :, CUT:, :], in_=token_major(0)[:, :, CUT:, :])
-        nc.vector.quantize_mx(out=g_codes[:, 0:K].bitcast(E5X4), scales=g_scales[:, 0:K], in_=g0[:].rearrange("p c j -> p (c j)"))
+        quantise(0, token_major(0), True)
         banks0 = []
         for r in range(4):
             bank = psa.tile([P, K], F32, tag="a", name="bank")
@@ -129,23 +135,24 @@ def tile_fullonlinehadamardhook_kernel(tc, x, had_K, grad_out, out):
             )
             banks0.append(bank)
 
-        slabs = raw_g[:, TA0:TA0 + NA, :].rearrange("p t (j c e) -> p c t e j", j=4, c=4)
+        subs = raw_g[:, TA0:TA0 + NA, :].rearrange("p t (j c l e) -> p c l t e j", j=4, c=4, l=2)
         for c in range(4):
-            quantise(K * (1 + c), slabs[:, c], False)
+            gt = grp.tile([P, K, 4], BF16, align_bytes=64, tag="g", name="gt")
+            for l in range(2):
+                nc.scalar.copy(out=gt[:, l * SUB:(l + 1) * SUB, :].rearrange("p (t e) j -> p t e j", t=NA), in_=subs[:, c, l])
+            cols = slice(STRIP0 + c * STRIP, STRIP0 + c * STRIP + 2 * SUB)
+            nc.vector.quantize_mx(out=g_codes[:, cols].bitcast(E5X4), scales=g_scales[:, cols], in_=gt[:].rearrange("p c j -> p (c j)"))
 
-        w0 = sm.tile([P, 14, M], F32, tag="w0", name="w0")
+        w0 = sm.tile([P, 13, M], F32, tag="w0", name="w0")
         empty_bank(banks0[0][:], 4, w0[:, 0:4, :])
         for r in range(1, 4):
             empty_bank(banks0[r][:, 0:3 * M], 3, w0[:, 1 + 3 * r:4 + 3 * r, :])
-        empty_bank(ident[:], 1, w0[:, 13:14, :])
-        w0 = middle_stages(w0, 14, M, [slice(0, 4), slice(4, 14)])
+        w0 = middle_stages(w0, 13, M, [slice(0, 4), slice(4, 13)])
         res0 = res[:, 0:N0, :].rearrange("p t (r h q) -> p r t h q", r=4, h=2)
         xa = w0[:, 0:4, :].rearrange("p g (q two) -> p g q two", two=2)
         butterfly(res0[:, 0, :, 0, :], res0[:, 0, :, 1, :], xa[:, :, :, 0], xa[:, :, :, 1])
         xb = w0[:, 4:13, :].rearrange("p (r g) (q two) -> p r g q two", r=3, two=2)
         butterfly(res0[:, 1:4, 0:3, 0, :], res0[:, 1:4, 0:3, 1, :], xb[:, :, :, :, 0], xb[:, :, :, :, 1])
-        xh = w0[:, 13, :].rearrange("p (q two) -> p q two", two=2)
-        butterfly(hmat[:, 0:M // 2], hmat[:, M // 2:M], xh[:, :, 0], xh[:, :, 1])
 
         def plain_token(t, col0, r0):
             cols = slice(col0, col0 + M)
@@ -162,38 +169,69 @@ def tile_fullonlinehadamardhook_kernel(tc, x, had_K, grad_out, out):
             for r in range(r0, 4):
                 rc = slice(r * P, (r + 1) * P)
                 nc.tensor.matmul(out=op[:, rc], lhsT=zs[:, rc], rhs=hmat[:], start=True, stop=True)
-            nc.scalar.copy(out=res[:, t, r0 * P:], in_=op[:, r0 * P:])
+            nc.scalar.mul(out=res[:, t, r0 * P:], in_=op[:, r0 * P:], mul=SCALE)
 
-        plain_token(3, 3 * M, 1)
-        nc.sync.dma_start(out=o_view[:, 0:N0, :], in_=res[:, 0:N0, :])
+        def plain_chunk_prepare(k):
+            quantise(TBC + k * K, token_major(TB0 + 4 * k), False)
 
-        for r in range(4):
+        def plain_chunk(k):
+            for tb in range(4 * k, 4 * k + 4):
+                t = TB0 + tb
+                plain_token(t, TBC + tb * M, 0)
+                if tb % 2 == 1:
+                    nc.sync.dma_start(out=o_view[:, t - 1:t + 1, :], in_=res[:, t - 1:t + 1, :])
+
+        def strip_extras():
+            for c in range(4):
+                gn = grp.tile([P, SUB, 4], BF16, align_bytes=64, tag="gn", name="gn")
+                nc.scalar.mul(out=gn[:].rearrange("p (t e) j -> p t e j", t=NA), in_=subs[:, c, 0], mul=-1.0)
+                cols = slice(STRIP0 + c * STRIP + 2 * SUB, STRIP0 + (c + 1) * STRIP)
+                nc.vector.quantize_mx(out=g_codes[:, cols].bitcast(E5X4), scales=g_scales[:, cols], in_=gn[:].rearrange("p c j -> p (c j)"))
+
+        def unit_banks(r):
             banks = []
             for d in range(4):
                 bank = psa.tile([P, K], F32, tag="a", name="bank")
+                windows = []
                 for c in range(4):
                     s = (((c & d) >> 1) ^ (c & d)) & 1
+                    windows.append((s, STRIP0 + c * STRIP))
+                    if FOLD3[r]:
+                        windows.append((s, STRIP0 + c * STRIP + SUB))
+                for i in range(len(windows)):
+                    s, col = windows[i]
                     nc.tensor.matmul_mx(
                         out=bank[:],
                         lhsT=h_codes[s][:, r * P:(r + 1) * P].bitcast(E4X4), lhsT_scale=h_scales[s][:, r * P:(r + 1) * P],
-                        rhs=g_codes[:, K * (1 + c):K * (2 + c)].bitcast(E5X4), rhs_scale=g_scales[:, K * (1 + c):K * (2 + c)],
-                        start=(c == 0), stop=(c == 3),
+                        rhs=g_codes[:, col:col + K].bitcast(E5X4), rhs_scale=g_scales[:, col:col + K],
+                        start=(i == 0), stop=(i == len(windows) - 1),
                     )
                 banks.append(bank)
-            if r < 3:
-                quantise(K * 5 + r * K, token_major(TB0 + 4 * r), False)
-                for tb in range(4 * r, 4 * r + 4):
-                    t = TB0 + tb
-                    plain_token(t, K * 5 + tb * M, 0)
-                    if tb % 2 == 1:
-                        nc.sync.dma_start(out=o_view[:, t - 1:t + 1, :], in_=res[:, t - 1:t + 1, :])
-            rcols = slice(r * M, (r + 1) * M)
-            w = sm.tile([P, 4 * NA, 32], F32, tag="w0", name="w")
+            return banks
+
+        def unit_empty(r, banks):
+            w = sm.tile([P, 8 * NA, 16], F32, tag="w0", name="w")
             for d in range(4):
-                empty_bank(banks[d][:], NA, w[:, d * NA:(d + 1) * NA, :])
-            w = middle_stages(w, 4 * NA, 32, [slice(0, 2 * NA), slice(2 * NA, 4 * NA)])
-            resa = res[:, TA0:TA0 + NA, rcols].rearrange("p t (d h q) -> p d t h q", d=4, h=2)
-            xv = w[:].rearrange("p (d t) (q two) -> p d t q two", d=4, two=2)
+                g0 = d * 2 * NA
+                if FOLD3[r]:
+                    empty_bank(banks[d][:, 0:SUB], NA, w[:, g0:g0 + NA, :])
+                    empty_bank(banks[d][:, SUB:K], NA, w[:, g0 + NA:g0 + 2 * NA, :], -SCALE)
+                else:
+                    empty_bank(banks[d][:], 2 * NA, w[:, g0:g0 + 2 * NA, :])
+            return w
+
+        def unit_stages(r, w):
+            rcols = slice(r * M, (r + 1) * M)
+            if not FOLD3[r]:
+                wn = wk.tile([P, 8 * NA, 16], F32, tag="w", name="wn")
+                xv = w[:].rearrange("p (d l g) x -> p d l (g x)", d=4, l=2)
+                yv = wn[:].rearrange("p (d l g) x -> p d l (g x)", d=4, l=2)
+                for ds in (slice(0, 2), slice(2, 4)):
+                    butterfly(yv[:, ds, 0, :], yv[:, ds, 1, :], xv[:, ds, 0, :], xv[:, ds, 1, :])
+                w = wn
+            w = middle_stages(w, 8 * NA, 16, [slice(0, 4 * NA), slice(4 * NA, 8 * NA)])
+            resa = res[:, TA0:TA0 + NA, rcols].rearrange("p t (d h q) -> p d t h q", d=8, h=2)
+            xv = w[:].rearrange("p (d t) (q two) -> p d t q two", d=8, two=2)
             n_cut = 4 if r == 3 else 2
             step = NA // n_cut
             for i in range(n_cut):
@@ -203,3 +241,17 @@ def tile_fullonlinehadamardhook_kernel(tc, x, had_K, grad_out, out):
                     nc.sync.dma_start(out=o_view[:, TA0 + i * step:TA0 + (i + 1) * step, rcols], in_=res[:, TA0 + i * step:TA0 + (i + 1) * step, rcols])
             if r < 3:
                 nc.sync.dma_start(out=o_view[:, TA0:TA0 + NA, rcols], in_=res[:, TA0:TA0 + NA, rcols])
+
+        plain_token(3, 3 * M, 1)
+        nc.sync.dma_start(out=o_view[:, 0:N0, :], in_=res[:, 0:N0, :])
+
+        ws = [unit_empty(0, unit_banks(0))]
+        strip_extras()
+        ws.append(unit_empty(1, unit_banks(1)))
+        for r in range(4):
+            if r < 3:
+                plain_chunk_prepare(r)
+                plain_chunk(r)
+            unit_stages(r, ws[r])
+            if r < 2:
+                ws.append(unit_empty(r + 2, unit_banks(r + 2)))

@@ -39,60 +39,48 @@ def tile_fullonlinehadamardhook_kernel(tc, x, had_K, grad_out, out):
     with ExitStack() as ctx:
         keep = ctx.enter_context(tc.tile_pool(name="keep", bufs=1))
         grp = ctx.enter_context(tc.tile_pool(name="grp", bufs=3))
+        ngp = ctx.enter_context(tc.tile_pool(name="ngp", bufs=4))
         wk = ctx.enter_context(tc.tile_pool(name="wk", bufs=4))
-        sm = ctx.enter_context(tc.tile_pool(name="sm", bufs=2))
+        sm = ctx.enter_context(tc.tile_pool(name="sm", bufs=3))
         zsp = ctx.enter_context(tc.tile_pool(name="zsp", bufs=3))
         psa = ctx.enter_context(tc.psum_pool(name="psa", bufs=4))
         psz = ctx.enter_context(tc.psum_pool(name="psz", bufs=2))
         pso = ctx.enter_context(tc.psum_pool(name="pso", bufs=2))
+        ctx.enter_context(tc.manual_schedule())
 
         raw_h = keep.tile([P, 4, K], BF16)
         nc.sync.dma_start(out=raw_h[:], in_=had_K.rearrange("(p j) c -> p j c", j=4))
         raw_g = keep.tile([P, T, K], BF16)
-        for c in range(T // 4):
+        for c in LOAD_ORDER:
             nc.sync.dma_start(out=raw_g[:, c * 4:(c + 1) * 4, :], in_=g_view[:, c * 4:(c + 1) * 4, :])
 
-        cur = keep.tile([P, P], F32, name="hid")
-        make_identity(nc, cur[:])
-        for k in range(7):
+        hts = [keep.tile([P, P], F32, name="hst%d" % k) for k in range(8)]
+        make_identity(nc, hts[0][:])
+
+        def h_stage(k):
             h = 1 << k
-            nxt = keep.tile([P, P], F32, name="hst%d" % k)
-            xv = cur[:].rearrange("p (m two h) -> p m two h", two=2, h=h)
-            yv = nxt[:].rearrange("p (m two h) -> p m two h", two=2, h=h)
+            xv = hts[k][:].rearrange("p (m two h) -> p m two h", two=2, h=h)
+            yv = hts[k + 1][:].rearrange("p (m two h) -> p m two h", two=2, h=h)
             nc.vector.tensor_tensor(out=yv[:, :, 0, :], in0=xv[:, :, 0, :], in1=xv[:, :, 1, :], op=ALU.add)
             nc.vector.tensor_tensor(out=yv[:, :, 1, :], in0=xv[:, :, 0, :], in1=xv[:, :, 1, :], op=ALU.subtract)
-            cur = nxt
-        hmat = cur
+
+        hmat = hts[7]
 
         g_codes = keep.tile([P, N_COLS], U32, align_bytes=64)
         g_scales = keep.tile([P, N_COLS], U8, align_bytes=64)
         res = keep.tile([P, T, K], F32)
 
-        h_codes = []
-        h_scales = []
-        for s in range(2):
-            hg = keep.tile([P, K, 4], BF16, align_bytes=64, name="hg%d" % s)
-            dst = hg[:].rearrange("p (r q) j -> p r q j", r=4)
-            src = raw_h[:].rearrange("p j (q r) -> p r q j", r=4)
-            if s == 0:
-                nc.vector.tensor_copy(out=dst, in_=src)
-            else:
-                nc.scalar.mul(out=dst, in_=src, mul=-1.0)
-            hc = keep.tile([P, K], U32, align_bytes=64, name="hc%d" % s)
-            hs = keep.tile([P, K], U8, align_bytes=64, name="hs%d" % s)
-            nc.vector.quantize_mx(out=hc[:].bitcast(E4X4), scales=hs[:], in_=hg[:].rearrange("p c j -> p (c j)"))
-            h_codes.append(hc)
-            h_scales.append(hs)
+        def quant_g(col0, width, tile_ap):
+            cols = slice(col0, col0 + width)
+            nc.vector.quantize_mx(out=g_codes[:, cols].bitcast(E5X4), scales=g_scales[:, cols], in_=tile_ap)
 
-        def quantise(col0, src4, on_vector):
-            gt = grp.tile([P, K, 4], BF16, align_bytes=64, tag="g", name="gt")
-            dst = gt[:].rearrange("p (x y) j -> p x y j", x=src4.shape[1])
-            if on_vector:
-                nc.vector.tensor_copy(out=dst, in_=src4)
-            else:
-                nc.scalar.copy(out=dst, in_=src4)
-            cols = slice(col0, col0 + K)
-            nc.vector.quantize_mx(out=g_codes[:, cols].bitcast(E5X4), scales=g_scales[:, cols], in_=gt[:].rearrange("p c j -> p (c j)"))
+        hg = [keep.tile([P, K, 4], BF16, align_bytes=64, name="hg%d" % s) for s in range(2)]
+        h_codes = [keep.tile([P, K], U32, align_bytes=64, name="hc%d" % s) for s in range(2)]
+        h_scales = [keep.tile([P, K], U8, align_bytes=64, name="hs%d" % s) for s in range(2)]
+        h_src = raw_h[:].rearrange("p j (q r) -> p r q j", r=4)
+
+        def quant_h(s):
+            nc.vector.quantize_mx(out=h_codes[s][:].bitcast(E4X4), scales=h_scales[s][:], in_=hg[s][:].rearrange("p c j -> p (c j)"))
 
         def token_major(t0):
             return raw_g[:, t0:t0 + 4, :].rearrange("p t (j a) -> p t a j", j=4)
@@ -101,60 +89,59 @@ def tile_fullonlinehadamardhook_kernel(tc, x, had_K, grad_out, out):
             nc.vector.tensor_tensor(out=out_u, in0=in_even, in1=in_odd, op=ALU.add)
             nc.vector.tensor_tensor(out=out_v, in0=in_even, in1=in_odd, op=ALU.subtract)
 
-        def empty_bank(bank_view, gb, w_rows, scale=SCALE):
+        def empty_bank(bank_view, gb, w_rows):
             nc.scalar.mul(
                 out=w_rows.rearrange("p g (x y) -> p g x y", y=4),
                 in_=bank_view.rearrange("p (g y x) -> p g x y", g=gb, y=4),
-                mul=scale,
+                mul=SCALE,
             )
 
-        def middle_stages(w, groups, length, parts):
-            for run in [h for h in (64, 32, 16, 8, 4) if h < length]:
-                wn = wk.tile([P, groups, length], F32, tag="w", name="wn")
-                for gs in parts:
+        def mx(bank, s, r, col, start, stop):
+            nc.tensor.matmul_mx(
+                out=bank[:],
+                lhsT=h_codes[s][:, r * P:(r + 1) * P].bitcast(E4X4), lhsT_scale=h_scales[s][:, r * P:(r + 1) * P],
+                rhs=g_codes[:, col:col + K].bitcast(E5X4), rhs_scale=g_scales[:, col:col + K],
+                start=start, stop=stop,
+            )
+
+        def stage_steps(first, groups, length, parts, final):
+            state = first
+            steps = []
+
+            def mid(run, gs, new):
+                def f():
+                    if new:
+                        state.append(wk.tile([P, groups, length], F32, tag="w", name="wn"))
+                    w, wn = state[-2], state[-1]
                     xv = w[:, gs, :].rearrange("p g (m two h) -> p g m two h", two=2, h=run)
                     yv = wn[:, gs, :].rearrange("p g (m two h) -> p g m two h", two=2, h=run)
                     butterfly(yv[:, :, :, 0, :], yv[:, :, :, 1, :], xv[:, :, :, 0, :], xv[:, :, :, 1, :])
-                w = wn
-            wn = wk.tile([P, groups, length], F32, tag="w", name="wn")
-            for gs in parts:
-                xv = w[:, gs, :].rearrange("p g (q two) -> p g q two", two=2)
-                yv = wn[:, gs, :].rearrange("p g (h q) -> p g h q", h=2)
-                butterfly(yv[:, :, 0, :], yv[:, :, 1, :], xv[:, :, :, 0], xv[:, :, :, 1])
-            return wn
+                return f
 
-        quantise(0, token_major(0), True)
-        banks0 = []
-        for r in range(4):
-            bank = psa.tile([P, K], F32, tag="a", name="bank")
-            nc.tensor.matmul_mx(
-                out=bank[:],
-                lhsT=h_codes[0][:, r * P:(r + 1) * P].bitcast(E4X4), lhsT_scale=h_scales[0][:, r * P:(r + 1) * P],
-                rhs=g_codes[:, 0:K].bitcast(E5X4), rhs_scale=g_scales[:, 0:K],
-                start=True, stop=True,
-            )
-            banks0.append(bank)
+            def shuf(gs, new):
+                def f():
+                    if new:
+                        state.append(wk.tile([P, groups, length], F32, tag="w", name="wn"))
+                    w, wn = state[-2], state[-1]
+                    xv = w[:, gs, :].rearrange("p g (q two) -> p g q two", two=2)
+                    yv = wn[:, gs, :].rearrange("p g (h q) -> p g h q", h=2)
+                    butterfly(yv[:, :, 0, :], yv[:, :, 1, :], xv[:, :, :, 0], xv[:, :, :, 1])
+                return f
 
-        subs = raw_g[:, TA0:TA0 + NA, :].rearrange("p t (j c l e) -> p c l t e j", j=4, c=4, l=2)
-        for c in range(4):
-            gt = grp.tile([P, K, 4], BF16, align_bytes=64, tag="g", name="gt")
-            for l in range(2):
-                nc.scalar.copy(out=gt[:, l * SUB:(l + 1) * SUB, :].rearrange("p (t e) j -> p t e j", t=NA), in_=subs[:, c, l])
-            cols = slice(STRIP0 + c * STRIP, STRIP0 + c * STRIP + 2 * SUB)
-            nc.vector.quantize_mx(out=g_codes[:, cols].bitcast(E5X4), scales=g_scales[:, cols], in_=gt[:].rearrange("p c j -> p (c j)"))
+            for run in [h for h in (64, 32, 16, 8, 4) if h < length]:
+                for i, gs in enumerate(parts):
+                    steps.append(mid(run, gs, i == 0))
+            for i, gs in enumerate(parts):
+                steps.append(shuf(gs, i == 0))
+            for f in final(state):
+                steps.append(f)
+            return steps
 
-        w0 = sm.tile([P, 13, M], F32, tag="w0", name="w0")
-        empty_bank(banks0[0][:], 4, w0[:, 0:4, :])
-        for r in range(1, 4):
-            empty_bank(banks0[r][:, 0:3 * M], 3, w0[:, 1 + 3 * r:4 + 3 * r, :])
-        w0 = middle_stages(w0, 13, M, [slice(0, 4), slice(4, 13)])
-        res0 = res[:, 0:N0, :].rearrange("p t (r h q) -> p r t h q", r=4, h=2)
-        xa = w0[:, 0:4, :].rearrange("p g (q two) -> p g q two", two=2)
-        butterfly(res0[:, 0, :, 0, :], res0[:, 0, :, 1, :], xa[:, :, :, 0], xa[:, :, :, 1])
-        xb = w0[:, 4:13, :].rearrange("p (r g) (q two) -> p r g q two", r=3, two=2)
-        butterfly(res0[:, 1:4, 0:3, 0, :], res0[:, 1:4, 0:3, 1, :], xb[:, :, :, :, 0], xb[:, :, :, :, 1])
+        zps = {}
+        zss = {}
+        ops = {}
 
-        def plain_token(t, col0, r0):
+        def zpass(t, col0):
             cols = slice(col0, col0 + M)
             zp = psz.tile([P, K], F32, name="zp")
             nc.tensor.matmul_mx(
@@ -163,95 +150,281 @@ def tile_fullonlinehadamardhook_kernel(tc, x, had_K, grad_out, out):
                 rhs=h_codes[0][:].bitcast(E4X4), rhs_scale=h_scales[0][:],
                 start=True, stop=True,
             )
+            zps[t] = zp
+
+        def zcopy(t, r0):
             zs = zsp.tile([P, K], F32, name="zs")
-            nc.scalar.copy(out=zs[:, r0 * P:], in_=zp[:, r0 * P:])
+            nc.scalar.copy(out=zs[:, r0 * P:], in_=zps[t][:, r0 * P:])
+            zss[t] = zs
+
+        def hmm(t, r0):
             op = pso.tile([P, K], F32, name="op")
             for r in range(r0, 4):
                 rc = slice(r * P, (r + 1) * P)
-                nc.tensor.matmul(out=op[:, rc], lhsT=zs[:, rc], rhs=hmat[:], start=True, stop=True)
-            nc.scalar.mul(out=res[:, t, r0 * P:], in_=op[:, r0 * P:], mul=SCALE)
+                nc.tensor.matmul(out=op[:, rc], lhsT=zss[t][:, rc], rhs=hmat[:], start=True, stop=True)
+            ops[t] = op
 
-        def plain_chunk_prepare(k):
-            quantise(TBC + k * K, token_major(TB0 + 4 * k), False)
+        def revac(t, r0):
+            nc.scalar.mul(out=res[:, t, r0 * P:], in_=ops[t][:, r0 * P:], mul=SCALE)
 
-        def plain_chunk(k):
-            for tb in range(4 * k, 4 * k + 4):
-                t = TB0 + tb
-                plain_token(t, TBC + tb * M, 0)
-                if tb % 2 == 1:
-                    nc.sync.dma_start(out=o_view[:, t - 1:t + 1, :], in_=res[:, t - 1:t + 1, :])
+        def store_tokens(t0, t1, eng=None):
+            (eng or nc.sync).dma_start(out=o_view[:, t0:t1, :], in_=res[:, t0:t1, :])
 
-        def strip_extras():
+        def prep_copy(k):
+            gt = grp.tile([P, K, 4], BF16, align_bytes=64, tag="g", name="gt")
+            nc.scalar.copy(out=gt[:].rearrange("p (x y) j -> p x y j", x=4), in_=token_major(TB0 + 4 * k))
+            return gt
+
+        subs = raw_g[:, TA0:TA0 + NA, :].rearrange("p t (j c l e) -> p c l t e j", j=4, c=4, l=2)
+
+        def strip_copy(c):
+            gt = grp.tile([P, K, 4], BF16, align_bytes=64, tag="g", name="gt")
+            for pos in range(2):
+                nc.scalar.copy(out=gt[:, pos * SUB:(pos + 1) * SUB, :].rearrange("p (t e) j -> p t e j", t=NA), in_=subs[:, c, 1 - pos])
+            return gt
+
+        def neg_copy(c):
+            gn = ngp.tile([P, SUB, 4], BF16, align_bytes=64, tag="gn", name="gn")
+            nc.scalar.mul(out=gn[:].rearrange("p (t e) j -> p t e j", t=NA), in_=subs[:, c, 1], mul=-1.0)
+            return gn
+
+        def windows(r, d):
+            ws = []
             for c in range(4):
-                gn = grp.tile([P, SUB, 4], BF16, align_bytes=64, tag="gn", name="gn")
-                nc.scalar.mul(out=gn[:].rearrange("p (t e) j -> p t e j", t=NA), in_=subs[:, c, 0], mul=-1.0)
-                cols = slice(STRIP0 + c * STRIP + 2 * SUB, STRIP0 + (c + 1) * STRIP)
-                nc.vector.quantize_mx(out=g_codes[:, cols].bitcast(E5X4), scales=g_scales[:, cols], in_=gn[:].rearrange("p c j -> p (c j)"))
-
-        def unit_banks(r):
-            banks = []
-            for d in range(4):
-                bank = psa.tile([P, K], F32, tag="a", name="bank")
-                windows = []
-                for c in range(4):
-                    s = (((c & d) >> 1) ^ (c & d)) & 1
-                    windows.append((s, STRIP0 + c * STRIP))
-                    if FOLD3[r]:
-                        windows.append((s, STRIP0 + c * STRIP + SUB))
-                for i in range(len(windows)):
-                    s, col = windows[i]
-                    nc.tensor.matmul_mx(
-                        out=bank[:],
-                        lhsT=h_codes[s][:, r * P:(r + 1) * P].bitcast(E4X4), lhsT_scale=h_scales[s][:, r * P:(r + 1) * P],
-                        rhs=g_codes[:, col:col + K].bitcast(E5X4), rhs_scale=g_scales[:, col:col + K],
-                        start=(i == 0), stop=(i == len(windows) - 1),
-                    )
-                banks.append(bank)
-            return banks
-
-        def unit_empty(r, banks):
-            w = sm.tile([P, 8 * NA, 16], F32, tag="w0", name="w")
-            for d in range(4):
-                g0 = d * 2 * NA
+                s = (((c & d) >> 1) ^ (c & d)) & 1
+                ws.append((c, s, STRIP0 + c * STRIP))
                 if FOLD3[r]:
-                    empty_bank(banks[d][:, 0:SUB], NA, w[:, g0:g0 + NA, :])
-                    empty_bank(banks[d][:, SUB:K], NA, w[:, g0 + NA:g0 + 2 * NA, :], -SCALE)
-                else:
-                    empty_bank(banks[d][:], 2 * NA, w[:, g0:g0 + 2 * NA, :])
-            return w
+                    ws.append((c, s, STRIP0 + c * STRIP + SUB))
+            return ws
 
-        def unit_stages(r, w):
+        def bank_passes(r, d):
+            bank = psa.tile([P, K], F32, tag="a", name="bank")
+            ws = windows(r, d)
+            for i, (c, s, col) in enumerate(ws):
+                mx(bank, s, r, col, i == 0, i == len(ws) - 1)
+            return bank
+
+        def unit_steps(r, w):
             rcols = slice(r * M, (r + 1) * M)
+            halves = [slice(0, 4 * NA), slice(4 * NA, 8 * NA)]
+            pre = []
+            state0 = [w]
             if not FOLD3[r]:
-                wn = wk.tile([P, 8 * NA, 16], F32, tag="w", name="wn")
-                xv = w[:].rearrange("p (d l g) x -> p d l (g x)", d=4, l=2)
-                yv = wn[:].rearrange("p (d l g) x -> p d l (g x)", d=4, l=2)
-                for ds in (slice(0, 2), slice(2, 4)):
-                    butterfly(yv[:, ds, 0, :], yv[:, ds, 1, :], xv[:, ds, 0, :], xv[:, ds, 1, :])
-                w = wn
-            w = middle_stages(w, 8 * NA, 16, [slice(0, 4 * NA), slice(4 * NA, 8 * NA)])
-            resa = res[:, TA0:TA0 + NA, rcols].rearrange("p t (d h q) -> p d t h q", d=8, h=2)
-            xv = w[:].rearrange("p (d t) (q two) -> p d t q two", d=8, two=2)
-            n_cut = 4 if r == 3 else 2
-            step = NA // n_cut
-            for i in range(n_cut):
-                ts = slice(i * step, (i + 1) * step)
-                butterfly(resa[:, :, ts, 0, :], resa[:, :, ts, 1, :], xv[:, :, ts, :, 0], xv[:, :, ts, :, 1])
-                if r == 3:
-                    nc.sync.dma_start(out=o_view[:, TA0 + i * step:TA0 + (i + 1) * step, rcols], in_=res[:, TA0 + i * step:TA0 + (i + 1) * step, rcols])
-            if r < 3:
-                nc.sync.dma_start(out=o_view[:, TA0:TA0 + NA, rcols], in_=res[:, TA0:TA0 + NA, rcols])
+                def lstage(ds, new):
+                    def f():
+                        if new:
+                            state0.append(wk.tile([P, 8 * NA, 16], F32, tag="w", name="wn"))
+                        xv = state0[0][:].rearrange("p (d l g) x -> p d l (g x)", d=4, l=2)
+                        yv = state0[1][:].rearrange("p (d l g) x -> p d l (g x)", d=4, l=2)
+                        butterfly(yv[:, ds, 0, :], yv[:, ds, 1, :], xv[:, ds, 1, :], xv[:, ds, 0, :])
+                    return f
+                pre = [lstage(slice(0, 2), True), lstage(slice(2, 4), False)]
 
-        plain_token(3, 3 * M, 1)
-        nc.sync.dma_start(out=o_view[:, 0:N0, :], in_=res[:, 0:N0, :])
+            def final(state):
+                n_cut = 4 if r == LAST_UNIT else 2
+                step = NA // n_cut
+                fs = []
+                def half(i):
+                    def f():
+                        resa = res[:, TA0:TA0 + NA, rcols].rearrange("p t (d h q) -> p d t h q", d=8, h=2)
+                        xv = state[-1][:].rearrange("p (d t) (q two) -> p d t q two", d=8, two=2)
+                        ds = slice(4 * i, 4 * i + 4)
+                        butterfly(resa[:, ds, :, 0, :], resa[:, ds, :, 1, :], xv[:, ds, :, :, 0], xv[:, ds, :, :, 1])
+                        if i == 1:
+                            nc.sync.dma_start(out=o_view[:, TA0:TA0 + NA, rcols], in_=res[:, TA0:TA0 + NA, rcols])
+                    return f
+                if r != LAST_UNIT:
+                    return [half(0), half(1)]
 
-        ws = [unit_empty(0, unit_banks(0))]
-        strip_extras()
-        ws.append(unit_empty(1, unit_banks(1)))
+                def cut(i):
+                    def f():
+                        resa = res[:, TA0:TA0 + NA, rcols].rearrange("p t (d h q) -> p d t h q", d=8, h=2)
+                        xv = state[-1][:].rearrange("p (d t) (q two) -> p d t q two", d=8, two=2)
+                        ts = slice(i * step, (i + 1) * step)
+                        butterfly(resa[:, :, ts, 0, :], resa[:, :, ts, 1, :], xv[:, :, ts, :, 0], xv[:, :, ts, :, 1])
+                        if r == LAST_UNIT:
+                            nc.sync.dma_start(out=o_view[:, TA0 + i * step:TA0 + (i + 1) * step, rcols], in_=res[:, TA0 + i * step:TA0 + (i + 1) * step, rcols])
+                        elif i == n_cut - 1:
+                            nc.sync.dma_start(out=o_view[:, TA0:TA0 + NA, rcols], in_=res[:, TA0:TA0 + NA, rcols])
+                    return f
+                return [cut(i) for i in range(n_cut)]
+
+            return pre, state0, halves, final
+
+        LAST_UNIT = 3
+
+        hk = [0]
+
+        def h_next(n=1):
+            for i in range(n):
+                if hk[0] < 7:
+                    h_stage(hk[0])
+                    hk[0] += 1
+
+        vq = []
+        vpos = [0]
+
+        def pull(n):
+            for f in vq[vpos[0]:vpos[0] + n]:
+                f()
+            vpos[0] = min(vpos[0] + n, len(vq))
+
+        plain = [TB0 + i for i in range(NB)]
+        front = [0]
+        back = [0]
+
+        def plain_front(n):
+            for t in plain[front[0]:front[0] + n]:
+                zpass(t, TBC + (t - TB0) * M)
+                zcopy(t, 0)
+            front[0] += n
+
+        def plain_back(n):
+            for t in plain[back[0]:back[0] + n]:
+                hmm(t, 0)
+                revac(t, 0)
+                store_tokens(t, t + 1, PLAIN_Q and nc.scalar)
+            back[0] += n
+
+        gts = {}
+        gns = {}
+        wU = {}
+
+        def flat(t):
+            return t[:].rearrange("p c j -> p (c j)")
+
+        h_next(H_FIRST)
+        nc.vector.tensor_copy(out=hg[0][:].rearrange("p (r q) j -> p r q j", r=4), in_=h_src)
+        gt0 = grp.tile([P, K, 4], BF16, align_bytes=64, tag="g", name="gt")
+        g0dst = gt0[:].rearrange("p (x y) j -> p x y j", x=4)
+        g0src = token_major(0)
+        nc.scalar.copy(out=g0dst[:, G0_V:4], in_=g0src[:, G0_V:4])
+        nc.vector.tensor_copy(out=g0dst[:, 0:G0_V], in_=g0src[:, 0:G0_V])
+        quant_h(0)
+        nc.vector.tensor_scalar_mul(out=flat(hg[1]), in0=flat(hg[0]), scalar1=-1.0)
+        quant_g(0, K, flat(gt0))
+        banks0 = []
         for r in range(4):
-            if r < 3:
-                plain_chunk_prepare(r)
-                plain_chunk(r)
-            unit_stages(r, ws[r])
-            if r < 2:
-                ws.append(unit_empty(r + 2, unit_banks(r + 2)))
+            bank = psa.tile([P, K], F32, tag="a", name="bank")
+            mx(bank, 0, r, 0, True, True)
+            banks0.append(bank)
+        zpass(3, 3 * M)
+        w0 = sm.tile([P, 13, M], F32, tag="w0", name="w0")
+        empty_bank(banks0[0][:], 4, w0[:, 0:4, :])
+        for r in range(1, 4):
+            empty_bank(banks0[r][:, 0:3 * M], 3, w0[:, 1 + 3 * r:4 + 3 * r, :])
+        zcopy(3, 1)
+        h_next()
+        quant_h(1)
+        h_next(7)
+
+        def final0(state):
+            def fa():
+                res0 = res[:, 0:N0, :].rearrange("p t (r h q) -> p r t h q", r=4, h=2)
+                xa = state[-1][:, 0:4, :].rearrange("p g (q two) -> p g q two", two=2)
+                butterfly(res0[:, 0, :, 0, :], res0[:, 0, :, 1, :], xa[:, :, :, 0], xa[:, :, :, 1])
+            def fb():
+                res0 = res[:, 0:N0, :].rearrange("p t (r h q) -> p r t h q", r=4, h=2)
+                xb = state[-1][:, 4:13, :].rearrange("p (r g) (q two) -> p r g q two", r=3, two=2)
+                butterfly(res0[:, 1:4, 0:3, 0, :], res0[:, 1:4, 0:3, 1, :], xb[:, :, :, :, 0], xb[:, :, :, :, 1])
+                store_tokens(0, N0)
+            return [fa, fb]
+
+        vq.extend(stage_steps([w0], 13, M, [slice(0, 4), slice(4, 13)], final0))
+
+        banksU = {}
+
+        def job(j):
+            kind = j[0]
+            if kind == "V":
+                pull(j[1])
+            elif kind == "strip":
+                gts[("s", j[1])] = strip_copy(j[1])
+            elif kind == "qs":
+                quant_g(STRIP0 + j[1] * STRIP, 2 * SUB, flat(gts[("s", j[1])]))
+            elif kind == "negS":
+                gns[j[1]] = neg_copy(j[1])
+            elif kind == "negV":
+                gn = ngp.tile([P, SUB, 4], BF16, align_bytes=64, tag="gn", name="gn")
+                nc.vector.tensor_scalar_mul(out=flat(gn), in0=gts[("s", j[1])][:, 0:SUB, :].rearrange("p c j -> p (c j)"), scalar1=-1.0)
+                gns[j[1]] = gn
+            elif kind == "qn":
+                quant_g(STRIP0 + j[1] * STRIP + 2 * SUB, SUB, flat(gns[j[1]]))
+            elif kind == "open":
+                banksU[j[1]] = [psa.tile([P, K], F32, tag="a", name="bank") for d in range(4)]
+            elif kind == "sp":
+                r, c, k = j[1], j[2], j[3]
+                n_w = 2 if FOLD3[r] else 1
+                for d in range(4):
+                    s = (((c & d) >> 1) ^ (c & d)) & 1
+                    mx(banksU[r][d], s, r, STRIP0 + c * STRIP + k * SUB, c == 0 and k == 0, c == 3 and k == n_w - 1)
+            elif kind == "w":
+                wU[j[1]] = sm.tile([P, 8 * NA, 16], F32, tag="w0", name="w")
+            elif kind == "ev":
+                r, d = j[1], j[2]
+                empty_bank(banksU[r][d][:], 2 * NA, wU[r][:, d * 2 * NA:(d + 1) * 2 * NA, :])
+            elif kind == "bank":
+                r, d = j[1], j[2]
+                bank = bank_passes(r, d)
+                empty_bank(bank[:], 2 * NA, wU[r][:, d * 2 * NA:(d + 1) * 2 * NA, :])
+            elif kind == "U":
+                pre, state0, halves, final = unit_steps(j[1], wU[j[1]])
+                vq.extend(pre)
+                vq.extend(stage_steps(state0, 8 * NA, 16, halves, final))
+            elif kind == "pf":
+                plain_front(j[1])
+            elif kind == "pb":
+                plain_back(j[1])
+            elif kind == "prep":
+                gts[j[1]] = prep_copy(j[1])
+            elif kind == "q":
+                quant_g(TBC + j[1] * K, K, flat(gts[j[1]]))
+            elif kind == "h3":
+                hmm(3, 1)
+            elif kind == "r3":
+                revac(3, 1)
+
+        for j in build_program():
+            job(j)
+        pull(1000)
+
+
+LOAD_ORDER = (0, 5, 1, 2, 3, 4, 6, 7)
+H_FIRST = 4
+G0_V = 2
+PLAIN_Q = True
+def build_program():
+    p = [("open", 0)]
+    for c in range(4):
+        p += [("strip", c), ("V", (4, 2, 2, 2)[c]), ("qs", c), ("sp", 0, c, 0)]
+        if c == 0:
+            p += [("h3",)]
+    p += [("prep", 0), ("r3",), ("w", 0)] + [("ev", 0, d) for d in range(4)] + [("U", 0)]
+    p += [("V", 2), ("q", 0)]
+    p += [("w", 1)] + [("bank", 1, d) for d in range(4)] + [("U", 1)]
+    p += [("pf", 1)]
+    for c in range(4):
+        p += [("negS", c)] + ([("pf", 1)] if c < 3 else []) + [("pb", 1)]
+    p += [("V", NV1)]
+    for c in range(4):
+        p += [("qn", c), ("V", 2)]
+    p += [("w", 2)]
+    for d in range(4):
+        p += [("bank", 2, d)]
+        if d == 0:
+            p += [("prep", 1)]
+        if d == 2:
+            p += [("prep", 2)]
+    p += [("U", 2), ("V", 2), ("q", 1), ("V", 5), ("q", 2)]
+    p += [("w", 3)]
+    for d in range(4):
+        p += [("bank", 3, d)]
+    p += [("U", 3)]
+    p += [("pf", 1)]
+    for i in range(7):
+        p += [("pf", 1), ("pb", 1)]
+    p += [("pb", 1)]
+    return p
+
+
+NV1 = 7

@@ -389,7 +389,7 @@ def tile_fullonlinehadamardhook_kernel(tc, x, had_K, grad_out, out):
         pull(1000)
 
 
-LOAD_ORDER = (0, 5, 1, 2, 3, 4, 6, 7)
+LOAD_ORDER = (0, 1, 2, 3, 4, 5, 6, 7)
 H_FIRST = 4
 G0_V = 2
 PLAIN_Q = True

@@ -43,9 +43,7 @@ def tile_fullonlinehadamardhook_kernel(tc, x, had_K, grad_out, out):
         wk = ctx.enter_context(tc.tile_pool(name="wk", bufs=4))
         sm = ctx.enter_context(tc.tile_pool(name="sm", bufs=3))
         zsp = ctx.enter_context(tc.tile_pool(name="zsp", bufs=3))
-        psa = ctx.enter_context(tc.psum_pool(name="psa", bufs=4))
-        psz = ctx.enter_context(tc.psum_pool(name="psz", bufs=2))
-        pso = ctx.enter_context(tc.psum_pool(name="pso", bufs=2))
+        psum = ctx.enter_context(tc.psum_pool(name="psum", bufs=1))
         ctx.enter_context(tc.manual_schedule())
 
         raw_h = keep.tile([P, 4, K], BF16)
@@ -69,6 +67,11 @@ def tile_fullonlinehadamardhook_kernel(tc, x, had_K, grad_out, out):
         g_codes = keep.tile([P, N_COLS], U32, align_bytes=64)
         g_scales = keep.tile([P, N_COLS], U8, align_bytes=64)
         res = keep.tile([P, T, K], F32)
+
+        def pbank(i):
+            return psum.tile([P, K], F32, tag="b%d" % i, name="bank%d" % i)
+
+        turn = {"z": 0, "o": 0}
 
         def quant_g(col0, width, tile_ap):
             cols = slice(col0, col0 + width)
@@ -143,7 +146,8 @@ def tile_fullonlinehadamardhook_kernel(tc, x, had_K, grad_out, out):
 
         def zpass(t, col0):
             cols = slice(col0, col0 + M)
-            zp = psz.tile([P, K], F32, name="zp")
+            zp = pbank(4 + turn["z"] % 2)
+            turn["z"] += 1
             nc.tensor.matmul_mx(
                 out=zp[:],
                 lhsT=g_codes[:, cols].bitcast(E5X4), lhsT_scale=g_scales[:, cols],
@@ -158,7 +162,8 @@ def tile_fullonlinehadamardhook_kernel(tc, x, had_K, grad_out, out):
             zss[t] = zs
 
         def hmm(t, r0):
-            op = pso.tile([P, K], F32, name="op")
+            op = pbank(6 + turn["o"] % 2)
+            turn["o"] += 1
             for r in range(r0, 4):
                 rc = slice(r * P, (r + 1) * P)
                 nc.tensor.matmul(out=op[:, rc], lhsT=zss[t][:, rc], rhs=hmat[:], start=True, stop=True)
@@ -198,7 +203,7 @@ def tile_fullonlinehadamardhook_kernel(tc, x, had_K, grad_out, out):
             return ws
 
         def bank_passes(r, d):
-            bank = psa.tile([P, K], F32, tag="a", name="bank")
+            bank = pbank(d)
             ws = windows(r, d)
             for i, (c, s, col) in enumerate(ws):
                 mx(bank, s, r, col, i == 0, i == len(ws) - 1)
@@ -305,7 +310,7 @@ def tile_fullonlinehadamardhook_kernel(tc, x, had_K, grad_out, out):
         quant_g(0, K, flat(gt0))
         banks0 = []
         for r in range(4):
-            bank = psa.tile([P, K], F32, tag="a", name="bank")
+            bank = pbank(r)
             mx(bank, 0, r, 0, True, True)
             banks0.append(bank)
         zpass(3, 3 * M)
@@ -351,7 +356,7 @@ def tile_fullonlinehadamardhook_kernel(tc, x, had_K, grad_out, out):
             elif kind == "qn":
                 quant_g(STRIP0 + j[1] * STRIP + 2 * SUB, SUB, flat(gns[j[1]]))
             elif kind == "open":
-                banksU[j[1]] = [psa.tile([P, K], F32, tag="a", name="bank") for d in range(4)]
+                banksU[j[1]] = [pbank(4 * (j[1] % 2) + d) for d in range(4)]
             elif kind == "sp":
                 r, c, k = j[1], j[2], j[3]
                 n_w = 2 if FOLD3[r] else 1
@@ -394,28 +399,24 @@ H_FIRST = 4
 G0_V = 2
 PLAIN_Q = True
 def build_program():
-    p = [("open", 0)]
+    p = [("h3",), ("open", 0)]
     for c in range(4):
-        p += [("strip", c), ("V", (4, 2, 2, 2)[c]), ("qs", c), ("sp", 0, c, 0)]
+        p += [("strip", c)]
         if c == 0:
-            p += [("h3",)]
-    p += [("prep", 0), ("r3",), ("w", 0)] + [("ev", 0, d) for d in range(4)] + [("U", 0)]
+            p += [("r3",), ("open", 1)]
+        p += [("V", (4, 2, 2, 2)[c]), ("qs", c), ("sp", 0, c, 0), ("sp", 1, c, 0)]
+    p += [("prep", 0), ("w", 0)] + [("ev", 0, d) for d in range(4)] + [("U", 0)]
     p += [("V", 2), ("q", 0)]
-    p += [("w", 1)] + [("bank", 1, d) for d in range(4)] + [("U", 1)]
+    p += [("w", 1)] + [("ev", 1, d) for d in range(4)] + [("U", 1)]
+    p += [("open", 2)] + [("sp", 2, c, 0) for c in range(4)]
     p += [("pf", 1)]
     for c in range(4):
         p += [("negS", c)] + ([("pf", 1)] if c < 3 else []) + [("pb", 1)]
     p += [("V", NV1)]
     for c in range(4):
-        p += [("qn", c), ("V", 2)]
-    p += [("w", 2)]
-    for d in range(4):
-        p += [("bank", 2, d)]
-        if d == 0:
-            p += [("prep", 1)]
-        if d == 2:
-            p += [("prep", 2)]
-    p += [("U", 2), ("V", 2), ("q", 1), ("V", 5), ("q", 2)]
+        p += [("qn", c), ("sp", 2, c, 1), ("V", 2)]
+    p += [("prep", 1), ("w", 2)] + [("ev", 2, d) for d in range(4)] + [("U", 2)]
+    p += [("prep", 2), ("V", 2), ("q", 1), ("V", 5), ("q", 2)]
     p += [("w", 3)]
     for d in range(4):
         p += [("bank", 3, d)]
@@ -427,4 +428,4 @@ def build_program():
     return p
 
 
-NV1 = 7
+NV1 = 8

@@ -26,7 +26,8 @@ TA0 = N0
 TB0 = N0 + NA
 SUB = 256
 STRIP = 3 * SUB
-STRIP0 = K
+W0N = 3 * SUB
+STRIP0 = W0N + M
 TBC = STRIP0 + 4 * STRIP
 N_COLS = TBC + NB * M
 FOLD3 = (False, False, True, True)
@@ -226,8 +227,8 @@ def tile_fullonlinehadamardhook_kernel(tc, x, had_K, grad_out, out):
                 pre = [lstage(slice(0, 2), True), lstage(slice(2, 4), False)]
 
             def final(state):
-                n_cut = 4 if r == LAST_UNIT else 2
-                step = NA // n_cut
+                bounds = (0, 4, 8, 12, 14, 16)
+                n_cut = len(bounds) - 1
                 fs = []
                 def half(i):
                     def f():
@@ -245,10 +246,10 @@ def tile_fullonlinehadamardhook_kernel(tc, x, had_K, grad_out, out):
                     def f():
                         resa = res[:, TA0:TA0 + NA, rcols].rearrange("p t (d h q) -> p d t h q", d=8, h=2)
                         xv = state[-1][:].rearrange("p (d t) (q two) -> p d t q two", d=8, two=2)
-                        ts = slice(i * step, (i + 1) * step)
+                        ts = slice(bounds[i], bounds[i + 1])
                         butterfly(resa[:, :, ts, 0, :], resa[:, :, ts, 1, :], xv[:, :, ts, :, 0], xv[:, :, ts, :, 1])
                         if r == LAST_UNIT:
-                            nc.sync.dma_start(out=o_view[:, TA0 + i * step:TA0 + (i + 1) * step, rcols], in_=res[:, TA0 + i * step:TA0 + (i + 1) * step, rcols])
+                            nc.sync.dma_start(out=o_view[:, TA0 + bounds[i]:TA0 + bounds[i + 1], rcols], in_=res[:, TA0 + bounds[i]:TA0 + bounds[i + 1], rcols])
                         elif i == n_cut - 1:
                             nc.sync.dma_start(out=o_view[:, TA0:TA0 + NA, rcols], in_=res[:, TA0:TA0 + NA, rcols])
                     return f
@@ -301,23 +302,29 @@ def tile_fullonlinehadamardhook_kernel(tc, x, had_K, grad_out, out):
         h_next(H_FIRST)
         nc.vector.tensor_copy(out=hg[0][:].rearrange("p (r q) j -> p r q j", r=4), in_=h_src)
         gt0 = grp.tile([P, K, 4], BF16, align_bytes=64, tag="g", name="gt")
-        g0dst = gt0[:].rearrange("p (x y) j -> p x y j", x=4)
-        g0src = token_major(0)
-        nc.scalar.copy(out=g0dst[:, G0_V:4], in_=g0src[:, G0_V:4])
-        nc.vector.tensor_copy(out=g0dst[:, 0:G0_V], in_=g0src[:, 0:G0_V])
+        g0dst = gt0[:].rearrange("p (l t e) j -> p l t e j", l=2, t=N0)
+        g0src = raw_g[:, 0:N0, :].rearrange("p t (j l e) -> p l t e j", j=4, l=2)
+        nc.scalar.copy(out=g0dst[:, 1], in_=g0src[:, 0])
+        nc.vector.tensor_copy(out=g0dst[:, 0], in_=g0src[:, 1])
+        gt3 = ngp.tile([P, M, 4], BF16, align_bytes=64, tag="gn", name="gt3")
+        nc.scalar.copy(out=gt3[:], in_=raw_g[:, 3, :].rearrange("p (j a) -> p a j", j=4))
         quant_h(0)
-        nc.vector.tensor_scalar_mul(out=flat(hg[1]), in0=flat(hg[0]), scalar1=-1.0)
+        gn0 = ngp.tile([P, SUB, 4], BF16, align_bytes=64, tag="gn", name="gn0")
+        nc.vector.tensor_scalar_mul(out=flat(gn0), in0=gt0[:, 0:SUB, :].rearrange("p c j -> p (c j)"), scalar1=-1.0)
         quant_g(0, K, flat(gt0))
-        banks0 = []
+        banks0 = [pbank(r) for r in range(4)]
+        quant_g(K, SUB, flat(gn0))
+        quant_g(W0N, M, flat(gt3))
         for r in range(4):
-            bank = pbank(r)
-            mx(bank, 0, r, 0, True, True)
-            banks0.append(bank)
-        zpass(3, 3 * M)
-        w0 = sm.tile([P, 13, M], F32, tag="w0", name="w0")
-        empty_bank(banks0[0][:], 4, w0[:, 0:4, :])
+            mx(banks0[r], 0, r, 0, True, False)
+            mx(banks0[r], 0, r, SUB, False, True)
+        zpass(3, W0N)
+        nc.vector.tensor_scalar_mul(out=flat(hg[1]), in0=flat(hg[0]), scalar1=-1.0)
+        w0 = sm.tile([P, 26, M // 2], F32, tag="w0", name="w0")
+        empty_bank(banks0[0][:], 8, w0[:, 0:8, :])
         for r in range(1, 4):
-            empty_bank(banks0[r][:, 0:3 * M], 3, w0[:, 1 + 3 * r:4 + 3 * r, :])
+            for l in range(2):
+                empty_bank(banks0[r][:, l * SUB:l * SUB + 3 * M // 2], 3, w0[:, 2 + 6 * r + 3 * l:5 + 6 * r + 3 * l, :])
         zcopy(3, 1)
         h_next()
         quant_h(1)
@@ -325,17 +332,17 @@ def tile_fullonlinehadamardhook_kernel(tc, x, had_K, grad_out, out):
 
         def final0(state):
             def fa():
-                res0 = res[:, 0:N0, :].rearrange("p t (r h q) -> p r t h q", r=4, h=2)
-                xa = state[-1][:, 0:4, :].rearrange("p g (q two) -> p g q two", two=2)
-                butterfly(res0[:, 0, :, 0, :], res0[:, 0, :, 1, :], xa[:, :, :, 0], xa[:, :, :, 1])
+                ya = res[:, 0:N0, 0:M].rearrange("p t (m h q) -> p m t h q", m=2, h=2)
+                xa = state[-1][:, 0:8, :].rearrange("p (m t) (q two) -> p m t q two", m=2, two=2)
+                butterfly(ya[:, :, :, 0, :], ya[:, :, :, 1, :], xa[:, :, :, :, 0], xa[:, :, :, :, 1])
             def fb():
-                res0 = res[:, 0:N0, :].rearrange("p t (r h q) -> p r t h q", r=4, h=2)
-                xb = state[-1][:, 4:13, :].rearrange("p (r g) (q two) -> p r g q two", r=3, two=2)
-                butterfly(res0[:, 1:4, 0:3, 0, :], res0[:, 1:4, 0:3, 1, :], xb[:, :, :, :, 0], xb[:, :, :, :, 1])
+                yb = res[:, 0:3, M:K].rearrange("p t (m h q) -> p m t h q", m=6, h=2)
+                xb = state[-1][:, 8:26, :].rearrange("p (m t) (q two) -> p m t q two", m=6, two=2)
+                butterfly(yb[:, :, :, 0, :], yb[:, :, :, 1, :], xb[:, :, :, :, 0], xb[:, :, :, :, 1])
                 store_tokens(0, N0)
             return [fa, fb]
 
-        vq.extend(stage_steps([w0], 13, M, [slice(0, 4), slice(4, 13)], final0))
+        vq.extend(stage_steps([w0], 26, M // 2, [slice(0, 8), slice(8, 26)], final0))
 
         banksU = {}
 
@@ -411,7 +418,7 @@ def build_program():
     p += [("open", 2)] + [("sp", 2, c, 0) for c in range(4)]
     p += [("pf", 1)]
     for c in range(4):
-        p += [("negS", c)] + ([("pf", 1)] if c < 3 else []) + [("pb", 1)]
+        p += ([("pf", 1)] if c < 3 else []) + [("negS", c), ("pb", 1)]
     p += [("V", NV1)]
     for c in range(4):
         p += [("qn", c), ("sp", 2, c, 1), ("V", 2)]

@@ -1,12 +1,12 @@
 from contextlib import ExitStack
 
 import concourse.mybir as mybir
-from concourse.masks import make_identity
 
 F32 = mybir.dt.float32
 BF16 = mybir.dt.bfloat16
 U32 = mybir.dt.uint32
 U8 = mybir.dt.uint8
+I32 = mybir.dt.int32
 E4X4 = mybir.dt.float8_e4m3fn_x4
 E5X4 = mybir.dt.float8_e5m2_x4
 ALU = mybir.AluOpType
@@ -53,17 +53,27 @@ def tile_fullonlinehadamardhook_kernel(tc, x, had_K, grad_out, out):
         for c in LOAD_ORDER:
             nc.sync.dma_start(out=raw_g[:, c * 4:(c + 1) * 4, :], in_=g_view[:, c * 4:(c + 1) * 4, :])
 
-        hts = [keep.tile([P, P], F32, name="hst%d" % k) for k in range(8)]
-        make_identity(nc, hts[0][:])
-
-        def h_stage(k):
-            h = 1 << k
-            xv = hts[k][:].rearrange("p (m two h) -> p m two h", two=2, h=h)
-            yv = hts[k + 1][:].rearrange("p (m two h) -> p m two h", two=2, h=h)
-            nc.vector.tensor_tensor(out=yv[:, :, 0, :], in0=xv[:, :, 0, :], in1=xv[:, :, 1, :], op=ALU.add)
-            nc.vector.tensor_tensor(out=yv[:, :, 1, :], in0=xv[:, :, 0, :], in1=xv[:, :, 1, :], op=ALU.subtract)
-
-        hmat = hts[7]
+        pidx = keep.tile([P, 7], I32, name="pidx")
+        kidx = keep.tile([P, 7], I32, name="kidx")
+        nc.gpsimd.iota(pidx[:], pattern=[[0, 7]], base=0, channel_multiplier=1)
+        nc.gpsimd.iota(kidx[:], pattern=[[1, 7]], base=0, channel_multiplier=0)
+        shifted = keep.tile([P, 7], I32, name="shifted")
+        nc.vector.tensor_tensor(out=shifted[:], in0=pidx[:], in1=kidx[:], op=ALU.logical_shift_right)
+        pbit = keep.tile([P, 7], I32, name="pbit")
+        nc.vector.tensor_single_scalar(out=pbit[:], in_=shifted[:], scalar=1, op=ALU.bitwise_and)
+        sgn = keep.tile([P, 7], F32, name="sgn")
+        nc.vector.tensor_scalar(out=sgn[:], in0=pbit[:], scalar1=-2.0, scalar2=1.0, op0=ALU.mult, op1=ALU.add)
+        hmat = keep.tile([P, P], F32, name="hmat")
+        nc.vector.memset(hmat[:, 0:1], 1.0)
+        for k in range(7):
+            nc.scalar.activation(out=hmat[:, (1 << k):(2 << k)], in_=hmat[:, 0:(1 << k)], func=mybir.ActivationFunctionType.Copy, scale=sgn[:, k:k + 1])
+        ones = keep.tile([P, K], BF16, align_bytes=64, name="ones")
+        nc.vector.memset(ones[:], 1.0)
+        one_codes = keep.tile([P, K + M], U32, align_bytes=64, name="one_codes")
+        one_scales = keep.tile([P, K + M], U8, align_bytes=64, name="one_scales")
+        for i in range(4):
+            nc.vector.quantize_mx(out=one_codes[:, i * M:(i + 1) * M].bitcast(E5X4), scales=one_scales[:, i * M:(i + 1) * M], in_=ones[:])
+        nc.vector.quantize_mx(out=one_codes[:, K:K + M].bitcast(E4X4), scales=one_scales[:, K:K + M], in_=ones[:])
 
         g_codes = keep.tile([P, N_COLS], U32, align_bytes=64)
         g_scales = keep.tile([P, N_COLS], U8, align_bytes=64)
@@ -259,14 +269,6 @@ def tile_fullonlinehadamardhook_kernel(tc, x, had_K, grad_out, out):
 
         LAST_UNIT = 3
 
-        hk = [0]
-
-        def h_next(n=1):
-            for i in range(n):
-                if hk[0] < 7:
-                    h_stage(hk[0])
-                    hk[0] += 1
-
         vq = []
         vpos = [0]
 
@@ -299,7 +301,14 @@ def tile_fullonlinehadamardhook_kernel(tc, x, had_K, grad_out, out):
         def flat(t):
             return t[:].rearrange("p c j -> p (c j)")
 
-        h_next(H_FIRST)
+        spare = pbank(7)
+        for i in range(N_WARM):
+            nc.tensor.matmul_mx(
+                out=spare[:],
+                lhsT=one_codes[:, K:K + M].bitcast(E4X4), lhsT_scale=one_scales[:, K:K + M],
+                rhs=one_codes[:, 0:K].bitcast(E5X4), rhs_scale=one_scales[:, 0:K],
+                start=True, stop=True,
+            )
         nc.vector.tensor_copy(out=hg[0][:].rearrange("p (r q) j -> p r q j", r=4), in_=h_src)
         gt0 = grp.tile([P, K, 4], BF16, align_bytes=64, tag="g", name="gt")
         g0dst = gt0[:].rearrange("p (l t e) j -> p l t e j", l=2, t=N0)
@@ -326,9 +335,7 @@ def tile_fullonlinehadamardhook_kernel(tc, x, had_K, grad_out, out):
             for l in range(2):
                 empty_bank(banks0[r][:, l * SUB:l * SUB + 3 * M // 2], 3, w0[:, 2 + 6 * r + 3 * l:5 + 6 * r + 3 * l, :])
         zcopy(3, 1)
-        h_next()
         quant_h(1)
-        h_next(7)
 
         def final0(state):
             def fa():
@@ -402,7 +409,6 @@ def tile_fullonlinehadamardhook_kernel(tc, x, had_K, grad_out, out):
 
 
 LOAD_ORDER = (0, 1, 2, 3, 4, 5, 6, 7)
-H_FIRST = 4
 G0_V = 2
 PLAIN_Q = True
 def build_program():
@@ -436,3 +442,4 @@ def build_program():
 
 
 NV1 = 8
+N_WARM = 8

@@ -193,10 +193,13 @@ def tile_fullonlinehadamardhook_kernel(tc, x, had_K, grad_out, out):
 
         subs = raw_g[:, TA0:TA0 + NA, :].rearrange("p t (j c l e) -> p c l t e j", j=4, c=4, l=2)
 
+        def strip_part(gt, c, t0, t1):
+            for pos in range(2):
+                nc.scalar.copy(out=gt[:, pos * SUB:(pos + 1) * SUB, :].rearrange("p (t e) j -> p t e j", t=NA)[:, t0:t1], in_=subs[:, c, 1 - pos, t0:t1])
+
         def strip_copy(c):
             gt = grp.tile([P, K, 4], BF16, align_bytes=64, tag="g", name="gt")
-            for pos in range(2):
-                nc.scalar.copy(out=gt[:, pos * SUB:(pos + 1) * SUB, :].rearrange("p (t e) j -> p t e j", t=NA), in_=subs[:, c, 1 - pos])
+            strip_part(gt, c, 0, NA)
             return gt
 
         def neg_copy(c):
@@ -317,6 +320,8 @@ def tile_fullonlinehadamardhook_kernel(tc, x, had_K, grad_out, out):
         nc.vector.tensor_copy(out=g0dst[:, 0], in_=g0src[:, 1])
         gt3 = ngp.tile([P, M, 4], BF16, align_bytes=64, tag="gn", name="gt3")
         nc.scalar.copy(out=gt3[:], in_=raw_g[:, 3, :].rearrange("p (j a) -> p a j", j=4))
+        gts[("s", 0)] = grp.tile([P, K, 4], BF16, align_bytes=64, tag="g", name="gt")
+        strip_part(gts[("s", 0)], 0, 0, NA // 2)
         quant_h(0)
         gn0 = ngp.tile([P, SUB, 4], BF16, align_bytes=64, tag="gn", name="gn0")
         nc.vector.tensor_scalar_mul(out=flat(gn0), in0=gt0[:, 0:SUB, :].rearrange("p c j -> p (c j)"), scalar1=-1.0)
@@ -329,27 +334,36 @@ def tile_fullonlinehadamardhook_kernel(tc, x, had_K, grad_out, out):
             mx(banks0[r], 0, r, SUB, False, True)
         zpass(3, W0N)
         nc.vector.tensor_scalar_mul(out=flat(hg[1]), in0=flat(hg[0]), scalar1=-1.0)
-        w0 = sm.tile([P, 26, M // 2], F32, tag="w0", name="w0")
-        empty_bank(banks0[0][:], 8, w0[:, 0:8, :])
+        w0a = sm.tile([P, 8, M // 2], F32, tag="w0", name="w0a")
+        w0b = sm.tile([P, 18, M // 2], F32, tag="w0", name="w0b")
+        empty_bank(banks0[0][:], 8, w0a[:])
         for r in range(1, 4):
             for l in range(2):
-                empty_bank(banks0[r][:, l * SUB:l * SUB + 3 * M // 2], 3, w0[:, 2 + 6 * r + 3 * l:5 + 6 * r + 3 * l, :])
+                empty_bank(banks0[r][:, l * SUB:l * SUB + 3 * M // 2], 3, w0b[:, 6 * r + 3 * l - 6:6 * r + 3 * l - 3, :])
         zcopy(3, 1)
         quant_h(1)
 
-        def final0(state):
+        def final_a(state):
             def fa():
                 ya = res[:, 0:N0, 0:M].rearrange("p t (m h q) -> p m t h q", m=2, h=2)
                 xa = state[-1][:, 0:8, :].rearrange("p (m t) (q two) -> p m t q two", m=2, two=2)
                 butterfly(ya[:, :, :, 0, :], ya[:, :, :, 1, :], xa[:, :, :, :, 0], xa[:, :, :, :, 1])
+            return [fa]
+
+        def final_b(state):
             def fb():
                 yb = res[:, 0:3, M:K].rearrange("p t (m h q) -> p m t h q", m=6, h=2)
-                xb = state[-1][:, 8:26, :].rearrange("p (m t) (q two) -> p m t q two", m=6, two=2)
+                xb = state[-1][:].rearrange("p (m t) (q two) -> p m t q two", m=6, two=2)
                 butterfly(yb[:, :, :, 0, :], yb[:, :, :, 1, :], xb[:, :, :, :, 0], xb[:, :, :, :, 1])
                 store_tokens(0, N0)
-            return [fa, fb]
+            return [fb]
 
-        vq.extend(stage_steps([w0], 26, M // 2, [slice(0, 8), slice(8, 26)], final0))
+        steps_a = stage_steps([w0a], 8, M // 2, [slice(0, 8)], final_a)
+        steps_b = stage_steps([w0b], 18, M // 2, [slice(0, 18)], final_b)
+        vq.append(steps_a[0])
+        for i in range(5):
+            vq.extend([steps_a[i + 1], steps_b[i]])
+        vq.append(steps_b[5])
 
         banksU = {}
 
@@ -358,7 +372,10 @@ def tile_fullonlinehadamardhook_kernel(tc, x, had_K, grad_out, out):
             if kind == "V":
                 pull(j[1])
             elif kind == "strip":
-                gts[("s", j[1])] = strip_copy(j[1])
+                if j[1] == 0:
+                    strip_part(gts[("s", 0)], 0, NA // 2, NA)
+                else:
+                    gts[("s", j[1])] = strip_copy(j[1])
             elif kind == "qs":
                 quant_g(STRIP0 + j[1] * STRIP, 2 * SUB, flat(gts[("s", j[1])]))
             elif kind == "negS":
@@ -417,7 +434,7 @@ def build_program():
         p += [("strip", c)]
         if c == 0:
             p += [("r3",), ("open", 1)]
-        p += [("V", (4, 2, 2, 2)[c]), ("qs", c), ("sp", 0, c, 0), ("sp", 1, c, 0)]
+        p += [("V", (4, 2, 2, 1)[c]), ("qs", c), ("sp", 0, c, 0), ("sp", 1, c, 0)]
     p += [("prep", 0), ("w", 0)] + [("ev", 0, d) for d in range(4)] + [("U", 0)]
     p += [("V", 2), ("q", 0)]
     p += [("w", 1)] + [("ev", 1, d) for d in range(4)] + [("U", 1)]

@@ -195,7 +195,8 @@ def tile_fullonlinehadamardhook_kernel(tc, x, had_K, grad_out, out):
 
         def strip_part(gt, c, t0, t1):
             for pos in range(2):
-                nc.scalar.copy(out=gt[:, pos * SUB:(pos + 1) * SUB, :].rearrange("p (t e) j -> p t e j", t=NA)[:, t0:t1], in_=subs[:, c, 1 - pos, t0:t1])
+                eng = nc.vector.tensor_copy if (pos == 1 and c in V_STRIPS) else nc.scalar.copy
+                eng(out=gt[:, pos * SUB:(pos + 1) * SUB, :].rearrange("p (t e) j -> p t e j", t=NA)[:, t0:t1], in_=subs[:, c, 1 - pos, t0:t1])
 
         def strip_copy(c):
             gt = grp.tile([P, K, 4], BF16, align_bytes=64, tag="g", name="gt")
@@ -460,3 +461,4 @@ def build_program():
 
 NV1 = 8
 N_WARM = 8
+V_STRIPS = (1,)

@@ -96,8 +96,11 @@ def tile_fullonlinehadamardhook_kernel(tc, x, had_K, grad_out, out):
         def quant_h(s):
             nc.vector.quantize_mx(out=h_codes[s][:].bitcast(E4X4), scales=h_scales[s][:], in_=hg[s][:].rearrange("p c j -> p (c j)"))
 
-        def token_major(t0):
-            return raw_g[:, t0:t0 + 4, :].rearrange("p t (j a) -> p t a j", j=4)
+        def by_fours(copy, dst, src, tokens):
+            copy(out=dst.rearrange("p (t x i) j -> p t x j i", t=tokens, i=4), in_=src)
+
+        def token_runs(t0, n):
+            return raw_g[:, t0:t0 + n, :].rearrange("p t (j x i) -> p t x j i", j=4, i=4)
 
         def butterfly(out_u, out_v, in_even, in_odd):
             nc.vector.tensor_tensor(out=out_u, in0=in_even, in1=in_odd, op=ALU.add)
@@ -188,15 +191,17 @@ def tile_fullonlinehadamardhook_kernel(tc, x, had_K, grad_out, out):
 
         def prep_copy(k):
             gt = grp.tile([P, K, 4], BF16, align_bytes=64, tag="g", name="gt")
-            nc.scalar.copy(out=gt[:].rearrange("p (x y) j -> p x y j", x=4), in_=token_major(TB0 + 4 * k))
+            by_fours(nc.scalar.copy, gt[:], token_runs(TB0 + 4 * k, 4), 4)
             return gt
 
         subs = raw_g[:, TA0:TA0 + NA, :].rearrange("p t (j c l e) -> p c l t e j", j=4, c=4, l=2)
+        sub_runs = raw_g[:, TA0:TA0 + NA, :].rearrange("p t (j c l x i) -> p c l t x j i", j=4, c=4, l=2, i=4)
 
         def strip_part(gt, c, t0, t1):
             for pos in range(2):
                 eng = nc.vector.tensor_copy if (pos == 1 and c in V_STRIPS) else nc.scalar.copy
-                eng(out=gt[:, pos * SUB:(pos + 1) * SUB, :].rearrange("p (t e) j -> p t e j", t=NA)[:, t0:t1], in_=subs[:, c, 1 - pos, t0:t1])
+                e = SUB // NA
+                by_fours(eng, gt[:, pos * SUB + t0 * e:pos * SUB + t1 * e, :], sub_runs[:, c, 1 - pos, t0:t1], t1 - t0)
 
         def strip_copy(c):
             gt = grp.tile([P, K, 4], BF16, align_bytes=64, tag="g", name="gt")
@@ -315,12 +320,11 @@ def tile_fullonlinehadamardhook_kernel(tc, x, had_K, grad_out, out):
             )
         nc.vector.tensor_copy(out=hg[0][:].rearrange("p (r q) j -> p r q j", r=4), in_=h_src)
         gt0 = grp.tile([P, K, 4], BF16, align_bytes=64, tag="g", name="gt")
-        g0dst = gt0[:].rearrange("p (l t e) j -> p l t e j", l=2, t=N0)
-        g0src = raw_g[:, 0:N0, :].rearrange("p t (j l e) -> p l t e j", j=4, l=2)
-        nc.scalar.copy(out=g0dst[:, 1], in_=g0src[:, 0])
-        nc.vector.tensor_copy(out=g0dst[:, 0], in_=g0src[:, 1])
+        g0src = raw_g[:, 0:N0, :].rearrange("p t (j l x i) -> p l t x j i", j=4, l=2, i=4)
+        by_fours(nc.scalar.copy, gt0[:, SUB:2 * SUB, :], g0src[:, 0], N0)
+        by_fours(nc.vector.tensor_copy, gt0[:, 0:SUB, :], g0src[:, 1], N0)
         gt3 = ngp.tile([P, M, 4], BF16, align_bytes=64, tag="gn", name="gt3")
-        nc.scalar.copy(out=gt3[:], in_=raw_g[:, 3, :].rearrange("p (j a) -> p a j", j=4))
+        by_fours(nc.scalar.copy, gt3[:], token_runs(3, 1), 1)
         gts[("s", 0)] = grp.tile([P, K, 4], BF16, align_bytes=64, tag="g", name="gt")
         strip_part(gts[("s", 0)], 0, 0, NA // 2)
         quant_h(0)

@@ -25,12 +25,14 @@ NB = 12
 TA0 = N0
 TB0 = N0 + NA
 SUB = 256
-STRIP = 3 * SUB
+HALF = 5 * SUB
 W0N = 3 * SUB
 STRIP0 = W0N + M
-TBC = STRIP0 + 4 * STRIP
+TBC = STRIP0 + 2 * HALF
 N_COLS = TBC + NB * M
-FOLD3 = (False, False, True, True)
+CYCLES = ((0, 1, 4, 7), (2, 3, 6, 5))
+BANKS = ((0, 1), (2, 7), (3, 6), (5, 4))
+NEGATIVE = 7
 
 
 def tile_fullonlinehadamardhook_kernel(tc, x, had_K, grad_out, out):
@@ -40,9 +42,9 @@ def tile_fullonlinehadamardhook_kernel(tc, x, had_K, grad_out, out):
     with ExitStack() as ctx:
         keep = ctx.enter_context(tc.tile_pool(name="keep", bufs=1))
         grp = ctx.enter_context(tc.tile_pool(name="grp", bufs=3))
-        ngp = ctx.enter_context(tc.tile_pool(name="ngp", bufs=4))
-        wk = ctx.enter_context(tc.tile_pool(name="wk", bufs=4))
-        sm = ctx.enter_context(tc.tile_pool(name="sm", bufs=3))
+        ngp = ctx.enter_context(tc.tile_pool(name="ngp", bufs=2))
+        wk = ctx.enter_context(tc.tile_pool(name="wk", bufs=3))
+        sm = ctx.enter_context(tc.tile_pool(name="sm", bufs=2))
         zsp = ctx.enter_context(tc.tile_pool(name="zsp", bufs=3))
         psum = ctx.enter_context(tc.psum_pool(name="psum", bufs=1))
         ctx.enter_context(tc.manual_schedule())
@@ -106,11 +108,11 @@ def tile_fullonlinehadamardhook_kernel(tc, x, had_K, grad_out, out):
             nc.vector.tensor_tensor(out=out_u, in0=in_even, in1=in_odd, op=ALU.add)
             nc.vector.tensor_tensor(out=out_v, in0=in_even, in1=in_odd, op=ALU.subtract)
 
-        def empty_bank(bank_view, gb, w_rows):
+        def empty_bank(bank_view, gb, w_rows, scale=SCALE):
             nc.scalar.mul(
                 out=w_rows.rearrange("p g (x y) -> p g x y", y=4),
                 in_=bank_view.rearrange("p (g y x) -> p g x y", g=gb, y=4),
-                mul=SCALE,
+                mul=scale,
             )
 
         def mx(bank, s, r, col, start, stop):
@@ -128,7 +130,7 @@ def tile_fullonlinehadamardhook_kernel(tc, x, had_K, grad_out, out):
             def mid(run, gs, new):
                 def f():
                     if new:
-                        state.append(wk.tile([P, groups, length], F32, tag="w", name="wn"))
+                        state.append(wk.tile([P, groups, length], F32, tag="w%d" % groups, name="wn", bufs=WK_BUFS[groups]))
                     w, wn = state[-2], state[-1]
                     xv = w[:, gs, :].rearrange("p g (m two h) -> p g m two h", two=2, h=run)
                     yv = wn[:, gs, :].rearrange("p g (m two h) -> p g m two h", two=2, h=run)
@@ -138,7 +140,7 @@ def tile_fullonlinehadamardhook_kernel(tc, x, had_K, grad_out, out):
             def shuf(gs, new):
                 def f():
                     if new:
-                        state.append(wk.tile([P, groups, length], F32, tag="w", name="wn"))
+                        state.append(wk.tile([P, groups, length], F32, tag="w%d" % groups, name="wn", bufs=WK_BUFS[groups]))
                     w, wn = state[-2], state[-1]
                     xv = w[:, gs, :].rearrange("p g (q two) -> p g q two", two=2)
                     yv = wn[:, gs, :].rearrange("p g (h q) -> p g h q", h=2)
@@ -194,87 +196,62 @@ def tile_fullonlinehadamardhook_kernel(tc, x, had_K, grad_out, out):
             by_fours(nc.scalar.copy, gt[:], token_runs(TB0 + 4 * k, 4), 4)
             return gt
 
-        subs = raw_g[:, TA0:TA0 + NA, :].rearrange("p t (j c l e) -> p c l t e j", j=4, c=4, l=2)
-        sub_runs = raw_g[:, TA0:TA0 + NA, :].rearrange("p t (j c l x i) -> p c l t x j i", j=4, c=4, l=2, i=4)
+        sub_runs = raw_g[:, TA0:TA0 + NA, :].rearrange("p t (j u x i) -> p u t x j i", j=4, u=8, i=4)
+        slab_tiles = {}
 
-        def strip_part(gt, c, t0, t1):
-            for pos in range(2):
-                eng = nc.vector.tensor_copy if (pos == 1 and c in V_STRIPS) else nc.scalar.copy
-                e = SUB // NA
-                by_fours(eng, gt[:, pos * SUB + t0 * e:pos * SUB + t1 * e, :], sub_runs[:, c, 1 - pos, t0:t1], t1 - t0)
+        def slab_copy(k, pos, t0, t1):
+            if k not in slab_tiles:
+                slab_tiles[k] = grp.tile([P, K, 4], BF16, align_bytes=64, tag="g", name="gt")
+            u = CYCLES[k // 2][2 * (k % 2) + pos]
+            eng = nc.vector.tensor_copy if (k, pos) in V_SLABS else nc.scalar.copy
+            e = SUB // NA
+            by_fours(eng, slab_tiles[k][:, pos * SUB + t0 * e:pos * SUB + t1 * e, :], sub_runs[:, u, t0:t1], t1 - t0)
 
-        def strip_copy(c):
-            gt = grp.tile([P, K, 4], BF16, align_bytes=64, tag="g", name="gt")
-            strip_part(gt, c, 0, NA)
-            return gt
+        def parity(v):
+            return (v ^ (v >> 1) ^ (v >> 2)) & 1
 
-        def neg_copy(c):
-            gn = ngp.tile([P, SUB, 4], BF16, align_bytes=64, tag="gn", name="gn")
-            nc.scalar.mul(out=gn[:].rearrange("p (t e) j -> p t e j", t=NA), in_=subs[:, c, 1], mul=-1.0)
-            return gn
+        def unit_pass(bank, r, d, cyc, i):
+            left = BANKS[d][0]
+            if d == 0 and i % 2 == 1:
+                return
+            mx(bank, parity(left & CYCLES[cyc][i]), r, STRIP0 + cyc * HALF + i * SUB,
+               (cyc, i) == (0, 0), (cyc, i) == (1, 2 if d == 0 else 3))
 
-        def windows(r, d):
-            ws = []
-            for c in range(4):
-                s = (((c & d) >> 1) ^ (c & d)) & 1
-                ws.append((c, s, STRIP0 + c * STRIP))
-                if FOLD3[r]:
-                    ws.append((c, s, STRIP0 + c * STRIP + SUB))
-            return ws
-
-        def bank_passes(r, d):
-            bank = pbank(d)
-            ws = windows(r, d)
-            for i, (c, s, col) in enumerate(ws):
-                mx(bank, s, r, col, i == 0, i == len(ws) - 1)
-            return bank
-
-        def unit_steps(r, w):
+        def unit_steps(r, w, pq):
             rcols = slice(r * M, (r + 1) * M)
             halves = [slice(0, 4 * NA), slice(4 * NA, 8 * NA)]
-            pre = []
-            state0 = [w]
-            if not FOLD3[r]:
-                def lstage(ds, new):
-                    def f():
-                        if new:
-                            state0.append(wk.tile([P, 8 * NA, 16], F32, tag="w", name="wn"))
-                        xv = state0[0][:].rearrange("p (d l g) x -> p d l (g x)", d=4, l=2)
-                        yv = state0[1][:].rearrange("p (d l g) x -> p d l (g x)", d=4, l=2)
-                        butterfly(yv[:, ds, 0, :], yv[:, ds, 1, :], xv[:, ds, 1, :], xv[:, ds, 0, :])
-                    return f
-                pre = [lstage(slice(0, 2), True), lstage(slice(2, 4), False)]
+
+            def low_pair():
+                butterfly(w[:, 0:NA, :], w[:, NA:2 * NA, :], pq[:, 0:NA, :], pq[:, NA:2 * NA, :])
 
             def final(state):
                 bounds = (0, 4, 8, 12, 14, 16)
-                n_cut = len(bounds) - 1
-                fs = []
+
+                def part(ds, ts):
+                    resa = res[:, TA0:TA0 + NA, rcols].rearrange("p t (d h q) -> p d t h q", d=8, h=2)
+                    xv = state[-1][:].rearrange("p (d t) (q two) -> p d t q two", d=8, two=2)
+                    butterfly(resa[:, ds, ts, 0, :], resa[:, ds, ts, 1, :], xv[:, ds, ts, :, 0], xv[:, ds, ts, :, 1])
+
+                def store(t0, t1):
+                    nc.sync.dma_start(out=o_view[:, TA0 + t0:TA0 + t1, rcols], in_=res[:, TA0 + t0:TA0 + t1, rcols])
+
                 def half(i):
                     def f():
-                        resa = res[:, TA0:TA0 + NA, rcols].rearrange("p t (d h q) -> p d t h q", d=8, h=2)
-                        xv = state[-1][:].rearrange("p (d t) (q two) -> p d t q two", d=8, two=2)
-                        ds = slice(4 * i, 4 * i + 4)
-                        butterfly(resa[:, ds, :, 0, :], resa[:, ds, :, 1, :], xv[:, ds, :, :, 0], xv[:, ds, :, :, 1])
+                        part(slice(4 * i, 4 * i + 4), slice(0, NA))
                         if i == 1:
-                            nc.sync.dma_start(out=o_view[:, TA0:TA0 + NA, rcols], in_=res[:, TA0:TA0 + NA, rcols])
+                            store(0, NA)
                     return f
-                if r != LAST_UNIT:
-                    return [half(0), half(1)]
 
                 def cut(i):
                     def f():
-                        resa = res[:, TA0:TA0 + NA, rcols].rearrange("p t (d h q) -> p d t h q", d=8, h=2)
-                        xv = state[-1][:].rearrange("p (d t) (q two) -> p d t q two", d=8, two=2)
-                        ts = slice(bounds[i], bounds[i + 1])
-                        butterfly(resa[:, :, ts, 0, :], resa[:, :, ts, 1, :], xv[:, :, ts, :, 0], xv[:, :, ts, :, 1])
-                        if r == LAST_UNIT:
-                            nc.sync.dma_start(out=o_view[:, TA0 + bounds[i]:TA0 + bounds[i + 1], rcols], in_=res[:, TA0 + bounds[i]:TA0 + bounds[i + 1], rcols])
-                        elif i == n_cut - 1:
-                            nc.sync.dma_start(out=o_view[:, TA0:TA0 + NA, rcols], in_=res[:, TA0:TA0 + NA, rcols])
+                        part(slice(0, 8), slice(bounds[i], bounds[i + 1]))
+                        store(bounds[i], bounds[i + 1])
                     return f
-                return [cut(i) for i in range(n_cut)]
+                if r != LAST_UNIT:
+                    return [half(0), half(1)]
+                return [cut(i) for i in range(len(bounds) - 1)]
 
-            return pre, state0, halves, final
+            return [low_pair] + stage_steps([w], 8 * NA, 16, halves, final)
 
         LAST_UNIT = 3
 
@@ -318,35 +295,39 @@ def tile_fullonlinehadamardhook_kernel(tc, x, had_K, grad_out, out):
                 rhs=one_codes[:, 0:K].bitcast(E5X4), rhs_scale=one_scales[:, 0:K],
                 start=True, stop=True,
             )
-        nc.vector.tensor_copy(out=hg[0][:].rearrange("p (r q) j -> p r q j", r=4), in_=h_src)
+        for eng, rs in ((nc.vector.tensor_copy, slice(0, 2)), (nc.scalar.copy, slice(2, 4))):
+            eng(out=hg[0][:].rearrange("p (r q) j -> p r q j", r=4)[:, rs], in_=h_src[:, rs])
         gt0 = grp.tile([P, K, 4], BF16, align_bytes=64, tag="g", name="gt")
         g0src = raw_g[:, 0:N0, :].rearrange("p t (j l x i) -> p l t x j i", j=4, l=2, i=4)
         by_fours(nc.scalar.copy, gt0[:, SUB:2 * SUB, :], g0src[:, 0], N0)
         by_fours(nc.vector.tensor_copy, gt0[:, 0:SUB, :], g0src[:, 1], N0)
         gt3 = ngp.tile([P, M, 4], BF16, align_bytes=64, tag="gn", name="gt3")
+        for pos in range(2):
+            slab_copy(0, pos, 0, 4)
         by_fours(nc.scalar.copy, gt3[:], token_runs(3, 1), 1)
-        gts[("s", 0)] = grp.tile([P, K, 4], BF16, align_bytes=64, tag="g", name="gt")
-        strip_part(gts[("s", 0)], 0, 0, NA // 2)
+        for pos in range(2):
+            slab_copy(0, pos, 4, 8)
         quant_h(0)
         gn0 = ngp.tile([P, SUB, 4], BF16, align_bytes=64, tag="gn", name="gn0")
         nc.vector.tensor_scalar_mul(out=flat(gn0), in0=gt0[:, 0:SUB, :].rearrange("p c j -> p (c j)"), scalar1=-1.0)
         quant_g(0, K, flat(gt0))
         banks0 = [pbank(r) for r in range(4)]
         quant_g(K, SUB, flat(gn0))
+        nc.vector.tensor_scalar_mul(out=flat(hg[1]), in0=flat(hg[0]), scalar1=-1.0)
         quant_g(W0N, M, flat(gt3))
         for r in range(4):
             mx(banks0[r], 0, r, 0, True, False)
             mx(banks0[r], 0, r, SUB, False, True)
         zpass(3, W0N)
-        nc.vector.tensor_scalar_mul(out=flat(hg[1]), in0=flat(hg[0]), scalar1=-1.0)
-        w0a = sm.tile([P, 8, M // 2], F32, tag="w0", name="w0a")
-        w0b = sm.tile([P, 18, M // 2], F32, tag="w0", name="w0b")
-        empty_bank(banks0[0][:], 8, w0a[:])
-        for r in range(1, 4):
-            for l in range(2):
-                empty_bank(banks0[r][:, l * SUB:l * SUB + 3 * M // 2], 3, w0b[:, 6 * r + 3 * l - 6:6 * r + 3 * l - 3, :])
-        zcopy(3, 1)
-        quant_h(1)
+        w0a = sm.tile([P, 8, M // 2], F32, tag="w0a", name="w0a", bufs=1)
+        w0b = sm.tile([P, 18, M // 2], F32, tag="w0b", name="w0b", bufs=1)
+
+        def empty_first(r):
+            if r == 0:
+                empty_bank(banks0[0][:], 8, w0a[:])
+            else:
+                for l in range(2):
+                    empty_bank(banks0[r][:, l * SUB:l * SUB + 3 * M // 2], 3, w0b[:, 6 * r + 3 * l - 6:6 * r + 3 * l - 3, :])
 
         def final_a(state):
             def fa():
@@ -363,55 +344,54 @@ def tile_fullonlinehadamardhook_kernel(tc, x, had_K, grad_out, out):
                 store_tokens(0, N0)
             return [fb]
 
-        steps_a = stage_steps([w0a], 8, M // 2, [slice(0, 8)], final_a)
+        steps_a = stage_steps([w0a], 8, M // 2, A_PARTS, final_a)
         steps_b = stage_steps([w0b], 18, M // 2, [slice(0, 18)], final_b)
-        vq.append(steps_a[0])
-        for i in range(5):
-            vq.extend([steps_a[i + 1], steps_b[i]])
-        vq.append(steps_b[5])
+        vq.extend(weave(steps_a, steps_b))
 
         banksU = {}
+        wPQ = {}
 
         def job(j):
             kind = j[0]
             if kind == "V":
                 pull(j[1])
-            elif kind == "strip":
-                if j[1] == 0:
-                    strip_part(gts[("s", 0)], 0, NA // 2, NA)
-                else:
-                    gts[("s", j[1])] = strip_copy(j[1])
-            elif kind == "qs":
-                quant_g(STRIP0 + j[1] * STRIP, 2 * SUB, flat(gts[("s", j[1])]))
-            elif kind == "negS":
-                gns[j[1]] = neg_copy(j[1])
-            elif kind == "negV":
-                gn = ngp.tile([P, SUB, 4], BF16, align_bytes=64, tag="gn", name="gn")
-                nc.vector.tensor_scalar_mul(out=flat(gn), in0=gts[("s", j[1])][:, 0:SUB, :].rearrange("p c j -> p (c j)"), scalar1=-1.0)
-                gns[j[1]] = gn
-            elif kind == "qn":
-                quant_g(STRIP0 + j[1] * STRIP + 2 * SUB, SUB, flat(gns[j[1]]))
+            elif kind == "piece":
+                for pos in range(2):
+                    slab_copy(j[1], pos, 0, NA)
+            elif kind == "pt":
+                for pos in range(2):
+                    slab_copy(j[1], pos, j[2], j[3])
+            elif kind == "qp":
+                k = j[1]
+                quant_g(STRIP0 + (k // 2) * HALF + (k % 2) * 2 * SUB, 2 * SUB, flat(slab_tiles[k]))
+            elif kind == "qd":
+                cyc = j[1]
+                quant_g(STRIP0 + cyc * HALF + 4 * SUB, SUB, slab_tiles[2 * cyc][:, 0:SUB, :].rearrange("p c j -> p (c j)"))
             elif kind == "open":
-                banksU[j[1]] = [pbank(4 * (j[1] % 2) + d) for d in range(4)]
-            elif kind == "sp":
-                r, c, k = j[1], j[2], j[3]
-                n_w = 2 if FOLD3[r] else 1
+                banksU[j[1]] = [pbank(UNIT_BANKS[j[1]] + d) for d in range(4)]
+            elif kind == "win":
                 for d in range(4):
-                    s = (((c & d) >> 1) ^ (c & d)) & 1
-                    mx(banksU[r][d], s, r, STRIP0 + c * STRIP + k * SUB, c == 0 and k == 0, c == 3 and k == n_w - 1)
+                    unit_pass(banksU[j[1]][d], j[1], d, j[2], j[3])
+            elif kind == "bank":
+                for cyc in range(2):
+                    for i in range(4):
+                        unit_pass(banksU[j[1]][j[2]], j[1], j[2], cyc, i)
             elif kind == "w":
-                wU[j[1]] = sm.tile([P, 8 * NA, 16], F32, tag="w0", name="w")
+                wU[j[1]] = sm.tile([P, 8 * NA, 16], F32, tag="wu", name="w", bufs=W_BUFS)
+                wPQ[j[1]] = sm.tile([P, 2 * NA, 16], F32, tag="pq", name="pq", bufs=W_BUFS)
             elif kind == "ev":
                 r, d = j[1], j[2]
-                empty_bank(banksU[r][d][:], 2 * NA, wU[r][:, d * 2 * NA:(d + 1) * 2 * NA, :])
-            elif kind == "bank":
-                r, d = j[1], j[2]
-                bank = bank_passes(r, d)
-                empty_bank(bank[:], 2 * NA, wU[r][:, d * 2 * NA:(d + 1) * 2 * NA, :])
+                bank = banksU[r][d]
+                if d == 0:
+                    empty_bank(bank[:], 2 * NA, wPQ[r][:])
+                else:
+                    for side in range(2):
+                        b = BANKS[d][side]
+                        empty_bank(bank[:, side * SUB:(side + 1) * SUB], NA, wU[r][:, b * NA:(b + 1) * NA, :], -SCALE if b == NEGATIVE else SCALE)
             elif kind == "U":
-                pre, state0, halves, final = unit_steps(j[1], wU[j[1]])
-                vq.extend(pre)
-                vq.extend(stage_steps(state0, 8 * NA, 16, halves, final))
+                steps = unit_steps(j[1], wU[j[1]], wPQ[j[1]])
+                vq.insert(max(vpos[0], len(vq) - 1), steps[0])
+                vq.extend(steps[1:])
             elif kind == "pf":
                 plain_front(j[1])
             elif kind == "pb":
@@ -420,6 +400,12 @@ def tile_fullonlinehadamardhook_kernel(tc, x, had_K, grad_out, out):
                 gts[j[1]] = prep_copy(j[1])
             elif kind == "q":
                 quant_g(TBC + j[1] * K, K, flat(gts[j[1]]))
+            elif kind == "e0":
+                empty_first(j[1])
+            elif kind == "qh1":
+                quant_h(1)
+            elif kind == "z3":
+                zcopy(3, 1)
             elif kind == "h3":
                 hmm(3, 1)
             elif kind == "r3":
@@ -431,38 +417,62 @@ def tile_fullonlinehadamardhook_kernel(tc, x, had_K, grad_out, out):
 
 
 LOAD_ORDER = (0, 1, 2, 3, 4, 5, 6, 7)
-G0_V = 2
 PLAIN_Q = True
+W_BUFS = 3
+UNIT_BANKS = (0, 4, 0, 0)
+N_WARM = 8
+A_PARTS = [slice(0, 4), slice(4, 8)]
+
+
+def weave(a, b):
+    out = list(a[:LEAD])
+    a = a[LEAD:]
+    while a or b:
+        out += a[:2] + b[:1]
+        a, b = a[2:], b[1:]
+    return out
+
+
+LEAD = 3
+WK_BUFS = {8: 2, 18: 2, 128: 3}
+V_SLABS = ((1, 1),)
+
+
 def build_program():
-    p = [("h3",), ("open", 0)]
-    for c in range(4):
-        p += [("strip", c)]
-        if c == 0:
+    p = [("qh1",), ("e0", 0), ("pt", 0, 8, 12), ("e0", 1), ("pt", 0, 12, 16), ("e0", 2), ("e0", 3), ("z3",), ("open", 0)]
+    for k in range(4):
+        if k:
+            p += [("piece", k)]
+        p += [("V", VN[k]), ("qp", k), ("win", 0, k // 2, k % 2)]
+        if k == 0:
+            p += [("h3",)]
+        if k == 1:
             p += [("r3",), ("open", 1)]
-        p += [("V", (4, 2, 2, 1)[c]), ("qs", c), ("sp", 0, c, 0), ("sp", 1, c, 0)]
+        if k % 2:
+            p += [("win", 0, k // 2, 2), ("qd", k // 2), ("win", 0, k // 2, 3)]
+        p += [("win", 1, w // 4, w % 4) for w in W1[k]]
+    p += [("win", 1, w // 4, w % 4) for w in W1[4]]
     p += [("prep", 0), ("w", 0)] + [("ev", 0, d) for d in range(4)] + [("U", 0)]
-    p += [("V", 2), ("q", 0)]
-    p += [("w", 1)] + [("ev", 1, d) for d in range(4)] + [("U", 1)]
-    p += [("open", 2)] + [("sp", 2, c, 0) for c in range(4)]
-    p += [("pf", 1)]
-    for c in range(4):
-        p += ([("pf", 1)] if c < 3 else []) + [("negS", c), ("pb", 1)]
-    p += [("V", NV1)]
-    for c in range(4):
-        p += [("qn", c), ("sp", 2, c, 1), ("V", 2)]
-    p += [("prep", 1), ("w", 2)] + [("ev", 2, d) for d in range(4)] + [("U", 2)]
-    p += [("prep", 2), ("V", 2), ("q", 1), ("V", 5), ("q", 2)]
-    p += [("w", 3)]
+    p += [("V", VN[4]), ("q", 0), ("prep", 1), ("V", VN[5]), ("q", 1), ("prep", 2), ("w", 1)]
     for d in range(4):
-        p += [("bank", 3, d)]
+        p += [("ev", 1, d)]
+    p += [("U", 1), ("V", VN[6]), ("q", 2)]
+    p += [("open", 2), ("w", 2), ("V", 4)]
+    for d in range(4):
+        p += [("bank", 2, d)] + ([("pf", 1)] if d > 1 else []) + [("ev", 2, d)]
+    p += [("U", 2)]
+    for i in range(4):
+        p += [("pb", 1), ("pf", 1)]
+    p += [("V", 8)]
+    p += [("open", 3), ("w", 3)]
+    for d in range(4):
+        p += [("bank", 3, d), ("ev", 3, d)]
     p += [("U", 3)]
-    p += [("pf", 1)]
-    for i in range(7):
-        p += [("pf", 1), ("pb", 1)]
-    p += [("pb", 1)]
+    for i in range(6):
+        p += [("pb", 1), ("pf", 1)]
+    p += [("pb", 1), ("pb", 1)]
     return p
 
 
-NV1 = 8
-N_WARM = 8
-V_STRIPS = (1,)
+VN = (4, 3, 3, 3, 4, 4, 4)
+W1 = ((), (0, 1), (), (), (2, 3, 4, 5, 6, 7))

@@ -26,13 +26,13 @@ TA0 = N0
 TB0 = N0 + NA
 SUB = 256
 HALF = 5 * SUB
-W0N = 3 * SUB
+FIRST = (0, 3, 1, 2)
+W0N = 7 * M
 STRIP0 = W0N + M
 TBC = STRIP0 + 2 * HALF
 N_COLS = TBC + NB * M
-CYCLES = ((0, 1, 4, 7), (2, 3, 6, 5))
-BANKS = ((0, 1), (2, 7), (3, 6), (5, 4))
-NEGATIVE = 7
+CYCLES = ((0, 1, 4, 5), (2, 3, 6, 7))
+HALF_PAIRS = ((0, 2), (0, 2), (), ())
 
 
 def tile_fullonlinehadamardhook_kernel(tc, x, had_K, grad_out, out):
@@ -45,7 +45,7 @@ def tile_fullonlinehadamardhook_kernel(tc, x, had_K, grad_out, out):
         ngp = ctx.enter_context(tc.tile_pool(name="ngp", bufs=2))
         wk = ctx.enter_context(tc.tile_pool(name="wk", bufs=3))
         sm = ctx.enter_context(tc.tile_pool(name="sm", bufs=2))
-        zsp = ctx.enter_context(tc.tile_pool(name="zsp", bufs=3))
+        zsp = ctx.enter_context(tc.tile_pool(name="zsp", bufs=ZS_BUFS))
         psum = ctx.enter_context(tc.psum_pool(name="psum", bufs=1))
         ctx.enter_context(tc.manual_schedule())
 
@@ -162,7 +162,7 @@ def tile_fullonlinehadamardhook_kernel(tc, x, had_K, grad_out, out):
 
         def zpass(t, col0):
             cols = slice(col0, col0 + M)
-            zp = pbank(4 + turn["z"] % 2)
+            zp = pbank(Z_BANKS[turn["z"]])
             turn["z"] += 1
             nc.tensor.matmul_mx(
                 out=zp[:],
@@ -178,7 +178,7 @@ def tile_fullonlinehadamardhook_kernel(tc, x, had_K, grad_out, out):
             zss[t] = zs
 
         def hmm(t, r0):
-            op = pbank(6 + turn["o"] % 2)
+            op = pbank(O_BANKS[turn["o"]])
             turn["o"] += 1
             for r in range(r0, 4):
                 rc = slice(r * P, (r + 1) * P)
@@ -197,61 +197,118 @@ def tile_fullonlinehadamardhook_kernel(tc, x, had_K, grad_out, out):
             return gt
 
         sub_runs = raw_g[:, TA0:TA0 + NA, :].rearrange("p t (j u x i) -> p u t x j i", j=4, u=8, i=4)
+        sub_plain = raw_g[:, TA0:TA0 + NA, :].rearrange("p t (j u e) -> p u t e j", j=4, u=8)
         slab_tiles = {}
 
-        def slab_copy(k, pos, t0, t1):
+        def slab_copy(k, pos, t0, t1, eng):
             if k not in slab_tiles:
                 slab_tiles[k] = grp.tile([P, K, 4], BF16, align_bytes=64, tag="g", name="gt")
             u = CYCLES[k // 2][2 * (k % 2) + pos]
-            eng = nc.vector.tensor_copy if (k, pos) in V_SLABS else nc.scalar.copy
             e = SUB // NA
-            by_fours(eng, slab_tiles[k][:, pos * SUB + t0 * e:pos * SUB + t1 * e, :], sub_runs[:, u, t0:t1], t1 - t0)
+            dst = slab_tiles[k][:, pos * SUB + t0 * e:pos * SUB + t1 * e, :]
+            if stored_negated(u):
+                dst = dst.rearrange("p (t e) j -> p t e j", t=t1 - t0)
+                if eng == "V":
+                    nc.vector.tensor_scalar_mul(out=dst, in0=sub_plain[:, u, t0:t1], scalar1=-1.0)
+                else:
+                    nc.scalar.mul(out=dst, in_=sub_plain[:, u, t0:t1], mul=-1.0)
+            else:
+                by_fours(nc.vector.tensor_copy if eng == "V" else nc.scalar.copy, dst, sub_runs[:, u, t0:t1], t1 - t0)
 
         def parity(v):
             return (v ^ (v >> 1) ^ (v >> 2)) & 1
 
+        def stored_negated(u):
+            return (u >> 2) & u & 1
+
+        def partner(left):
+            x, y, l = left >> 2, (left >> 1) & 1, left & 1
+            return ((x ^ 1) << 2) | (y << 1) | (l ^ x ^ 1), l ^ x ^ 1
+
+        def unit_banks(r):
+            banks = []
+            for c in (0, 1):
+                half = c in HALF_PAIRS[r]
+                banks += [(2 * c, half), (2 * c + (4 if half else 1), half)]
+            return banks
+
         def unit_pass(bank, r, d, cyc, i):
-            left = BANKS[d][0]
-            if d == 0 and i % 2 == 1:
+            left, half = unit_banks(r)[d]
+            if half and i % 2 == 1:
                 return
-            mx(bank, parity(left & CYCLES[cyc][i]), r, STRIP0 + cyc * HALF + i * SUB,
-               (cyc, i) == (0, 0), (cyc, i) == (1, 2 if d == 0 else 3))
+            u = CYCLES[cyc][i]
+            mx(bank, parity(left & u) ^ stored_negated(u), r, STRIP0 + cyc * HALF + i * SUB,
+               (cyc, i) == (0, 0), (cyc, i) == (1, 2 if half else 3))
+
+        def unit_evac(r, d, side):
+            left, half = unit_banks(r)[d]
+            b, turned = partner(left) if side else (left, 0)
+            if half:
+                g = HALF_PAIRS[r].index(b >> 1) * 2 + side
+                dst, scale = wPQ[r][:, g * NA:(g + 1) * NA, :], SCALE
+            else:
+                dst, scale = wU[r][:, b * NA:(b + 1) * NA, :], -SCALE if turned else SCALE
+            empty_bank(banksU[r][d][:, side * SUB:(side + 1) * SUB], NA, dst, scale)
 
         def unit_steps(r, w, pq):
             rcols = slice(r * M, (r + 1) * M)
-            halves = [slice(0, 4 * NA), slice(4 * NA, 8 * NA)]
+            shape = [P, 8 * NA, 16]
 
-            def low_pair():
-                butterfly(w[:, 0:NA, :], w[:, NA:2 * NA, :], pq[:, 0:NA, :], pq[:, NA:2 * NA, :])
+            def low(i0, c0, step):
+                def f():
+                    wv = w[:].rearrange("p (c l g) x -> p c l (g x)", c=4, l=2)[:, c0:c0 + step + 1:step]
+                    pv = pq[:].rearrange("p (c l g) x -> p c l (g x)", l=2, g=NA)[:, i0:i0 + 2]
+                    butterfly(wv[:, :, 0], wv[:, :, 1], pv[:, :, 0], pv[:, :, 1])
+                return f
 
-            def final(state):
-                bounds = (0, 4, 8, 12, 14, 16)
+            cs = HALF_PAIRS[r]
+            lows = [low(i, cs[i], cs[i + 1] - cs[i]) for i in range(0, len(cs), 2)]
+            tiles = [w]
 
-                def part(ds, ts):
+            def split(tile):
+                return tile[:].rearrange("p (d t) x -> p d t x", d=8)
+
+            def stage(i, ds, ts):
+                def f():
+                    while len(tiles) < i + 2:
+                        tiles.append(wk.tile(shape, F32, tag="w128", name="wn", bufs=WK_BUFS[128]))
+                    src, dst = split(tiles[i])[:, ds, ts], split(tiles[i + 1])[:, ds, ts]
+                    if i < 2:
+                        run = (8, 4)[i]
+                        xv = src.rearrange("p d t (m two h) -> p d t m two h", two=2, h=run)
+                        yv = dst.rearrange("p d t (m two h) -> p d t m two h", two=2, h=run)
+                        if i == 0:
+                            butterfly(yv[:, :, :, 0, 0], yv[:, :, :, 0, 1], xv[:, :, :, 0, 0], xv[:, :, :, 0, 1])
+                        else:
+                            butterfly(yv[:, :, :, :, 0], yv[:, :, :, :, 1], xv[:, :, :, :, 0], xv[:, :, :, :, 1])
+                    else:
+                        xv = src.rearrange("p d t (q two) -> p d t q two", two=2)
+                        yv = dst.rearrange("p d t (h q) -> p d t h q", h=2)
+                        butterfly(yv[:, :, :, 0], yv[:, :, :, 1], xv[:, :, :, :, 0], xv[:, :, :, :, 1])
+                return f
+
+            def final(ds, ts, store):
+                def f():
                     resa = res[:, TA0:TA0 + NA, rcols].rearrange("p t (d h q) -> p d t h q", d=8, h=2)
-                    xv = state[-1][:].rearrange("p (d t) (q two) -> p d t q two", d=8, two=2)
-                    butterfly(resa[:, ds, ts, 0, :], resa[:, ds, ts, 1, :], xv[:, ds, ts, :, 0], xv[:, ds, ts, :, 1])
+                    xv = split(tiles[3])[:, ds, ts].rearrange("p d t (q two) -> p d t q two", two=2)
+                    butterfly(resa[:, ds, ts, 0, :], resa[:, ds, ts, 1, :], xv[:, :, :, :, 0], xv[:, :, :, :, 1])
+                    if store:
+                        nc.sync.dma_start(out=o_view[:, TA0 + ts.start:TA0 + ts.stop, rcols], in_=res[:, TA0 + ts.start:TA0 + ts.stop, rcols])
+                return f
 
-                def store(t0, t1):
-                    nc.sync.dma_start(out=o_view[:, TA0 + t0:TA0 + t1, rcols], in_=res[:, TA0 + t0:TA0 + t1, rcols])
-
-                def half(i):
-                    def f():
-                        part(slice(4 * i, 4 * i + 4), slice(0, NA))
-                        if i == 1:
-                            store(0, NA)
-                    return f
-
-                def cut(i):
-                    def f():
-                        part(slice(0, 8), slice(bounds[i], bounds[i + 1]))
-                        store(bounds[i], bounds[i + 1])
-                    return f
-                if r != LAST_UNIT:
-                    return [half(0), half(1)]
-                return [cut(i) for i in range(len(bounds) - 1)]
-
-            return [low_pair] + stage_steps([w], 8 * NA, 16, halves, final)
+            steps = []
+            if r != LAST_UNIT:
+                parts = [(slice(0, 8), slice(0, NA // 2)), (slice(0, 8), slice(NA // 2, NA))]
+                for i in range(3):
+                    steps += [stage(i, ds, ts) for ds, ts in parts]
+                steps += [final(ds, ts, True) for ds, ts in parts]
+            else:
+                for group in LAST_PARTS:
+                    parts = [(slice(0, 8), slice(t0, t1)) for t0, t1 in group[0]]
+                    for i in range(3):
+                        steps += [stage(i, ds, ts) for ds, ts in parts]
+                    steps += [final(slice(0, 8), slice(t0, t1), True) for t0, t1 in group[1]]
+            return lows, steps
 
         LAST_UNIT = 3
 
@@ -295,57 +352,76 @@ def tile_fullonlinehadamardhook_kernel(tc, x, had_K, grad_out, out):
                 rhs=one_codes[:, 0:K].bitcast(E5X4), rhs_scale=one_scales[:, 0:K],
                 start=True, stop=True,
             )
-        for eng, rs in ((nc.vector.tensor_copy, slice(0, 2)), (nc.scalar.copy, slice(2, 4))):
-            eng(out=hg[0][:].rearrange("p (r q) j -> p r q j", r=4)[:, rs], in_=h_src[:, rs])
         gt0 = grp.tile([P, K, 4], BF16, align_bytes=64, tag="g", name="gt")
-        g0src = raw_g[:, 0:N0, :].rearrange("p t (j l x i) -> p l t x j i", j=4, l=2, i=4)
-        by_fours(nc.scalar.copy, gt0[:, SUB:2 * SUB, :], g0src[:, 0], N0)
-        by_fours(nc.vector.tensor_copy, gt0[:, 0:SUB, :], g0src[:, 1], N0)
         gt3 = ngp.tile([P, M, 4], BF16, align_bytes=64, tag="gn", name="gt3")
-        for pos in range(2):
-            slab_copy(0, pos, 0, 4)
-        by_fours(nc.scalar.copy, gt3[:], token_runs(3, 1), 1)
-        for pos in range(2):
-            slab_copy(0, pos, 4, 8)
-        quant_h(0)
-        gn0 = ngp.tile([P, SUB, 4], BF16, align_bytes=64, tag="gn", name="gn0")
-        nc.vector.tensor_scalar_mul(out=flat(gn0), in0=gt0[:, 0:SUB, :].rearrange("p c j -> p (c j)"), scalar1=-1.0)
-        quant_g(0, K, flat(gt0))
+        g0src = raw_g[:, 0:N0, :].rearrange("p t (j u x i) -> p u t x j i", j=4, u=4, i=4)
+        g0plain = raw_g[:, 0:N0, :].rearrange("p t (j u e) -> p u t e j", j=4, u=4)
         banks0 = [pbank(r) for r in range(4)]
-        quant_g(K, SUB, flat(gn0))
-        nc.vector.tensor_scalar_mul(out=flat(hg[1]), in0=flat(hg[0]), scalar1=-1.0)
-        quant_g(W0N, M, flat(gt3))
-        for r in range(4):
-            mx(banks0[r], 0, r, 0, True, False)
-            mx(banks0[r], 0, r, SUB, False, True)
-        zpass(3, W0N)
-        w0a = sm.tile([P, 8, M // 2], F32, tag="w0a", name="w0a", bufs=1)
-        w0b = sm.tile([P, 18, M // 2], F32, tag="w0b", name="w0b", bufs=1)
+
+        def v_negate(out, in_):
+            nc.vector.tensor_scalar_mul(out=out, in0=in_, scalar1=-1.0)
+
+        def head(kind, j):
+            if kind == "h":
+                eng = nc.vector.tensor_copy if j[1] == "V" else nc.scalar.copy
+                eng(out=hg[0][:].rearrange("p (r q) j -> p r q j", r=4)[:, j[2]:j[3]], in_=h_src[:, j[2]:j[3]])
+            elif kind == "g0":
+                eng = nc.scalar.copy if j[1] == "S" else v_negate if j[2] == 1 else nc.vector.tensor_copy
+                if eng is v_negate:
+                    eng(out=gt0[:, j[2] * M:(j[2] + 1) * M, :].rearrange("p (t e) j -> p t e j", t=N0), in_=g0plain[:, FIRST[j[2]]])
+                else:
+                    by_fours(eng, gt0[:, j[2] * M:(j[2] + 1) * M, :], g0src[:, FIRST[j[2]]], N0)
+            elif kind == "gt3":
+                by_fours(nc.scalar.copy, gt3[:], token_runs(3, 1), 1)
+            elif kind == "qh":
+                quant_h(j[1])
+            elif kind == "negh":
+                nc.vector.tensor_scalar_mul(out=flat(hg[1]), in0=flat(hg[0]), scalar1=-1.0)
+            elif kind == "qg0":
+                quant_g(0, K, flat(gt0))
+            elif kind == "qd01":
+                quant_g(4 * M, 2 * M, gt0[:, 0:2 * M, :].rearrange("p c j -> p (c j)"))
+            elif kind == "qd2":
+                quant_g(6 * M, M, gt0[:, 2 * M:3 * M, :].rearrange("p c j -> p (c j)"))
+            elif kind == "qg3":
+                quant_g(W0N, M, flat(gt3))
+            elif kind == "m0":
+                r, p = j[1], j[2]
+                mx(banks0[r], 1 if p == 1 else 0, r, p * M, p == 0, p == 1)
+            elif kind == "zp3":
+                zpass(3, W0N)
+
+        w0a = sm.tile([P, 16, M // 4], F32, tag="w0a", name="w0a", bufs=1)
+        w0b = sm.tile([P, 36, M // 4], F32, tag="w0b", name="w0b", bufs=1)
 
         def empty_first(r):
-            if r == 0:
-                empty_bank(banks0[0][:], 8, w0a[:])
-            else:
-                for l in range(2):
-                    empty_bank(banks0[r][:, l * SUB:l * SUB + 3 * M // 2], 3, w0b[:, 6 * r + 3 * l - 6:6 * r + 3 * l - 3, :])
+            nt = 4 if r == 0 else 3
+            dst = w0a[:] if r == 0 else w0b[:, 12 * (r - 1):12 * r, :]
+            cuts = ((0, 3), (3, 4)) if r == 0 else ((0, 1), (1, 2), (2, 3), (3, 4))
+            for k0, k1 in cuts:
+                nc.scalar.mul(
+                    out=dst[:, k0 * nt:k1 * nt, :].rearrange("p g (x y) -> p g x y", y=4),
+                    in_=banks0[r][:, k0 * M:k0 * M + (k1 - k0) * nt * 32].rearrange("p (g y x) -> p g x y", y=4, x=8),
+                    mul=-SCALE if k0 == 3 else SCALE,
+                )
 
         def final_a(state):
             def fa():
-                ya = res[:, 0:N0, 0:M].rearrange("p t (m h q) -> p m t h q", m=2, h=2)
-                xa = state[-1][:, 0:8, :].rearrange("p (m t) (q two) -> p m t q two", m=2, two=2)
+                ya = res[:, 0:N0, 0:M].rearrange("p t (m h q) -> p m t h q", m=4, h=2)
+                xa = state[-1][:].rearrange("p (m t) (q two) -> p m t q two", m=4, two=2)
                 butterfly(ya[:, :, :, 0, :], ya[:, :, :, 1, :], xa[:, :, :, :, 0], xa[:, :, :, :, 1])
             return [fa]
 
         def final_b(state):
             def fb():
-                yb = res[:, 0:3, M:K].rearrange("p t (m h q) -> p m t h q", m=6, h=2)
-                xb = state[-1][:].rearrange("p (m t) (q two) -> p m t q two", m=6, two=2)
+                yb = res[:, 0:3, M:K].rearrange("p t (m h q) -> p m t h q", m=12, h=2)
+                xb = state[-1][:].rearrange("p (m t) (q two) -> p m t q two", m=12, two=2)
                 butterfly(yb[:, :, :, 0, :], yb[:, :, :, 1, :], xb[:, :, :, :, 0], xb[:, :, :, :, 1])
                 store_tokens(0, N0)
             return [fb]
 
-        steps_a = stage_steps([w0a], 8, M // 2, A_PARTS, final_a)
-        steps_b = stage_steps([w0b], 18, M // 2, [slice(0, 18)], final_b)
+        steps_a = stage_steps([w0a], 16, M // 4, A_PARTS, final_a)
+        steps_b = stage_steps([w0b], 36, M // 4, [slice(0, 36)], final_b)
         vq.extend(weave(steps_a, steps_b))
 
         banksU = {}
@@ -357,10 +433,14 @@ def tile_fullonlinehadamardhook_kernel(tc, x, had_K, grad_out, out):
                 pull(j[1])
             elif kind == "piece":
                 for pos in range(2):
-                    slab_copy(j[1], pos, 0, NA)
+                    slab_copy(j[1], pos, 0, NA, j[2][pos])
             elif kind == "pt":
                 for pos in range(2):
-                    slab_copy(j[1], pos, j[2], j[3])
+                    slab_copy(j[1], pos, j[2], j[3], j[4][pos])
+            elif kind == "ps":
+                slab_copy(j[1], j[4], j[2], j[3], j[5])
+            elif kind in HEAD:
+                head(kind, j)
             elif kind == "qp":
                 k = j[1]
                 quant_g(STRIP0 + (k // 2) * HALF + (k % 2) * 2 * SUB, 2 * SUB, flat(slab_tiles[k]))
@@ -378,20 +458,17 @@ def tile_fullonlinehadamardhook_kernel(tc, x, had_K, grad_out, out):
                         unit_pass(banksU[j[1]][j[2]], j[1], j[2], cyc, i)
             elif kind == "w":
                 wU[j[1]] = sm.tile([P, 8 * NA, 16], F32, tag="wu", name="w", bufs=W_BUFS)
-                wPQ[j[1]] = sm.tile([P, 2 * NA, 16], F32, tag="pq", name="pq", bufs=W_BUFS)
+                n = len(HALF_PAIRS[j[1]]) * 2 * NA
+                if n:
+                    wPQ[j[1]] = sm.tile([P, n, 16], F32, tag="pq%d" % n, name="pq", bufs=1)
             elif kind == "ev":
-                r, d = j[1], j[2]
-                bank = banksU[r][d]
-                if d == 0:
-                    empty_bank(bank[:], 2 * NA, wPQ[r][:])
-                else:
-                    for side in range(2):
-                        b = BANKS[d][side]
-                        empty_bank(bank[:, side * SUB:(side + 1) * SUB], NA, wU[r][:, b * NA:(b + 1) * NA, :], -SCALE if b == NEGATIVE else SCALE)
+                for side in range(2):
+                    unit_evac(j[1], j[2], side)
             elif kind == "U":
-                steps = unit_steps(j[1], wU[j[1]], wPQ[j[1]])
-                vq.insert(max(vpos[0], len(vq) - 1), steps[0])
-                vq.extend(steps[1:])
+                lows, steps = unit_steps(j[1], wU[j[1]], wPQ.get(j[1]))
+                for f in lows:
+                    vq.insert(max(vpos[0], len(vq) - 1), f)
+                vq.extend(steps)
             elif kind == "pf":
                 plain_front(j[1])
             elif kind == "pb":
@@ -418,10 +495,13 @@ def tile_fullonlinehadamardhook_kernel(tc, x, had_K, grad_out, out):
 
 LOAD_ORDER = (0, 1, 2, 3, 4, 5, 6, 7)
 PLAIN_Q = True
+Z_BANKS = (4, 4, 5, 4, 5, 4, 5, 4, 5, 4, 5, 4, 5)
+O_BANKS = (6, 6, 7, 6, 7, 6, 7, 6, 7, 6, 7, 6, 7)
+ZS_BUFS = 3
 W_BUFS = 3
 UNIT_BANKS = (0, 4, 0, 0)
 N_WARM = 8
-A_PARTS = [slice(0, 4), slice(4, 8)]
+A_PARTS = [slice(0, 8), slice(8, 16)]
 
 
 def weave(a, b):
@@ -433,20 +513,26 @@ def weave(a, b):
     return out
 
 
-LEAD = 3
-WK_BUFS = {8: 2, 18: 2, 128: 3}
-V_SLABS = ((1, 1),)
+LEAD = 4
+LAST_PARTS = ((((0, 4), (4, 8)), ((0, 4), (4, 8))), (((8, 12), (12, 16)), ((8, 12), (12, 14), (14, 16))))
+WK_BUFS = {16: 2, 36: 2, 128: 3}
+HEAD = ("h", "g0", "gt3", "qh", "negh", "qg0", "qd01", "qd2", "qg3", "m0", "zp3")
 
 
 def build_program():
-    p = [("qh1",), ("e0", 0), ("pt", 0, 8, 12), ("e0", 1), ("pt", 0, 12, 16), ("e0", 2), ("e0", 3), ("z3",), ("open", 0)]
+    p = [("h", "V", 0, 2), ("h", "S", 2, 4), ("g0", "S", 0), ("g0", "V", 1), ("g0", "V", 2), ("g0", "S", 3)]
+    p += [("ps", 0, 0, 4, 0, "S"), ("gt3",), ("ps", 0, 4, 8, 0, "S"), ("pt", 1, 0, 4, "SS"), ("pt", 1, 4, 8, "SS"), ("ps", 0, 8, 12, 0, "S")]
+    p += [("qh", 0), ("qg0",), ("negh",), ("qd01",), ("qd2",), ("qh", 1), ("qg3",)]
+    p += [("m0", r, 0) for r in range(4)] + [("m0", r, w) for r in range(4) for w in (2, 3, 1)] + [("zp3",)]
+    p += [("ps", 0, t, t + 4, 1, "V") for t in range(0, 16, 4)]
+    p += [("e0", 0), ("ps", 0, 12, 16, 0, "S"), ("e0", 1), ("e0", 2), ("e0", 3), ("ps", 1, 8, 16, 0, "S"), ("z3",), ("open", 0)]
     for k in range(4):
-        if k:
-            p += [("piece", k)]
-        p += [("V", VN[k]), ("qp", k), ("win", 0, k // 2, k % 2)]
+        if k > 1:
+            p += [("piece", k, PIECE_ENG[k])]
+        p += [("V", VN[k] - 1)] + ([("ps", 1, 8, 16, 1, "V")] if k == 1 else []) + [("V", 1), ("qp", k), ("win", 0, k // 2, k % 2)]
         if k == 0:
             p += [("h3",)]
-        if k == 1:
+        if k == R3:
             p += [("r3",), ("open", 1)]
         if k % 2:
             p += [("win", 0, k // 2, 2), ("qd", k // 2), ("win", 0, k // 2, 3)]
@@ -461,18 +547,21 @@ def build_program():
     for d in range(4):
         p += [("bank", 2, d)] + ([("pf", 1)] if d > 1 else []) + [("ev", 2, d)]
     p += [("U", 2)]
-    for i in range(4):
-        p += [("pb", 1), ("pf", 1)]
+    for i in range(N_MID):
+        p += [("pf", 1), ("pb", 1)]
     p += [("V", 8)]
     p += [("open", 3), ("w", 3)]
     for d in range(4):
         p += [("bank", 3, d), ("ev", 3, d)]
     p += [("U", 3)]
-    for i in range(6):
-        p += [("pb", 1), ("pf", 1)]
+    for i in range(10 - N_MID):
+        p += [("pf", 1), ("pb", 1)]
     p += [("pb", 1), ("pb", 1)]
     return p
 
 
-VN = (4, 3, 3, 3, 4, 4, 4)
-W1 = ((), (0, 1), (), (), (2, 3, 4, 5, 6, 7))
+VN = (3, 3, 3, 2, 3, 4, 4)
+W1 = ((), (), (0, 1), (), (2, 3, 4, 5, 6, 7))
+PIECE_ENG = ("SS", "SS", "SS", "SS")
+R3 = 2
+N_MID = 6

@@ -32,7 +32,7 @@ STRIP0 = W0N + M
 TBC = STRIP0 + 2 * HALF
 N_COLS = TBC + NB * M
 CYCLES = ((0, 1, 4, 5), (2, 3, 6, 7))
-HALF_PAIRS = ((0, 2), (0, 2), (), ())
+HALF_PAIRS = ((0, 2), (), (), (0, 2))
 
 
 def tile_fullonlinehadamardhook_kernel(tc, x, had_K, grad_out, out):
@@ -52,8 +52,8 @@ def tile_fullonlinehadamardhook_kernel(tc, x, had_K, grad_out, out):
         raw_h = keep.tile([P, 4, K], BF16)
         nc.sync.dma_start(out=raw_h[:], in_=had_K.rearrange("(p j) c -> p j c", j=4))
         raw_g = keep.tile([P, T, K], BF16)
-        for c in LOAD_ORDER:
-            nc.sync.dma_start(out=raw_g[:, c * 4:(c + 1) * 4, :], in_=g_view[:, c * 4:(c + 1) * 4, :])
+        for t0, t1 in LOADS:
+            nc.sync.dma_start(out=raw_g[:, t0:t1, :], in_=g_view[:, t0:t1, :])
 
         pidx = keep.tile([P, 7], I32, name="pidx")
         kidx = keep.tile([P, 7], I32, name="kidx")
@@ -95,8 +95,9 @@ def tile_fullonlinehadamardhook_kernel(tc, x, had_K, grad_out, out):
         h_scales = [keep.tile([P, K], U8, align_bytes=64, name="hs%d" % s) for s in range(2)]
         h_src = raw_h[:].rearrange("p j (q r) -> p r q j", r=4)
 
-        def quant_h(s):
-            nc.vector.quantize_mx(out=h_codes[s][:].bitcast(E4X4), scales=h_scales[s][:], in_=hg[s][:].rearrange("p c j -> p (c j)"))
+        def quant_h(s, r0, r1):
+            cols = slice(r0 * P, r1 * P)
+            nc.vector.quantize_mx(out=h_codes[s][:, cols].bitcast(E4X4), scales=h_scales[s][:, cols], in_=hg[s][:, cols, :].rearrange("p c j -> p (c j)"))
 
         def by_fours(copy, dst, src, tokens):
             copy(out=dst.rearrange("p (t x i) j -> p t x j i", t=tokens, i=4), in_=src)
@@ -358,25 +359,28 @@ def tile_fullonlinehadamardhook_kernel(tc, x, had_K, grad_out, out):
         g0plain = raw_g[:, 0:N0, :].rearrange("p t (j u e) -> p u t e j", j=4, u=4)
         banks0 = [pbank(r) for r in range(4)]
 
-        def v_negate(out, in_):
-            nc.vector.tensor_scalar_mul(out=out, in0=in_, scalar1=-1.0)
-
         def head(kind, j):
             if kind == "h":
                 eng = nc.vector.tensor_copy if j[1] == "V" else nc.scalar.copy
                 eng(out=hg[0][:].rearrange("p (r q) j -> p r q j", r=4)[:, j[2]:j[3]], in_=h_src[:, j[2]:j[3]])
             elif kind == "g0":
-                eng = nc.scalar.copy if j[1] == "S" else v_negate if j[2] == 1 else nc.vector.tensor_copy
-                if eng is v_negate:
-                    eng(out=gt0[:, j[2] * M:(j[2] + 1) * M, :].rearrange("p (t e) j -> p t e j", t=N0), in_=g0plain[:, FIRST[j[2]]])
+                pos, t0, t1 = j[2:5]
+                dst = gt0[:, pos * M + t0 * 32:pos * M + t1 * 32, :]
+                if FIRST[pos] == 3:
+                    dst = dst.rearrange("p (t e) j -> p t e j", e=32)
+                    if j[1] == "V":
+                        nc.vector.tensor_scalar_mul(out=dst, in0=g0plain[:, FIRST[pos], t0:t1], scalar1=-1.0)
+                    else:
+                        nc.scalar.mul(out=dst, in_=g0plain[:, FIRST[pos], t0:t1], mul=-1.0)
                 else:
-                    by_fours(eng, gt0[:, j[2] * M:(j[2] + 1) * M, :], g0src[:, FIRST[j[2]]], N0)
+                    by_fours(nc.vector.tensor_copy if j[1] == "V" else nc.scalar.copy, dst, g0src[:, FIRST[pos], t0:t1], t1 - t0)
             elif kind == "gt3":
                 by_fours(nc.scalar.copy, gt3[:], token_runs(3, 1), 1)
             elif kind == "qh":
-                quant_h(j[1])
+                quant_h(j[1], j[2], j[3])
             elif kind == "negh":
-                nc.vector.tensor_scalar_mul(out=flat(hg[1]), in0=flat(hg[0]), scalar1=-1.0)
+                cols = slice(j[1] * P, j[2] * P)
+                nc.vector.tensor_scalar_mul(out=hg[1][:, cols, :].rearrange("p c j -> p (c j)"), in0=hg[0][:, cols, :].rearrange("p c j -> p (c j)"), scalar1=-1.0)
             elif kind == "qg0":
                 quant_g(0, K, flat(gt0))
             elif kind == "qd01":
@@ -446,7 +450,9 @@ def tile_fullonlinehadamardhook_kernel(tc, x, had_K, grad_out, out):
                 quant_g(STRIP0 + (k // 2) * HALF + (k % 2) * 2 * SUB, 2 * SUB, flat(slab_tiles[k]))
             elif kind == "qd":
                 cyc = j[1]
-                quant_g(STRIP0 + cyc * HALF + 4 * SUB, SUB, slab_tiles[2 * cyc][:, 0:SUB, :].rearrange("p c j -> p (c j)"))
+                first, again = slice(STRIP0 + cyc * HALF, STRIP0 + cyc * HALF + SUB), slice(STRIP0 + cyc * HALF + 4 * SUB, STRIP0 + cyc * HALF + 5 * SUB)
+                for plane in (g_codes, g_scales):
+                    nc.sync.dma_start(out=plane[:, again].bitcast(I32), in_=plane[:, first].bitcast(I32))
             elif kind == "open":
                 banksU[j[1]] = [pbank(UNIT_BANKS[j[1]] + d) for d in range(4)]
             elif kind == "win":
@@ -493,7 +499,7 @@ def tile_fullonlinehadamardhook_kernel(tc, x, had_K, grad_out, out):
         pull(1000)
 
 
-LOAD_ORDER = (0, 1, 2, 3, 4, 5, 6, 7)
+LOADS = [(0, 2), (2, 4)] + [(t, t + 4) for t in range(4, 32, 4)]
 PLAIN_Q = True
 Z_BANKS = (4, 4, 5, 4, 5, 4, 5, 4, 5, 4, 5, 4, 5)
 O_BANKS = (6, 6, 7, 6, 7, 6, 7, 6, 7, 6, 7, 6, 7)
@@ -520,22 +526,25 @@ HEAD = ("h", "g0", "gt3", "qh", "negh", "qg0", "qd01", "qd2", "qg3", "m0", "zp3"
 
 
 def build_program():
-    p = [("h", "V", 0, 2), ("h", "S", 2, 4), ("g0", "S", 0), ("g0", "V", 1), ("g0", "V", 2), ("g0", "S", 3)]
-    p += [("ps", 0, 0, 4, 0, "S"), ("gt3",), ("ps", 0, 4, 8, 0, "S"), ("pt", 1, 0, 4, "SS"), ("pt", 1, 4, 8, "SS"), ("ps", 0, 8, 12, 0, "S")]
-    p += [("qh", 0), ("qg0",), ("negh",), ("qd01",), ("qd2",), ("qh", 1), ("qg3",)]
+    p = [("h", "V", 0, 2), ("h", "S", 2, 4)]
+    p += [("g0", "S", 0, 0, 2), ("g0", "V", 1, 0, 2), ("g0", "V", 2, 0, 2), ("g0", "S", 3, 0, 2), ("qh", 0, 0, 2)]
+    p += [("g0", "S", 0, 2, 4), ("g0", "V", 1, 2, 4), ("g0", "V", 2, 2, 4), ("g0", "V", 3, 2, 4)]
+    p += [("ps", 0, 0, 4, 0, "S"), ("gt3",), ("ps", 0, 4, 8, 0, "S"), ("ps", 1, 0, 4, 0, "S"), ("ps", 1, 4, 8, 0, "S"), ("ps", 0, 8, 12, 0, "S")]
+    p += [("qg0",), ("qh", 0, 2, 4), ("negh", 0, 4), ("qd01",), ("qd2",), ("qh", 1, 0, 4), ("qg3",)]
     p += [("m0", r, 0) for r in range(4)] + [("m0", r, w) for r in range(4) for w in (2, 3, 1)] + [("zp3",)]
     p += [("ps", 0, t, t + 4, 1, "V") for t in range(0, 16, 4)]
+    p += [("ps", 1, 0, 8, 1, "V")]
     p += [("e0", 0), ("ps", 0, 12, 16, 0, "S"), ("e0", 1), ("e0", 2), ("e0", 3), ("ps", 1, 8, 16, 0, "S"), ("z3",), ("open", 0)]
     for k in range(4):
         if k > 1:
             p += [("piece", k, PIECE_ENG[k])]
-        p += [("V", VN[k] - 1)] + ([("ps", 1, 8, 16, 1, "V")] if k == 1 else []) + [("V", 1), ("qp", k), ("win", 0, k // 2, k % 2)]
+        p += [("V", VN[k] - 1)] + ([("ps", 1, 8, 16, 1, "V")] if k == 1 else []) + [("V", 1), ("qp", k)] + ([("qd", k // 2)] if k % 2 == 0 else []) + [("win", 0, k // 2, k % 2)]
         if k == 0:
             p += [("h3",)]
         if k == R3:
             p += [("r3",), ("open", 1)]
         if k % 2:
-            p += [("win", 0, k // 2, 2), ("qd", k // 2), ("win", 0, k // 2, 3)]
+            p += [("win", 0, k // 2, 2), ("win", 0, k // 2, 3)]
         p += [("win", 1, w // 4, w % 4) for w in W1[k]]
     p += [("win", 1, w // 4, w % 4) for w in W1[4]]
     p += [("prep", 0), ("w", 0)] + [("ev", 0, d) for d in range(4)] + [("U", 0)]
@@ -561,7 +570,7 @@ def build_program():
 
 
 VN = (3, 3, 3, 2, 3, 4, 4)
-W1 = ((), (), (0, 1), (), (2, 3, 4, 5, 6, 7))
+W1 = ((), (), (0,), (), (1, 2, 3, 4, 5, 6, 7))
 PIECE_ENG = ("SS", "SS", "SS", "SS")
 R3 = 2
-N_MID = 6
+N_MID = 5

@@ -67,8 +67,10 @@ def tile_fullonlinehadamardhook_kernel(tc, x, had_K, grad_out, out):
         nc.vector.tensor_scalar(out=sgn[:], in0=pbit[:], scalar1=-2.0, scalar2=1.0, op0=ALU.mult, op1=ALU.add)
         hmat = keep.tile([P, P], F32, name="hmat")
         nc.vector.memset(hmat[:, 0:1], 1.0)
-        for k in range(7):
+
+        def double_h(k):
             nc.scalar.activation(out=hmat[:, (1 << k):(2 << k)], in_=hmat[:, 0:(1 << k)], func=mybir.ActivationFunctionType.Copy, scale=sgn[:, k:k + 1])
+
         ones = keep.tile([P, K], BF16, align_bytes=64, name="ones")
         nc.vector.memset(ones[:], 1.0)
         one_codes = keep.tile([P, K + M], U32, align_bytes=64, name="one_codes")
@@ -255,15 +257,13 @@ def tile_fullonlinehadamardhook_kernel(tc, x, had_K, grad_out, out):
             rcols = slice(r * M, (r + 1) * M)
             shape = [P, 8 * NA, 16]
 
-            def low(i0, c0, step):
+            def low(i, c):
                 def f():
-                    wv = w[:].rearrange("p (c l g) x -> p c l (g x)", c=4, l=2)[:, c0:c0 + step + 1:step]
-                    pv = pq[:].rearrange("p (c l g) x -> p c l (g x)", l=2, g=NA)[:, i0:i0 + 2]
-                    butterfly(wv[:, :, 0], wv[:, :, 1], pv[:, :, 0], pv[:, :, 1])
+                    butterfly(w[:, 2 * c * NA:(2 * c + 1) * NA, :], w[:, (2 * c + 1) * NA:(2 * c + 2) * NA, :],
+                              pq[:, 2 * i * NA:(2 * i + 1) * NA, :], pq[:, (2 * i + 1) * NA:(2 * i + 2) * NA, :])
                 return f
 
-            cs = HALF_PAIRS[r]
-            lows = [low(i, cs[i], cs[i + 1] - cs[i]) for i in range(0, len(cs), 2)]
+            lows = [low(i, c) for i, c in enumerate(HALF_PAIRS[r])]
             tiles = [w]
 
             def split(tile):
@@ -394,6 +394,8 @@ def tile_fullonlinehadamardhook_kernel(tc, x, had_K, grad_out, out):
                 mx(banks0[r], 1 if p == 1 else 0, r, p * M, p == 0, p == 1)
             elif kind == "zp3":
                 zpass(3, W0N)
+            elif kind == "dbl":
+                double_h(j[1])
 
         w0a = sm.tile([P, 16, M // 4], F32, tag="w0a", name="w0a", bufs=1)
         w0b = sm.tile([P, 36, M // 4], F32, tag="w0b", name="w0b", bufs=1)
@@ -506,7 +508,7 @@ O_BANKS = (6, 6, 7, 6, 7, 6, 7, 6, 7, 6, 7, 6, 7)
 ZS_BUFS = 3
 W_BUFS = 3
 UNIT_BANKS = (0, 4, 0, 0)
-N_WARM = 8
+N_WARM = 7
 A_PARTS = [slice(0, 8), slice(8, 16)]
 
 
@@ -522,23 +524,24 @@ def weave(a, b):
 LEAD = 4
 LAST_PARTS = ((((0, 4), (4, 8)), ((0, 4), (4, 8))), (((8, 12), (12, 16)), ((8, 12), (12, 14), (14, 16))))
 WK_BUFS = {16: 2, 36: 2, 128: 3}
-HEAD = ("h", "g0", "gt3", "qh", "negh", "qg0", "qd01", "qd2", "qg3", "m0", "zp3")
+HEAD = ("h", "g0", "gt3", "qh", "negh", "qg0", "qd01", "qd2", "qg3", "m0", "zp3", "dbl")
 
 
 def build_program():
-    p = [("h", "V", 0, 2), ("h", "S", 2, 4)]
+    p = [("dbl", k) for k in range(5)]
+    p += [("h", "V", 0, 2), ("h", "S", 2, 4)]
     p += [("g0", "S", 0, 0, 2), ("g0", "V", 1, 0, 2), ("g0", "V", 2, 0, 2), ("g0", "S", 3, 0, 2), ("qh", 0, 0, 2)]
     p += [("g0", "S", 0, 2, 4), ("g0", "V", 1, 2, 4), ("g0", "V", 2, 2, 4), ("g0", "V", 3, 2, 4)]
-    p += [("ps", 0, 0, 4, 0, "S"), ("gt3",), ("ps", 0, 4, 8, 0, "S"), ("ps", 1, 0, 4, 0, "S"), ("ps", 1, 4, 8, 0, "S"), ("ps", 0, 8, 12, 0, "S")]
+    p += [("ps", 0, 0, 4, 0, "S"), ("dbl", 5), ("gt3",), ("dbl", 6), ("ps", 1, 0, 4, 0, "S"), ("ps", 0, 4, 8, 0, "S"), ("ps", 1, 4, 8, 0, "S")]
     p += [("qg0",), ("qh", 0, 2, 4), ("negh", 0, 4), ("qd01",), ("qd2",), ("qh", 1, 0, 4), ("qg3",)]
+    p += [("ps", 2, 0, 4, 0, "S"), ("ps", 2, 0, 4, 1, "S"), ("ps", 0, 8, 12, 0, "S")]
     p += [("m0", r, 0) for r in range(4)] + [("m0", r, w) for r in range(4) for w in (2, 3, 1)] + [("zp3",)]
-    p += [("ps", 0, t, t + 4, 1, "V") for t in range(0, 16, 4)]
-    p += [("ps", 1, 0, 8, 1, "V")]
+    p += [("ps", 0, t, t + 4, 1, "V") for t in range(0, 12, 4)] + [("ps", 1, 0, 8, 1, "V")]
     p += [("e0", 0), ("ps", 0, 12, 16, 0, "S"), ("e0", 1), ("e0", 2), ("e0", 3), ("ps", 1, 8, 16, 0, "S"), ("z3",), ("open", 0)]
     for k in range(4):
-        if k > 1:
-            p += [("piece", k, PIECE_ENG[k])]
-        p += [("V", VN[k] - 1)] + ([("ps", 1, 8, 16, 1, "V")] if k == 1 else []) + [("V", 1), ("qp", k)] + ([("qd", k // 2)] if k % 2 == 0 else []) + [("win", 0, k // 2, k % 2)]
+        p += [("ps", k) + c for c in REST[k]]
+        p += [("V", VN[k] - 1)] + ([("ps", 1, 8, 16, 1, "V")] if k == 1 else [("ps", 0, 12, 16, 1, "V")] if k == 0 else []) + [("V", 1), ("qp", k)]
+        p += ([("qd", k // 2)] if k % 2 == 0 else []) + [("win", 0, k // 2, k % 2)]
         if k == 0:
             p += [("h3",)]
         if k == R3:
@@ -574,3 +577,4 @@ W1 = ((), (), (0,), (), (1, 2, 3, 4, 5, 6, 7))
 PIECE_ENG = ("SS", "SS", "SS", "SS")
 R3 = 2
 N_MID = 5
+REST = ((), (), ((4, 16, 0, "S"), (4, 16, 1, "S")), ((0, 16, 0, "S"), (0, 16, 1, "S")))

@@ -32,7 +32,7 @@ STRIP0 = W0N + M
 TBC = STRIP0 + 2 * HALF
 N_COLS = TBC + NB * M
 CYCLES = ((0, 1, 4, 5), (2, 3, 6, 7))
-HALF_PAIRS = ((0, 2), (), (), (0, 2))
+HALF_PAIRS = ((0, 2), (), (0, 2), (0, 2))
 
 
 def tile_fullonlinehadamardhook_kernel(tc, x, had_K, grad_out, out):
@@ -188,6 +188,18 @@ def tile_fullonlinehadamardhook_kernel(tc, x, had_K, grad_out, out):
                 nc.tensor.matmul(out=op[:, rc], lhsT=zss[t][:, rc], rhs=hmat[:], start=True, stop=True)
             ops[t] = op
 
+        def last_token(t):
+            for i in range(2):
+                op = pbank(i)
+                for k in range(2):
+                    rc = slice((2 * i + k) * P, (2 * i + k + 1) * P)
+                    nc.tensor.matmul(out=op[:, k * P:(k + 1) * P], lhsT=zss[t][:, rc], rhs=hmat[:], start=True, stop=True)
+                nc.scalar.mul(out=res[:, t, 2 * i * P:(2 * i + 2) * P], in_=op[:, 0:2 * P], mul=SCALE)
+                store_waiting()
+            for i in range(2):
+                half = slice(2 * i * P, (2 * i + 2) * P)
+                nc.scalar.dma_start(out=o_view[:, t:t + 1, half], in_=res[:, t:t + 1, half])
+
         def revac(t, r0):
             nc.scalar.mul(out=res[:, t, r0 * P:], in_=ops[t][:, r0 * P:], mul=SCALE)
 
@@ -232,7 +244,7 @@ def tile_fullonlinehadamardhook_kernel(tc, x, had_K, grad_out, out):
             banks = []
             for c in (0, 1):
                 half = c in HALF_PAIRS[r]
-                banks += [(2 * c, half), (2 * c + (4 if half else 1), half)]
+                banks += [(2 * c, half) if half else (2 * c + 4, half), (2 * c + 4 if half else 2 * c + 5, half)]
             return banks
 
         def unit_pass(bank, r, d, cyc, i):
@@ -243,73 +255,107 @@ def tile_fullonlinehadamardhook_kernel(tc, x, had_K, grad_out, out):
             mx(bank, parity(left & u) ^ stored_negated(u), r, STRIP0 + cyc * HALF + i * SUB,
                (cyc, i) == (0, 0), (cyc, i) == (1, 2 if half else 3))
 
-        def unit_evac(r, d, side):
-            left, half = unit_banks(r)[d]
-            b, turned = partner(left) if side else (left, 0)
-            if half:
-                g = HALF_PAIRS[r].index(b >> 1) * 2 + side
-                dst, scale = wPQ[r][:, g * NA:(g + 1) * NA, :], SCALE
+        def unit_evac(r, d):
+            bank = banksU[r][d][:]
+            if unit_banks(r)[d][1]:
+                nc.scalar.mul(out=wU[r][:, d], in_=bank[:, SUB:], mul=SCALE)
             else:
-                dst, scale = wU[r][:, b * NA:(b + 1) * NA, :], -SCALE if turned else SCALE
-            empty_bank(banksU[r][d][:, side * SUB:(side + 1) * SUB], NA, dst, scale)
+                nc.scalar.mul(out=wU[r][:, d].rearrange("p (n x) -> p n x", x=2), in_=bank.rearrange("p (n two x) -> p n two x", two=2, x=2)[:, :, 1], mul=SCALE)
 
-        def unit_steps(r, w, pq):
+        def unit_steps(r):
             rcols = slice(r * M, (r + 1) * M)
             shape = [P, 8 * NA, 16]
-
-            def low(i, c):
-                def f():
-                    butterfly(w[:, 2 * c * NA:(2 * c + 1) * NA, :], w[:, (2 * c + 1) * NA:(2 * c + 2) * NA, :],
-                              pq[:, 2 * i * NA:(2 * i + 1) * NA, :], pq[:, (2 * i + 1) * NA:(2 * i + 2) * NA, :])
-                return f
-
-            lows = [low(i, c) for i, c in enumerate(HALF_PAIRS[r])]
-            tiles = [w]
+            tiles = []
 
             def split(tile):
                 return tile[:].rearrange("p (d t) x -> p d t x", d=8)
 
-            def stage(i, ds, ts):
+            def need(n):
+                while len(tiles) < n:
+                    tiles.append(wk.tile(shape, F32, tag="w128", name="wn", bufs=WK_BUFS[128]))
+
+            def first_view(view):
+                return view.rearrange("p g (b y x) -> p g b y x", b=2, y=4)
+
+            def scaled_butterfly(out_u, out_v, from_bank, from_sbuf, turned):
+                scale = -SCALE if turned else SCALE
+                nc.vector.scalar_tensor_tensor(out=out_u, in0=from_bank, scalar=scale, in1=from_sbuf, op0=ALU.mult, op1=ALU.subtract if turned else ALU.add)
+                nc.vector.scalar_tensor_tensor(out=out_v, in0=from_bank, scalar=scale, in1=from_sbuf, op0=ALU.mult, op1=ALU.add if turned else ALU.subtract)
+
+            banks = unit_banks(r)
+            halves = HALF_PAIRS[r]
+            sums = []
+
+            def from_bank(d):
                 def f():
-                    while len(tiles) < i + 2:
-                        tiles.append(wk.tile(shape, F32, tag="w128", name="wn", bufs=WK_BUFS[128]))
-                    src, dst = split(tiles[i])[:, ds, ts], split(tiles[i + 1])[:, ds, ts]
-                    if i < 2:
-                        run = (8, 4)[i]
-                        xv = src.rearrange("p d t (m two h) -> p d t m two h", two=2, h=run)
-                        yv = dst.rearrange("p d t (m two h) -> p d t m two h", two=2, h=run)
-                        if i == 0:
-                            butterfly(yv[:, :, :, 0, 0], yv[:, :, :, 0, 1], xv[:, :, :, 0, 0], xv[:, :, :, 0, 1])
-                        else:
-                            butterfly(yv[:, :, :, :, 0], yv[:, :, :, :, 1], xv[:, :, :, :, 0], xv[:, :, :, :, 1])
+                    need(1)
+                    for side in range(2):
+                        b, turned = partner(banks[d][0]) if side else (banks[d][0], 0)
+                        z0 = banksU[r][d][:, side * SUB:(side + 1) * SUB].rearrange("p (g y two x) -> p g y two x", y=4, two=2, x=2)[:, :, :, 0]
+                        z1 = wU[r][:, d, side * M:(side + 1) * M].rearrange("p (g y x) -> p g y x", y=4, x=2)
+                        out = first_view(tiles[0][:, b * NA:(b + 1) * NA, :])
+                        scaled_butterfly(out[:, :, 0], out[:, :, 1], z0, z1, turned)
+                return f
+
+            def join(i):
+                def f():
+                    if not sums:
+                        sums.append(sm.tile([P, 2 * len(halves) * NA, 16], F32, tag="sums", name="sums", bufs=2))
+                    c = halves[i]
+                    d_even = [k for k in range(4) if banks[k][1] and banks[k][0] == 2 * c][0]
+                    d_odd = [k for k in range(4) if banks[k][1] and partner(banks[k][0])[0] >> 1 == c][0]
+                    rows = [sums[0][:, (2 * i + l) * NA:(2 * i + l + 1) * NA, :].rearrange("p g x -> p (g x)") for l in range(2)]
+                    scaled_butterfly(rows[0], rows[1], banksU[r][d_even][:, 0:SUB], wU[r][:, d_odd], 0)
+                return f
+
+            def from_sums(i):
+                def f():
+                    need(1)
+                    x = sums[0][:, 2 * i * NA:2 * (i + 1) * NA, :].rearrange("p g (y two x) -> p g y two x", y=4, two=2)
+                    out = first_view(tiles[0][:, 2 * halves[i] * NA:2 * (halves[i] + 1) * NA, :])
+                    butterfly(out[:, :, 0], out[:, :, 1], x[:, :, :, 0], x[:, :, :, 1])
+                return f
+
+            def stage(i, ts):
+                def f():
+                    need(i + 1)
+                    src, dst = split(tiles[i - 1])[:, :, ts], split(tiles[i])[:, :, ts]
+                    if i == 1:
+                        xv = src.rearrange("p d t (b y two) -> p d t b y two", b=2, two=2)
+                        yv = dst.rearrange("p d t (b h y) -> p d t b h y", b=2, h=2)
+                        butterfly(yv[:, :, :, :, 0], yv[:, :, :, :, 1], xv[..., 0], xv[..., 1])
                     else:
                         xv = src.rearrange("p d t (q two) -> p d t q two", two=2)
                         yv = dst.rearrange("p d t (h q) -> p d t h q", h=2)
                         butterfly(yv[:, :, :, 0], yv[:, :, :, 1], xv[:, :, :, :, 0], xv[:, :, :, :, 1])
                 return f
 
-            def final(ds, ts, store):
+            def final(ts, eng=nc.vector):
                 def f():
                     resa = res[:, TA0:TA0 + NA, rcols].rearrange("p t (d h q) -> p d t h q", d=8, h=2)
-                    xv = split(tiles[3])[:, ds, ts].rearrange("p d t (q two) -> p d t q two", two=2)
-                    butterfly(resa[:, ds, ts, 0, :], resa[:, ds, ts, 1, :], xv[:, :, :, :, 0], xv[:, :, :, :, 1])
-                    if store:
-                        nc.sync.dma_start(out=o_view[:, TA0 + ts.start:TA0 + ts.stop, rcols], in_=res[:, TA0 + ts.start:TA0 + ts.stop, rcols])
+                    xv = split(tiles[2])[:, :, ts].rearrange("p d t (q two) -> p d t q two", two=2)
+                    eng.tensor_tensor(out=resa[:, :, ts, 0, :], in0=xv[:, :, :, :, 0], in1=xv[:, :, :, :, 1], op=ALU.add)
+                    eng.tensor_tensor(out=resa[:, :, ts, 1, :], in0=xv[:, :, :, :, 0], in1=xv[:, :, :, :, 1], op=ALU.subtract)
+                    nc.sync.dma_start(out=o_view[:, TA0 + ts.start:TA0 + ts.stop, rcols], in_=res[:, TA0 + ts.start:TA0 + ts.stop, rcols])
                 return f
 
+            head_steps = [join(i) for i in range(len(halves))] + [from_bank(d) for d in range(4) if not banks[d][1]]
+            sum_steps = [from_sums(i) for i in range(len(halves))]
             steps = []
             if r != LAST_UNIT:
-                parts = [(slice(0, 8), slice(0, NA // 2)), (slice(0, 8), slice(NA // 2, NA))]
-                for i in range(3):
-                    steps += [stage(i, ds, ts) for ds, ts in parts]
-                steps += [final(ds, ts, True) for ds, ts in parts]
+                early, late = slice(0, NA - G_TOKENS), slice(NA - G_TOKENS, NA)
+                va, vb = slice(0, NA // 2), slice(NA // 2, NA)
+                for i in (1, 2):
+                    steps += [stage(i, va), stage(i, vb)]
+                if G_TOKENS:
+                    steps += [final(late, nc.gpsimd)]
+                steps += [final(early)]
             else:
                 for group in LAST_PARTS:
-                    parts = [(slice(0, 8), slice(t0, t1)) for t0, t1 in group[0]]
-                    for i in range(3):
-                        steps += [stage(i, ds, ts) for ds, ts in parts]
-                    steps += [final(slice(0, 8), slice(t0, t1), True) for t0, t1 in group[1]]
-            return lows, steps
+                    for i in (1, 2):
+                        steps += [stage(i, slice(t0, t1)) for t0, t1 in group[0]]
+                    steps += [final(slice(t0, t1)) for t0, t1 in group[1]]
+            return head_steps, sum_steps, steps
 
         LAST_UNIT = 3
 
@@ -331,11 +377,19 @@ def tile_fullonlinehadamardhook_kernel(tc, x, had_K, grad_out, out):
                 zcopy(t, 0)
             front[0] += n
 
+        waiting = []
+
+        def store_waiting():
+            for t in waiting:
+                store_tokens(t, t + 1, nc.scalar)
+            waiting.clear()
+
         def plain_back(n):
             for t in plain[back[0]:back[0] + n]:
                 hmm(t, 0)
+                store_waiting()
                 revac(t, 0)
-                store_tokens(t, t + 1, PLAIN_Q and nc.scalar)
+                waiting.append(t)
             back[0] += n
 
         gts = {}
@@ -419,24 +473,33 @@ def tile_fullonlinehadamardhook_kernel(tc, x, had_K, grad_out, out):
             return [fa]
 
         def final_b(state):
+            def part(eng, m0, m1):
+                yb = res[:, 0:3, M:K].rearrange("p t (m h q) -> p m t h q", m=12, h=2)[:, m0:m1]
+                xb = state[-1][:].rearrange("p (m t) (q two) -> p m t q two", m=12, two=2)[:, m0:m1]
+                eng.tensor_tensor(out=yb[:, :, :, 0, :], in0=xb[:, :, :, :, 0], in1=xb[:, :, :, :, 1], op=ALU.add)
+                eng.tensor_tensor(out=yb[:, :, :, 1, :], in0=xb[:, :, :, :, 0], in1=xb[:, :, :, :, 1], op=ALU.subtract)
+
+            def fg():
+                part(nc.gpsimd, 0, G_FIRST)
+
             def fb():
-                yb = res[:, 0:3, M:K].rearrange("p t (m h q) -> p m t h q", m=12, h=2)
-                xb = state[-1][:].rearrange("p (m t) (q two) -> p m t q two", m=12, two=2)
-                butterfly(yb[:, :, :, 0, :], yb[:, :, :, 1, :], xb[:, :, :, :, 0], xb[:, :, :, :, 1])
+                part(nc.vector, G_FIRST, 12)
                 store_tokens(0, N0)
-            return [fb]
+            return [fg, fb] if G_FIRST else [fb]
 
         steps_a = stage_steps([w0a], 16, M // 4, A_PARTS, final_a)
         steps_b = stage_steps([w0b], 36, M // 4, [slice(0, 36)], final_b)
         vq.extend(weave(steps_a, steps_b))
 
         banksU = {}
-        wPQ = {}
+        heads_end = {}
 
         def job(j):
             kind = j[0]
             if kind == "V":
                 pull(j[1])
+            elif kind == "VU":
+                pull(vq.index(heads_end[j[1]]) + 1 - vpos[0])
             elif kind == "piece":
                 for pos in range(2):
                     slab_copy(j[1], pos, 0, NA, j[2][pos])
@@ -465,22 +528,21 @@ def tile_fullonlinehadamardhook_kernel(tc, x, had_K, grad_out, out):
                     for i in range(4):
                         unit_pass(banksU[j[1]][j[2]], j[1], j[2], cyc, i)
             elif kind == "w":
-                wU[j[1]] = sm.tile([P, 8 * NA, 16], F32, tag="wu", name="w", bufs=W_BUFS)
-                n = len(HALF_PAIRS[j[1]]) * 2 * NA
-                if n:
-                    wPQ[j[1]] = sm.tile([P, n, 16], F32, tag="pq%d" % n, name="pq", bufs=1)
+                wU[j[1]] = sm.tile([P, 4, SUB], F32, tag="wu", name="w", bufs=W_BUFS)
             elif kind == "ev":
-                for side in range(2):
-                    unit_evac(j[1], j[2], side)
+                unit_evac(j[1], j[2])
             elif kind == "U":
-                lows, steps = unit_steps(j[1], wU[j[1]], wPQ.get(j[1]))
-                for f in lows:
-                    vq.insert(max(vpos[0], len(vq) - 1), f)
+                head_steps, sum_steps, steps = unit_steps(j[1])
+                at = max(vpos[0], len(vq) - 1)
+                vq[at:at] = head_steps + sum_steps
+                heads_end[j[1]] = head_steps[-1]
                 vq.extend(steps)
             elif kind == "pf":
                 plain_front(j[1])
             elif kind == "pb":
                 plain_back(j[1])
+            elif kind == "pl":
+                last_token(plain[-1])
             elif kind == "prep":
                 gts[j[1]] = prep_copy(j[1])
             elif kind == "q":
@@ -502,11 +564,12 @@ def tile_fullonlinehadamardhook_kernel(tc, x, had_K, grad_out, out):
 
 
 LOADS = [(0, 2), (2, 4)] + [(t, t + 4) for t in range(4, 32, 4)]
-PLAIN_Q = True
 Z_BANKS = (4, 4, 5, 4, 5, 4, 5, 4, 5, 4, 5, 4, 5)
 O_BANKS = (6, 6, 7, 6, 7, 6, 7, 6, 7, 6, 7, 6, 7)
 ZS_BUFS = 3
 W_BUFS = 3
+G_TOKENS = 6
+G_FIRST = 0
 UNIT_BANKS = (0, 4, 0, 0)
 N_WARM = 7
 A_PARTS = [slice(0, 8), slice(8, 16)]
@@ -522,7 +585,7 @@ def weave(a, b):
 
 
 LEAD = 4
-LAST_PARTS = ((((0, 4), (4, 8)), ((0, 4), (4, 8))), (((8, 12), (12, 16)), ((8, 12), (12, 14), (14, 16))))
+LAST_PARTS = ((((0, 5), (5, 10)), ((0, 5), (5, 10))), (((10, 13), (13, 16)), ((10, 13), (13, 16))))
 WK_BUFS = {16: 2, 36: 2, 128: 3}
 HEAD = ("h", "g0", "gt3", "qh", "negh", "qg0", "qd01", "qd2", "qg3", "m0", "zp3", "dbl")
 
@@ -534,9 +597,9 @@ def build_program():
     p += [("g0", "S", 0, 2, 4), ("g0", "V", 1, 2, 4), ("g0", "V", 2, 2, 4), ("g0", "V", 3, 2, 4)]
     p += [("ps", 0, 0, 4, 0, "S"), ("dbl", 5), ("gt3",), ("dbl", 6), ("ps", 1, 0, 4, 0, "S"), ("ps", 0, 4, 8, 0, "S"), ("ps", 1, 4, 8, 0, "S")]
     p += [("qg0",), ("qh", 0, 2, 4), ("negh", 0, 4), ("qd01",), ("qd2",), ("qh", 1, 0, 4), ("qg3",)]
-    p += [("ps", 2, 0, 4, 0, "S"), ("ps", 2, 0, 4, 1, "S"), ("ps", 0, 8, 12, 0, "S")]
+    p += [("ps", 2, 0, 4, 1, "S"), ("ps", 0, 8, 12, 0, "S")]
     p += [("m0", r, 0) for r in range(4)] + [("m0", r, w) for r in range(4) for w in (2, 3, 1)] + [("zp3",)]
-    p += [("ps", 0, t, t + 4, 1, "V") for t in range(0, 12, 4)] + [("ps", 1, 0, 8, 1, "V")]
+    p += [("ps", 0, t, t + 4, 1, "V") for t in range(0, 12, 4)] + [("ps", 1, 0, 8, 1, "V"), ("ps", 2, 0, 4, 0, "V")]
     p += [("e0", 0), ("ps", 0, 12, 16, 0, "S"), ("e0", 1), ("e0", 2), ("e0", 3), ("ps", 1, 8, 16, 0, "S"), ("z3",), ("open", 0)]
     for k in range(4):
         p += [("ps", k) + c for c in REST[k]]
@@ -551,28 +614,27 @@ def build_program():
         p += [("win", 1, w // 4, w % 4) for w in W1[k]]
     p += [("win", 1, w // 4, w % 4) for w in W1[4]]
     p += [("prep", 0), ("w", 0)] + [("ev", 0, d) for d in range(4)] + [("U", 0)]
-    p += [("V", VN[4]), ("q", 0), ("prep", 1), ("V", VN[5]), ("q", 1), ("prep", 2), ("w", 1)]
+    p += [("V", VN[4]), ("q", 0), ("prep", 1), ("VU", 0), ("V", VN[5]), ("q", 1), ("prep", 2), ("w", 1)]
     for d in range(4):
         p += [("ev", 1, d)]
-    p += [("U", 1), ("V", VN[6]), ("q", 2)]
-    p += [("open", 2), ("w", 2), ("V", 4)]
+    p += [("U", 1), ("V", VN[6]), ("q", 2), ("VU", 1)]
+    p += [("open", 2), ("w", 2)]
     for d in range(4):
         p += [("bank", 2, d)] + ([("pf", 1)] if d > 1 else []) + [("ev", 2, d)]
-    p += [("U", 2)]
+    p += [("U", 2), ("VU", 2)]
     for i in range(N_MID):
         p += [("pf", 1), ("pb", 1)]
-    p += [("V", 8)]
     p += [("open", 3), ("w", 3)]
     for d in range(4):
         p += [("bank", 3, d), ("ev", 3, d)]
     p += [("U", 3)]
     for i in range(10 - N_MID):
         p += [("pf", 1), ("pb", 1)]
-    p += [("pb", 1), ("pb", 1)]
+    p += [("pb", 1), ("VU", 3), ("pl",)]
     return p
 
 
-VN = (3, 3, 3, 2, 3, 4, 4)
+VN = (3, 3, 3, 2, 3, 4, 2)
 W1 = ((), (), (0,), (), (1, 2, 3, 4, 5, 6, 7))
 PIECE_ENG = ("SS", "SS", "SS", "SS")
 R3 = 2

@@ -308,13 +308,11 @@ def tile_fullonlinehadamardhook_kernel(tc, x, had_K, grad_out, out):
                     scaled_butterfly(rows[0], rows[1], banksU[r][d_even][:, 0:SUB], wU[r][:, d_odd], 0)
                 return f
 
-            def from_sums(i):
-                def f():
-                    need(1)
-                    x = sums[0][:, 2 * i * NA:2 * (i + 1) * NA, :].rearrange("p g (y two x) -> p g y two x", y=4, two=2)
-                    out = first_view(tiles[0][:, 2 * halves[i] * NA:2 * (halves[i] + 1) * NA, :])
-                    butterfly(out[:, :, 0], out[:, :, 1], x[:, :, :, 0], x[:, :, :, 1])
-                return f
+            def from_sums():
+                need(1)
+                x = sums[0][:].rearrange("p (c g) (y two x) -> p c g y two x", c=2, y=4, two=2)
+                out = tiles[0][:].rearrange("p (c g) (b y x) -> p c g b y x", c=2, b=2, y=4)[:, :, 0:len(halves) * NA]
+                butterfly(out[:, :, :, 0], out[:, :, :, 1], x[:, :, :, :, 0], x[:, :, :, :, 1])
 
             def stage(i, ts):
                 def f():
@@ -340,7 +338,7 @@ def tile_fullonlinehadamardhook_kernel(tc, x, had_K, grad_out, out):
                 return f
 
             head_steps = [join(i) for i in range(len(halves))] + [from_bank(d) for d in range(4) if not banks[d][1]]
-            sum_steps = [from_sums(i) for i in range(len(halves))]
+            sum_steps = [from_sums] if halves else []
             steps = []
             if r != LAST_UNIT:
                 early, late = slice(0, NA - G_TOKENS), slice(NA - G_TOKENS, NA)
@@ -569,7 +567,7 @@ O_BANKS = (6, 6, 7, 6, 7, 6, 7, 6, 7, 6, 7, 6, 7)
 ZS_BUFS = 3
 W_BUFS = 3
 G_TOKENS = 6
-G_FIRST = 0
+G_FIRST = 8
 UNIT_BANKS = (0, 4, 0, 0)
 N_WARM = 7
 A_PARTS = [slice(0, 8), slice(8, 16)]
@@ -634,7 +632,7 @@ def build_program():
     return p
 
 
-VN = (3, 3, 3, 2, 3, 4, 2)
+VN = (3, 3, 3, 2, 2, 4, 1)
 W1 = ((), (), (0,), (), (1, 2, 3, 4, 5, 6, 7))
 PIECE_ENG = ("SS", "SS", "SS", "SS")
 R3 = 2

@@ -126,7 +126,7 @@ def tile_fullonlinehadamardhook_kernel(tc, x, had_K, grad_out, out):
                 start=start, stop=stop,
             )
 
-        def stage_steps(first, groups, length, parts, final):
+        def stage_steps(first, groups, length, parts, shuf_parts, final):
             state = first
             steps = []
 
@@ -153,7 +153,7 @@ def tile_fullonlinehadamardhook_kernel(tc, x, had_K, grad_out, out):
             for run in [h for h in (64, 32, 16, 8, 4) if h < length]:
                 for i, gs in enumerate(parts):
                     steps.append(mid(run, gs, i == 0))
-            for i, gs in enumerate(parts):
+            for i, gs in enumerate(shuf_parts):
                 steps.append(shuf(gs, i == 0))
             for f in final(state):
                 steps.append(f)
@@ -341,13 +341,9 @@ def tile_fullonlinehadamardhook_kernel(tc, x, had_K, grad_out, out):
             sum_steps = [from_sums] if halves else []
             steps = []
             if r != LAST_UNIT:
-                early, late = slice(0, NA - G_TOKENS), slice(NA - G_TOKENS, NA)
-                va, vb = slice(0, NA // 2), slice(NA // 2, NA)
-                for i in (1, 2):
-                    steps += [stage(i, va), stage(i, vb)]
-                if G_TOKENS:
-                    steps += [final(late, nc.gpsimd)]
-                steps += [final(early)]
+                cut = NA - G_TOKENS
+                steps += [stage(1, slice(0, NA // 2)), stage(1, slice(NA // 2, NA)), stage(2, slice(0, cut - G_LEAD)), stage(2, slice(cut, NA)),
+                          final(slice(cut, NA), nc.gpsimd), stage(2, slice(cut - G_LEAD, cut)), final(slice(0, cut))]
             else:
                 for group in LAST_PARTS:
                     for i in (1, 2):
@@ -483,10 +479,11 @@ def tile_fullonlinehadamardhook_kernel(tc, x, had_K, grad_out, out):
             def fb():
                 part(nc.vector, G_FIRST, 12)
                 store_tokens(0, N0)
-            return [fg, fb] if G_FIRST else [fb]
+            return [fg, fb]
 
-        steps_a = stage_steps([w0a], 16, M // 4, A_PARTS, final_a)
-        steps_b = stage_steps([w0b], 36, M // 4, [slice(0, 36)], final_b)
+        steps_a = stage_steps([w0a], 16, M // 4, A_PARTS, A_PARTS, final_a)
+        steps_b = stage_steps([w0b], 36, M // 4, [slice(0, 36)], [slice(0, 3 * G_FIRST), slice(3 * G_FIRST, 36)], final_b)
+        steps_b[-3:-1] = [steps_b[-2], steps_b[-3]]
         vq.extend(weave(steps_a, steps_b))
 
         banksU = {}
@@ -566,7 +563,8 @@ Z_BANKS = (4, 4, 5, 4, 5, 4, 5, 4, 5, 4, 5, 4, 5)
 O_BANKS = (6, 6, 7, 6, 7, 6, 7, 6, 7, 6, 7, 6, 7)
 ZS_BUFS = 3
 W_BUFS = 3
-G_TOKENS = 6
+G_TOKENS = 7
+G_LEAD = 2
 G_FIRST = 8
 UNIT_BANKS = (0, 4, 0, 0)
 N_WARM = 7
@@ -612,7 +610,7 @@ def build_program():
         p += [("win", 1, w // 4, w % 4) for w in W1[k]]
     p += [("win", 1, w // 4, w % 4) for w in W1[4]]
     p += [("prep", 0), ("w", 0)] + [("ev", 0, d) for d in range(4)] + [("U", 0)]
-    p += [("V", VN[4]), ("q", 0), ("prep", 1), ("VU", 0), ("V", VN[5]), ("q", 1), ("prep", 2), ("w", 1)]
+    p += [("V", VN[4]), ("prep", 1), ("VU", 0), ("q", 0), ("V", VN[5]), ("q", 1), ("prep", 2), ("w", 1)]
     for d in range(4):
         p += [("ev", 1, d)]
     p += [("U", 1), ("V", VN[6]), ("q", 2), ("VU", 1)]
@@ -636,5 +634,5 @@ VN = (3, 3, 3, 2, 2, 4, 1)
 W1 = ((), (), (0,), (), (1, 2, 3, 4, 5, 6, 7))
 PIECE_ENG = ("SS", "SS", "SS", "SS")
 R3 = 2
-N_MID = 5
+N_MID = 4
 REST = ((), (), ((4, 16, 0, "S"), (4, 16, 1, "S")), ((0, 16, 0, "S"), (0, 16, 1, "S")))

from contextlib import ExitStack

import concourse.mybir as mybir

F32 = mybir.dt.float32
BF16 = mybir.dt.bfloat16
U32 = mybir.dt.uint32
U8 = mybir.dt.uint8
I32 = mybir.dt.int32
E4X4 = mybir.dt.float8_e4m3fn_x4
E5X4 = mybir.dt.float8_e5m2_x4
ALU = mybir.AluOpType

P = 128
T = 32
K = 512
M = 128
SCALE = 1.0 / 256.0
FLOPS = 2 * K * K * T * M + 7 * T * K * M
BYTES = T * K * M * 2 + K * K * 2 + T * K * M * 4

N0 = 4
NA = 16
NB = 12
TA0 = N0
TB0 = N0 + NA
SUB = 256
HALF = 5 * SUB
FIRST = (0, 3, 1, 2)
W0N = 7 * M
STRIP0 = W0N + M
TBC = STRIP0 + 2 * HALF
N_COLS = TBC + NB * M
CYCLES = ((0, 1, 4, 5), (2, 3, 6, 7))
HALF_PAIRS = ((0, 2), (), (0, 2), (0, 2))


def tile_fullonlinehadamardhook_kernel(tc, x, had_K, grad_out, out):
    nc = tc.nc
    g_view = grad_out.rearrange("b s (p x) -> p (b s) x", p=P)
    o_view = out.rearrange("b s (p x) -> p (b s) x", p=P)
    with ExitStack() as ctx:
        keep = ctx.enter_context(tc.tile_pool(name="keep", bufs=1))
        grp = ctx.enter_context(tc.tile_pool(name="grp", bufs=3))
        ngp = ctx.enter_context(tc.tile_pool(name="ngp", bufs=2))
        wk = ctx.enter_context(tc.tile_pool(name="wk", bufs=3))
        sm = ctx.enter_context(tc.tile_pool(name="sm", bufs=2))
        zsp = ctx.enter_context(tc.tile_pool(name="zsp", bufs=ZS_BUFS))
        psum = ctx.enter_context(tc.psum_pool(name="psum", bufs=1))
        ctx.enter_context(tc.manual_schedule())

        raw_h = keep.tile([P, 4, K], BF16)
        nc.sync.dma_start(out=raw_h[:], in_=had_K.rearrange("(p j) c -> p j c", j=4))
        raw_g = keep.tile([P, T, K], BF16)
        for t0, t1 in LOADS:
            nc.sync.dma_start(out=raw_g[:, t0:t1, :], in_=g_view[:, t0:t1, :])

        pidx = keep.tile([P, 7], I32, name="pidx")
        kidx = keep.tile([P, 7], I32, name="kidx")
        nc.gpsimd.iota(pidx[:], pattern=[[0, 7]], base=0, channel_multiplier=1)
        nc.gpsimd.iota(kidx[:], pattern=[[1, 7]], base=0, channel_multiplier=0)
        shifted = keep.tile([P, 7], I32, name="shifted")
        nc.vector.tensor_tensor(out=shifted[:], in0=pidx[:], in1=kidx[:], op=ALU.logical_shift_right)
        pbit = keep.tile([P, 7], I32, name="pbit")
        nc.vector.tensor_single_scalar(out=pbit[:], in_=shifted[:], scalar=1, op=ALU.bitwise_and)
        sgn = keep.tile([P, 7], F32, name="sgn")
        nc.vector.tensor_scalar(out=sgn[:], in0=pbit[:], scalar1=-2.0, scalar2=1.0, op0=ALU.mult, op1=ALU.add)
        hmat = keep.tile([P, P], F32, name="hmat")
        nc.vector.memset(hmat[:, 0:1], 1.0)

        def double_h(k):
            nc.scalar.activation(out=hmat[:, (1 << k):(2 << k)], in_=hmat[:, 0:(1 << k)], func=mybir.ActivationFunctionType.Copy, scale=sgn[:, k:k + 1])

        ones = keep.tile([P, K], BF16, align_bytes=64, name="ones")
        nc.vector.memset(ones[:], 1.0)
        one_codes = keep.tile([P, K + M], U32, align_bytes=64, name="one_codes")
        one_scales = keep.tile([P, K + M], U8, align_bytes=64, name="one_scales")
        for i in range(4):
            nc.vector.quantize_mx(out=one_codes[:, i * M:(i + 1) * M].bitcast(E5X4), scales=one_scales[:, i * M:(i + 1) * M], in_=ones[:])
        nc.vector.quantize_mx(out=one_codes[:, K:K + M].bitcast(E4X4), scales=one_scales[:, K:K + M], in_=ones[:])

        g_codes = keep.tile([P, N_COLS], U32, align_bytes=64)
        g_scales = keep.tile([P, N_COLS], U8, align_bytes=64)
        res = keep.tile([P, T, K], F32)

        def pbank(i):
            return psum.tile([P, K], F32, tag="b%d" % i, name="bank%d" % i)

        turn = {"z": 0, "o": 0}

        def quant_g(col0, width, tile_ap):
            cols = slice(col0, col0 + width)
            nc.vector.quantize_mx(out=g_codes[:, cols].bitcast(E5X4), scales=g_scales[:, cols], in_=tile_ap)

        hg = [keep.tile([P, K, 4], BF16, align_bytes=64, name="hg%d" % s) for s in range(2)]
        h_codes = [keep.tile([P, K], U32, align_bytes=64, name="hc%d" % s) for s in range(2)]
        h_scales = [keep.tile([P, K], U8, align_bytes=64, name="hs%d" % s) for s in range(2)]
        h_src = raw_h[:].rearrange("p j (q r) -> p r q j", r=4)

        def quant_h(s, r0, r1):
            cols = slice(r0 * P, r1 * P)
            nc.vector.quantize_mx(out=h_codes[s][:, cols].bitcast(E4X4), scales=h_scales[s][:, cols], in_=hg[s][:, cols, :].rearrange("p c j -> p (c j)"))

        def by_fours(copy, dst, src, tokens):
            copy(out=dst.rearrange("p (t x i) j -> p t x j i", t=tokens, i=4), in_=src)

        def token_runs(t0, n):
            return raw_g[:, t0:t0 + n, :].rearrange("p t (j x i) -> p t x j i", j=4, i=4)

        def butterfly(out_u, out_v, in_even, in_odd):
            nc.vector.tensor_tensor(out=out_u, in0=in_even, in1=in_odd, op=ALU.add)
            nc.vector.tensor_tensor(out=out_v, in0=in_even, in1=in_odd, op=ALU.subtract)

        def empty_bank(bank_view, gb, w_rows, scale=SCALE):
            nc.scalar.mul(
                out=w_rows.rearrange("p g (x y) -> p g x y", y=4),
                in_=bank_view.rearrange("p (g y x) -> p g x y", g=gb, y=4),
                mul=scale,
            )

        def mx(bank, s, r, col, start, stop):
            nc.tensor.matmul_mx(
                out=bank[:],
                lhsT=h_codes[s][:, r * P:(r + 1) * P].bitcast(E4X4), lhsT_scale=h_scales[s][:, r * P:(r + 1) * P],
                rhs=g_codes[:, col:col + K].bitcast(E5X4), rhs_scale=g_scales[:, col:col + K],
                start=start, stop=stop,
            )

        def stage_steps(first, groups, length, parts, shuf_parts, final):
            state = first
            steps = []

            def mid(run, gs, new):
                def f():
                    if new:
                        state.append(wk.tile([P, groups, length], F32, tag="w%d" % groups, name="wn", bufs=WK_BUFS[groups]))
                    w, wn = state[-2], state[-1]
                    xv = w[:, gs, :].rearrange("p g (m two h) -> p g m two h", two=2, h=run)
                    yv = wn[:, gs, :].rearrange("p g (m two h) -> p g m two h", two=2, h=run)
                    butterfly(yv[:, :, :, 0, :], yv[:, :, :, 1, :], xv[:, :, :, 0, :], xv[:, :, :, 1, :])
                return f

            def shuf(gs, new):
                def f():
                    if new:
                        state.append(wk.tile([P, groups, length], F32, tag="w%d" % groups, name="wn", bufs=WK_BUFS[groups]))
                    w, wn = state[-2], state[-1]
                    xv = w[:, gs, :].rearrange("p g (q two) -> p g q two", two=2)
                    yv = wn[:, gs, :].rearrange("p g (h q) -> p g h q", h=2)
                    butterfly(yv[:, :, 0, :], yv[:, :, 1, :], xv[:, :, :, 0], xv[:, :, :, 1])
                return f

            for run in [h for h in (64, 32, 16, 8, 4) if h < length]:
                for i, gs in enumerate(parts):
                    steps.append(mid(run, gs, i == 0))
            for i, gs in enumerate(shuf_parts):
                steps.append(shuf(gs, i == 0))
            for f in final(state):
                steps.append(f)
            return steps

        zps = {}
        zss = {}
        ops = {}

        def zpass(t, col0):
            cols = slice(col0, col0 + M)
            zp = pbank(Z_BANKS[turn["z"]])
            turn["z"] += 1
            nc.tensor.matmul_mx(
                out=zp[:],
                lhsT=g_codes[:, cols].bitcast(E5X4), lhsT_scale=g_scales[:, cols],
                rhs=h_codes[0][:].bitcast(E4X4), rhs_scale=h_scales[0][:],
                start=True, stop=True,
            )
            zps[t] = zp

        def zcopy(t, r0):
            zs = zsp.tile([P, K], F32, name="zs")
            nc.scalar.copy(out=zs[:, r0 * P:], in_=zps[t][:, r0 * P:])
            zss[t] = zs

        def hmm(t, r0):
            op = pbank(O_BANKS[turn["o"]])
            turn["o"] += 1
            for r in range(r0, 4):
                rc = slice(r * P, (r + 1) * P)
                nc.tensor.matmul(out=op[:, rc], lhsT=zss[t][:, rc], rhs=hmat[:], start=True, stop=True)
            ops[t] = op

        def last_token(t):
            for i in range(2):
                op = pbank(i)
                for k in range(2):
                    rc = slice((2 * i + k) * P, (2 * i + k + 1) * P)
                    nc.tensor.matmul(out=op[:, k * P:(k + 1) * P], lhsT=zss[t][:, rc], rhs=hmat[:], start=True, stop=True)
                nc.scalar.mul(out=res[:, t, 2 * i * P:(2 * i + 2) * P], in_=op[:, 0:2 * P], mul=SCALE)
                store_waiting()
            for i in range(2):
                half = slice(2 * i * P, (2 * i + 2) * P)
                nc.scalar.dma_start(out=o_view[:, t:t + 1, half], in_=res[:, t:t + 1, half])

        def revac(t, r0):
            nc.scalar.mul(out=res[:, t, r0 * P:], in_=ops[t][:, r0 * P:], mul=SCALE)

        def store_tokens(t0, t1, eng=None):
            (eng or nc.sync).dma_start(out=o_view[:, t0:t1, :], in_=res[:, t0:t1, :])

        def prep_copy(k):
            gt = grp.tile([P, K, 4], BF16, align_bytes=64, tag="g", name="gt")
            by_fours(nc.scalar.copy, gt[:], token_runs(TB0 + 4 * k, 4), 4)
            return gt

        sub_runs = raw_g[:, TA0:TA0 + NA, :].rearrange("p t (j u x i) -> p u t x j i", j=4, u=8, i=4)
        sub_plain = raw_g[:, TA0:TA0 + NA, :].rearrange("p t (j u e) -> p u t e j", j=4, u=8)
        slab_tiles = {}

        def slab_copy(k, pos, t0, t1, eng):
            if k not in slab_tiles:
                slab_tiles[k] = grp.tile([P, K, 4], BF16, align_bytes=64, tag="g", name="gt")
            u = CYCLES[k // 2][2 * (k % 2) + pos]
            e = SUB // NA
            dst = slab_tiles[k][:, pos * SUB + t0 * e:pos * SUB + t1 * e, :]
            if stored_negated(u):
                dst = dst.rearrange("p (t e) j -> p t e j", t=t1 - t0)
                if eng == "V":
                    nc.vector.tensor_scalar_mul(out=dst, in0=sub_plain[:, u, t0:t1], scalar1=-1.0)
                else:
                    nc.scalar.mul(out=dst, in_=sub_plain[:, u, t0:t1], mul=-1.0)
            else:
                by_fours(nc.vector.tensor_copy if eng == "V" else nc.scalar.copy, dst, sub_runs[:, u, t0:t1], t1 - t0)

        def parity(v):
            return (v ^ (v >> 1) ^ (v >> 2)) & 1

        def stored_negated(u):
            return (u >> 2) & u & 1

        def partner(left):
            x, y, l = left >> 2, (left >> 1) & 1, left & 1
            return ((x ^ 1) << 2) | (y << 1) | (l ^ x ^ 1), l ^ x ^ 1

        def unit_banks(r):
            banks = []
            for c in (0, 1):
                half = c in HALF_PAIRS[r]
                banks += [(2 * c, half) if half else (2 * c + 4, half), (2 * c + 4 if half else 2 * c + 5, half)]
            return banks

        def unit_pass(bank, r, d, cyc, i):
            left, half = unit_banks(r)[d]
            if half and i % 2 == 1:
                return
            u = CYCLES[cyc][i]
            mx(bank, parity(left & u) ^ stored_negated(u), r, STRIP0 + cyc * HALF + i * SUB,
               (cyc, i) == (0, 0), (cyc, i) == (1, 2 if half else 3))

        def unit_evac(r, d):
            bank = banksU[r][d][:]
            if unit_banks(r)[d][1]:
                nc.scalar.mul(out=wU[r][:, d], in_=bank[:, SUB:], mul=SCALE)
            else:
                nc.scalar.mul(out=wU[r][:, d].rearrange("p (n x) -> p n x", x=2), in_=bank.rearrange("p (n two x) -> p n two x", two=2, x=2)[:, :, 1], mul=SCALE)

        def unit_steps(r):
            rcols = slice(r * M, (r + 1) * M)
            shape = [P, 8 * NA, 16]
            tiles = []

            def split(tile):
                return tile[:].rearrange("p (d t) x -> p d t x", d=8)

            def need(n):
                while len(tiles) < n:
                    tiles.append(wk.tile(shape, F32, tag="w128", name="wn", bufs=WK_BUFS[128]))

            def first_view(view):
                return view.rearrange("p g (b y x) -> p g b y x", b=2, y=4)

            def scaled_butterfly(out_u, out_v, from_bank, from_sbuf, turned):
                scale = -SCALE if turned else SCALE
                nc.vector.scalar_tensor_tensor(out=out_u, in0=from_bank, scalar=scale, in1=from_sbuf, op0=ALU.mult, op1=ALU.subtract if turned else ALU.add)
                nc.vector.scalar_tensor_tensor(out=out_v, in0=from_bank, scalar=scale, in1=from_sbuf, op0=ALU.mult, op1=ALU.add if turned else ALU.subtract)

            banks = unit_banks(r)
            halves = HALF_PAIRS[r]
            sums = []

            def from_bank(d):
                def f():
                    need(1)
                    for side in range(2):
                        b, turned = partner(banks[d][0]) if side else (banks[d][0], 0)
                        z0 = banksU[r][d][:, side * SUB:(side + 1) * SUB].rearrange("p (g y two x) -> p g y two x", y=4, two=2, x=2)[:, :, :, 0]
                        z1 = wU[r][:, d, side * M:(side + 1) * M].rearrange("p (g y x) -> p g y x", y=4, x=2)
                        out = first_view(tiles[0][:, b * NA:(b + 1) * NA, :])
                        scaled_butterfly(out[:, :, 0], out[:, :, 1], z0, z1, turned)
                return f

            def join(i):
                def f():
                    if not sums:
                        sums.append(sm.tile([P, 2 * len(halves) * NA, 16], F32, tag="sums", name="sums", bufs=2))
                    c = halves[i]
                    d_even = [k for k in range(4) if banks[k][1] and banks[k][0] == 2 * c][0]
                    d_odd = [k for k in range(4) if banks[k][1] and partner(banks[k][0])[0] >> 1 == c][0]
                    rows = [sums[0][:, (2 * i + l) * NA:(2 * i + l + 1) * NA, :].rearrange("p g x -> p (g x)") for l in range(2)]
                    scaled_butterfly(rows[0], rows[1], banksU[r][d_even][:, 0:SUB], wU[r][:, d_odd], 0)
                return f

            def from_sums():
                need(1)
                x = sums[0][:].rearrange("p (c g) (y two x) -> p c g y two x", c=2, y=4, two=2)
                out = tiles[0][:].rearrange("p (c g) (b y x) -> p c g b y x", c=2, b=2, y=4)[:, :, 0:len(halves) * NA]
                butterfly(out[:, :, :, 0], out[:, :, :, 1], x[:, :, :, :, 0], x[:, :, :, :, 1])

            def stage(i, ts):
                def f():
                    need(i + 1)
                    src, dst = split(tiles[i - 1])[:, :, ts], split(tiles[i])[:, :, ts]
                    if i == 1:
                        xv = src.rearrange("p d t (b y two) -> p d t b y two", b=2, two=2)
                        yv = dst.rearrange("p d t (b h y) -> p d t b h y", b=2, h=2)
                        butterfly(yv[:, :, :, :, 0], yv[:, :, :, :, 1], xv[..., 0], xv[..., 1])
                    else:
                        xv = src.rearrange("p d t (q two) -> p d t q two", two=2)
                        yv = dst.rearrange("p d t (h q) -> p d t h q", h=2)
                        butterfly(yv[:, :, :, 0], yv[:, :, :, 1], xv[:, :, :, :, 0], xv[:, :, :, :, 1])
                return f

            def final(ts, eng=nc.vector):
                def f():
                    resa = res[:, TA0:TA0 + NA, rcols].rearrange("p t (d h q) -> p d t h q", d=8, h=2)
                    xv = split(tiles[2])[:, :, ts].rearrange("p d t (q two) -> p d t q two", two=2)
                    eng.tensor_tensor(out=resa[:, :, ts, 0, :], in0=xv[:, :, :, :, 0], in1=xv[:, :, :, :, 1], op=ALU.add)
                    eng.tensor_tensor(out=resa[:, :, ts, 1, :], in0=xv[:, :, :, :, 0], in1=xv[:, :, :, :, 1], op=ALU.subtract)
                    nc.sync.dma_start(out=o_view[:, TA0 + ts.start:TA0 + ts.stop, rcols], in_=res[:, TA0 + ts.start:TA0 + ts.stop, rcols])
                return f

            head_steps = [join(i) for i in range(len(halves))] + [from_bank(d) for d in range(4) if not banks[d][1]]
            sum_steps = [from_sums] if halves else []
            steps = []
            if r != LAST_UNIT:
                cut = NA - G_TOKENS
                steps += [stage(1, slice(0, NA // 2)), stage(1, slice(NA // 2, NA)), stage(2, slice(0, cut - G_LEAD)), stage(2, slice(cut, NA)),
                          final(slice(cut, NA), nc.gpsimd), stage(2, slice(cut - G_LEAD, cut)), final(slice(0, cut))]
            else:
                for group in LAST_PARTS:
                    for i in (1, 2):
                        steps += [stage(i, slice(t0, t1)) for t0, t1 in group[0]]
                    steps += [final(slice(t0, t1)) for t0, t1 in group[1]]
            return head_steps, sum_steps, steps

        LAST_UNIT = 3

        vq = []
        vpos = [0]

        def pull(n):
            for f in vq[vpos[0]:vpos[0] + n]:
                f()
            vpos[0] = min(vpos[0] + n, len(vq))

        plain = [TB0 + i for i in range(NB)]
        front = [0]
        back = [0]

        def plain_front(n):
            for t in plain[front[0]:front[0] + n]:
                zpass(t, TBC + (t - TB0) * M)
                zcopy(t, 0)
            front[0] += n

        waiting = []

        def store_waiting():
            for t in waiting:
                store_tokens(t, t + 1, nc.scalar)
            waiting.clear()

        def plain_back(n):
            for t in plain[back[0]:back[0] + n]:
                hmm(t, 0)
                store_waiting()
                revac(t, 0)
                waiting.append(t)
            back[0] += n

        gts = {}
        gns = {}
        wU = {}

        def flat(t):
            return t[:].rearrange("p c j -> p (c j)")

        spare = pbank(7)
        for i in range(N_WARM):
            nc.tensor.matmul_mx(
                out=spare[:],
                lhsT=one_codes[:, K:K + M].bitcast(E4X4), lhsT_scale=one_scales[:, K:K + M],
                rhs=one_codes[:, 0:K].bitcast(E5X4), rhs_scale=one_scales[:, 0:K],
                start=True, stop=True,
            )
        gt0 = grp.tile([P, K, 4], BF16, align_bytes=64, tag="g", name="gt")
        gt3 = ngp.tile([P, M, 4], BF16, align_bytes=64, tag="gn", name="gt3")
        g0src = raw_g[:, 0:N0, :].rearrange("p t (j u x i) -> p u t x j i", j=4, u=4, i=4)
        g0plain = raw_g[:, 0:N0, :].rearrange("p t (j u e) -> p u t e j", j=4, u=4)
        banks0 = [pbank(r) for r in range(4)]

        def head(kind, j):
            if kind == "h":
                eng = nc.vector.tensor_copy if j[1] == "V" else nc.scalar.copy
                eng(out=hg[0][:].rearrange("p (r q) j -> p r q j", r=4)[:, j[2]:j[3]], in_=h_src[:, j[2]:j[3]])
            elif kind == "g0":
                pos, t0, t1 = j[2:5]
                dst = gt0[:, pos * M + t0 * 32:pos * M + t1 * 32, :]
                if FIRST[pos] == 3:
                    dst = dst.rearrange("p (t e) j -> p t e j", e=32)
                    if j[1] == "V":
                        nc.vector.tensor_scalar_mul(out=dst, in0=g0plain[:, FIRST[pos], t0:t1], scalar1=-1.0)
                    else:
                        nc.scalar.mul(out=dst, in_=g0plain[:, FIRST[pos], t0:t1], mul=-1.0)
                else:
                    by_fours(nc.vector.tensor_copy if j[1] == "V" else nc.scalar.copy, dst, g0src[:, FIRST[pos], t0:t1], t1 - t0)
            elif kind == "gt3":
                by_fours(nc.scalar.copy, gt3[:], token_runs(3, 1), 1)
            elif kind == "qh":
                quant_h(j[1], j[2], j[3])
            elif kind == "negh":
                cols = slice(j[1] * P, j[2] * P)
                nc.vector.tensor_scalar_mul(out=hg[1][:, cols, :].rearrange("p c j -> p (c j)"), in0=hg[0][:, cols, :].rearrange("p c j -> p (c j)"), scalar1=-1.0)
            elif kind == "qg0":
                quant_g(0, K, flat(gt0))
            elif kind == "qd01":
                quant_g(4 * M, 2 * M, gt0[:, 0:2 * M, :].rearrange("p c j -> p (c j)"))
            elif kind == "qd2":
                quant_g(6 * M, M, gt0[:, 2 * M:3 * M, :].rearrange("p c j -> p (c j)"))
            elif kind == "qg3":
                quant_g(W0N, M, flat(gt3))
            elif kind == "m0":
                r, p = j[1], j[2]
                mx(banks0[r], 1 if p == 1 else 0, r, p * M, p == 0, p == 1)
            elif kind == "zp3":
                zpass(3, W0N)
            elif kind == "dbl":
                double_h(j[1])

        w0a = sm.tile([P, 16, M // 4], F32, tag="w0a", name="w0a", bufs=1)
        w0b = sm.tile([P, 36, M // 4], F32, tag="w0b", name="w0b", bufs=1)

        def empty_first(r):
            nt = 4 if r == 0 else 3
            dst = w0a[:] if r == 0 else w0b[:, 12 * (r - 1):12 * r, :]
            cuts = ((0, 3), (3, 4)) if r == 0 else ((0, 1), (1, 2), (2, 3), (3, 4))
            for k0, k1 in cuts:
                nc.scalar.mul(
                    out=dst[:, k0 * nt:k1 * nt, :].rearrange("p g (x y) -> p g x y", y=4),
                    in_=banks0[r][:, k0 * M:k0 * M + (k1 - k0) * nt * 32].rearrange("p (g y x) -> p g x y", y=4, x=8),
                    mul=-SCALE if k0 == 3 else SCALE,
                )

        def final_a(state):
            def fa():
                ya = res[:, 0:N0, 0:M].rearrange("p t (m h q) -> p m t h q", m=4, h=2)
                xa = state[-1][:].rearrange("p (m t) (q two) -> p m t q two", m=4, two=2)
                butterfly(ya[:, :, :, 0, :], ya[:, :, :, 1, :], xa[:, :, :, :, 0], xa[:, :, :, :, 1])
            return [fa]

        def final_b(state):
            def part(eng, m0, m1):
                yb = res[:, 0:3, M:K].rearrange("p t (m h q) -> p m t h q", m=12, h=2)[:, m0:m1]
                xb = state[-1][:].rearrange("p (m t) (q two) -> p m t q two", m=12, two=2)[:, m0:m1]
                eng.tensor_tensor(out=yb[:, :, :, 0, :], in0=xb[:, :, :, :, 0], in1=xb[:, :, :, :, 1], op=ALU.add)
                eng.tensor_tensor(out=yb[:, :, :, 1, :], in0=xb[:, :, :, :, 0], in1=xb[:, :, :, :, 1], op=ALU.subtract)

            def fg():
                part(nc.gpsimd, 0, G_FIRST)

            def fb():
                part(nc.vector, G_FIRST, 12)
                store_tokens(0, N0)
            return [fg, fb]

        steps_a = stage_steps([w0a], 16, M // 4, A_PARTS, A_PARTS, final_a)
        steps_b = stage_steps([w0b], 36, M // 4, [slice(0, 36)], [slice(0, 3 * G_FIRST), slice(3 * G_FIRST, 36)], final_b)
        steps_b[-3:-1] = [steps_b[-2], steps_b[-3]]
        vq.extend(weave(steps_a, steps_b))

        banksU = {}
        heads_end = {}

        def job(j):
            kind = j[0]
            if kind == "V":
                pull(j[1])
            elif kind == "VU":
                pull(vq.index(heads_end[j[1]]) + 1 - vpos[0])
            elif kind == "piece":
                for pos in range(2):
                    slab_copy(j[1], pos, 0, NA, j[2][pos])
            elif kind == "pt":
                for pos in range(2):
                    slab_copy(j[1], pos, j[2], j[3], j[4][pos])
            elif kind == "ps":
                slab_copy(j[1], j[4], j[2], j[3], j[5])
            elif kind in HEAD:
                head(kind, j)
            elif kind == "qp":
                k = j[1]
                quant_g(STRIP0 + (k // 2) * HALF + (k % 2) * 2 * SUB, 2 * SUB, flat(slab_tiles[k]))
            elif kind == "qd":
                cyc = j[1]
                first, again = slice(STRIP0 + cyc * HALF, STRIP0 + cyc * HALF + SUB), slice(STRIP0 + cyc * HALF + 4 * SUB, STRIP0 + cyc * HALF + 5 * SUB)
                for plane in (g_codes, g_scales):
                    nc.sync.dma_start(out=plane[:, again].bitcast(I32), in_=plane[:, first].bitcast(I32))
            elif kind == "open":
                banksU[j[1]] = [pbank(UNIT_BANKS[j[1]] + d) for d in range(4)]
            elif kind == "win":
                for d in range(4):
                    unit_pass(banksU[j[1]][d], j[1], d, j[2], j[3])
            elif kind == "bank":
                for cyc in range(2):
                    for i in range(4):
                        unit_pass(banksU[j[1]][j[2]], j[1], j[2], cyc, i)
            elif kind == "w":
                wU[j[1]] = sm.tile([P, 4, SUB], F32, tag="wu", name="w", bufs=W_BUFS)
            elif kind == "ev":
                unit_evac(j[1], j[2])
            elif kind == "U":
                head_steps, sum_steps, steps = unit_steps(j[1])
                at = max(vpos[0], len(vq) - 1)
                vq[at:at] = head_steps + sum_steps
                heads_end[j[1]] = head_steps[-1]
                vq.extend(steps)
            elif kind == "pf":
                plain_front(j[1])
            elif kind == "pb":
                plain_back(j[1])
            elif kind == "pl":
                last_token(plain[-1])
            elif kind == "prep":
                gts[j[1]] = prep_copy(j[1])
            elif kind == "q":
                quant_g(TBC + j[1] * K, K, flat(gts[j[1]]))
            elif kind == "e0":
                empty_first(j[1])
            elif kind == "qh1":
                quant_h(1)
            elif kind == "z3":
                zcopy(3, 1)
            elif kind == "h3":
                hmm(3, 1)
            elif kind == "r3":
                revac(3, 1)

        for j in build_program():
            job(j)
        pull(1000)


LOADS = [(0, 2), (2, 4)] + [(t, t + 4) for t in range(4, 32, 4)]
Z_BANKS = (4, 4, 5, 4, 5, 4, 5, 4, 5, 4, 5, 4, 5)
O_BANKS = (6, 6, 7, 6, 7, 6, 7, 6, 7, 6, 7, 6, 7)
ZS_BUFS = 3
W_BUFS = 3
G_TOKENS = 7
G_LEAD = 2
G_FIRST = 8
UNIT_BANKS = (0, 4, 0, 0)
N_WARM = 7
A_PARTS = [slice(0, 8), slice(8, 16)]


def weave(a, b):
    out = list(a[:LEAD])
    a = a[LEAD:]
    while a or b:
        out += a[:2] + b[:1]
        a, b = a[2:], b[1:]
    return out


LEAD = 4
LAST_PARTS = ((((0, 5), (5, 10)), ((0, 5), (5, 10))), (((10, 13), (13, 16)), ((10, 13), (13, 16))))
WK_BUFS = {16: 2, 36: 2, 128: 3}
HEAD = ("h", "g0", "gt3", "qh", "negh", "qg0", "qd01", "qd2", "qg3", "m0", "zp3", "dbl")


def build_program():
    p = [("dbl", k) for k in range(5)]
    p += [("h", "V", 0, 2), ("h", "S", 2, 4)]
    p += [("g0", "S", 0, 0, 2), ("g0", "V", 1, 0, 2), ("g0", "V", 2, 0, 2), ("g0", "S", 3, 0, 2), ("qh", 0, 0, 2)]
    p += [("g0", "S", 0, 2, 4), ("g0", "V", 1, 2, 4), ("g0", "V", 2, 2, 4), ("g0", "V", 3, 2, 4)]
    p += [("ps", 0, 0, 4, 0, "S"), ("dbl", 5), ("gt3",), ("dbl", 6), ("ps", 1, 0, 4, 0, "S"), ("ps", 0, 4, 8, 0, "S"), ("ps", 1, 4, 8, 0, "S")]
    p += [("qg0",), ("qh", 0, 2, 4), ("negh", 0, 4), ("qd01",), ("qd2",), ("qh", 1, 0, 4), ("qg3",)]
    p += [("ps", 2, 0, 4, 1, "S"), ("ps", 0, 8, 12, 0, "S")]
    p += [("m0", r, 0) for r in range(4)] + [("m0", r, w) for r in range(4) for w in (2, 3, 1)] + [("zp3",)]
    p += [("ps", 0, t, t + 4, 1, "V") for t in range(0, 12, 4)] + [("ps", 1, 0, 8, 1, "V"), ("ps", 2, 0, 4, 0, "V")]
    p += [("e0", 0), ("ps", 0, 12, 16, 0, "S"), ("e0", 1), ("e0", 2), ("e0", 3), ("ps", 1, 8, 16, 0, "S"), ("z3",), ("open", 0)]
    for k in range(4):
        p += [("ps", k) + c for c in REST[k]]
        p += [("V", VN[k] - 1)] + ([("ps", 1, 8, 16, 1, "V")] if k == 1 else [("ps", 0, 12, 16, 1, "V")] if k == 0 else []) + [("V", 1), ("qp", k)]
        p += ([("qd", k // 2)] if k % 2 == 0 else []) + [("win", 0, k // 2, k % 2)]
        if k == 0:
            p += [("h3",)]
        if k == R3:
            p += [("r3",), ("open", 1)]
        if k % 2:
            p += [("win", 0, k // 2, 2), ("win", 0, k // 2, 3)]
        p += [("win", 1, w // 4, w % 4) for w in W1[k]]
    p += [("win", 1, w // 4, w % 4) for w in W1[4]]
    p += [("prep", 0), ("w", 0)] + [("ev", 0, d) for d in range(4)] + [("U", 0)]
    p += [("V", VN[4]), ("prep", 1), ("VU", 0), ("q", 0), ("V", VN[5]), ("q", 1), ("prep", 2), ("w", 1)]
    for d in range(4):
        p += [("ev", 1, d)]
    p += [("U", 1), ("V", VN[6]), ("q", 2), ("VU", 1)]
    p += [("open", 2), ("w", 2)]
    for d in range(4):
        p += [("bank", 2, d)] + ([("pf", 1)] if d > 1 else []) + [("ev", 2, d)]
    p += [("U", 2), ("VU", 2)]
    for i in range(N_MID):
        p += [("pf", 1), ("pb", 1)]
    p += [("open", 3), ("w", 3)]
    for d in range(4):
        p += [("bank", 3, d), ("ev", 3, d)]
    p += [("U", 3)]
    for i in range(10 - N_MID):
        p += [("pf", 1), ("pb", 1)]
    p += [("pb", 1), ("VU", 3), ("pl",)]
    return p


VN = (3, 3, 3, 2, 2, 4, 1)
W1 = ((), (), (0,), (), (1, 2, 3, 4, 5, 6, 7))
PIECE_ENG = ("SS", "SS", "SS", "SS")
R3 = 2
N_MID = 4
REST = ((), (), ((4, 16, 0, "S"), (4, 16, 1, "S")), ((0, 16, 0, "S"), (0, 16, 1, "S")))
